import numpy as np
import ml_dtypes


def mxq(x, axis, fmt="e4m3"):
    dtype, down = {"e4m3": (ml_dtypes.float8_e4m3fn, 7), "e5m2": (ml_dtypes.float8_e5m2, 14)}[fmt]
    v = np.moveaxis(np.asarray(x, np.float32).astype(ml_dtypes.bfloat16).astype(np.float64), axis, -1)
    blocks = v.reshape(v.shape[:-1] + (-1, 32))
    amax = np.abs(blocks).max(-1, keepdims=True)
    byte = np.maximum(np.where(amax > 0, np.frexp(amax)[1] - 1 + 127, 0) - down, 1)
    scale = np.exp2(byte - 127.0)
    codes = (blocks / scale).astype(np.float32).astype(dtype).astype(np.float64)
    return np.moveaxis((codes * scale).reshape(v.shape), -1, axis)


WIDE = False


def mx_kscale(k):
    if not WIDE:
        return np.ones(k)
    levels = np.array([18, -18])
    if k % 512:
        return np.exp2(np.random.permutation(np.resize(levels, k // 32))).repeat(32)
    a = np.empty((k // 512, 16))
    for p in range(k // 512):
        a[p, :8] = np.random.permutation(np.resize(levels, 8))
        for g in range(8):
            far = levels[np.abs(levels - a[p, g]) >= 10]
            a[p, g + 8] = far[np.random.randint(len(far))]
    return np.exp2(a.ravel()).repeat(32)


BF16 = ml_dtypes.bfloat16


def bf(x):
    return np.asarray(x, np.float32).astype(BF16)


def f64(x):
    return np.asarray(x).astype(np.float64)


B, HG, H, D, LSEQ, LK = 1, 40, 8, 128, 1024, 512
N = HG * HG
C = H * D
DILATIONS = (1, 2, 3)
POOL = 2


def landmarks(x):
    xg = f64(x).reshape(B, HG, HG, C)
    xm = np.concatenate([xg[:, ::d, ::d, :].reshape(B, -1, C) for d in DILATIONS], axis=1)
    return xm[:, :POOL * LSEQ].reshape(B, LSEQ, POOL, C).mean(axis=2)


def landmarks_back(dxl):
    sides = [len(range(0, HG, d)) for d in DILATIONS]
    dm = np.zeros((sum(r * r for r in sides), C))
    dm[:POOL * LSEQ] = np.repeat(dxl, POOL, axis=0) / POOL
    dg = np.zeros((HG, HG, C))
    start = 0
    for d, r in zip(DILATIONS, sides):
        dg[::d, ::d] += dm[start:start + r * r].reshape(r, r, C)
        start += r * r
    return dg.reshape(N, C)


def setup_inputs():
    u = mx_kscale(LK)
    v = mx_kscale(2 * C)
    s = mx_kscale(LSEQ)
    st = np.repeat(s[:N // POOL], POOL)
    se = np.where(np.arange(LSEQ) < N // POOL, s, np.max(s))
    x0 = bf(np.random.standard_normal((B, N, C)))
    W0 = bf(np.random.standard_normal((C, 2 * C)) * 1.6 / np.sqrt(C))
    b_kv = bf(np.random.standard_normal(2 * C) * 0.2)
    Ek0 = bf(np.random.standard_normal((LSEQ, LK)) / np.sqrt(LSEQ))
    Ev0 = bf(np.random.standard_normal((LSEQ, LK)) / np.sqrt(LSEQ))
    vk = v[:C].reshape(1, H, 1, D)
    vv = v[C:].reshape(1, H, 1, D)
    uj = u[None, None, :, None]
    grad_0 = bf(np.random.standard_normal((B, H, LK, D)) * np.exp2(np.random.randint(-6, 1, (B, 1, LK, 1))) * uj * vk)
    grad_1 = bf(np.random.standard_normal((B, H, LK, D)) * np.exp2(np.random.randint(-6, 1, (B, 1, LK, 1))) * uj * vv)
    kv = landmarks(x0) @ f64(W0) + f64(b_kv)
    return {"x": bf(f64(x0) * st[None, :, None]),
            "W_kv": bf(f64(W0) / v[None, :]),
            "b_kv": b_kv,
            "E_k": bf(f64(Ek0) / se[:, None] / u[None, :]),
            "E_v": bf(f64(Ev0) / se[:, None] / u[None, :]),
            "kv": np.asarray(kv, np.float32),
            "grad_0": grad_0,
            "grad_1": grad_1}


def reference(x, W_kv, b_kv, E_k, E_v, kv, grad_0, grad_1):
    g = np.stack([f64(t)[0].transpose(1, 0, 2).reshape(LK, C) for t in (grad_0, grad_1)])
    e = np.stack([f64(E_k), f64(E_v)])
    dh = mxq(e, 2, "e4m3") @ mxq(g, 1, "e5m2")
    dkv = np.concatenate([dh[0], dh[1]], axis=1)
    xl = landmarks(x)[0]
    dxl = mxq(dkv, 1, "e5m2") @ mxq(f64(W_kv), 1, "e4m3").T
    dW = mxq(xl, 0, "e4m3").T @ mxq(dkv, 0, "e5m2")
    dx = landmarks_back(dxl).reshape(B, N, C)
    return dx, dW

@@ -1,0 +1,424 @@
+from contextlib import ExitStack
+
+import concourse.mybir as mybir
+from concourse.masks import make_identity
+
+F32 = mybir.dt.float32
+BF16 = mybir.dt.bfloat16
+U32 = mybir.dt.uint32
+I32 = mybir.dt.int32
+U8 = mybir.dt.uint8
+E4X4 = mybir.dt.float8_e4m3fn_x4
+E5X4 = mybir.dt.float8_e5m2_x4
+COPY = mybir.ActivationFunctionType.Copy
+ADD = mybir.AluOpType.add
+MULT = mybir.AluOpType.mult
+
+FLOPS = 2 * 1024 * 512 * 2048 + 2 * 1024 * 2048 * 1024 + 2 * 1024 * 1024 * 2048
+BYTES = 2 * (1600 * 1024 + 1024 * 2048 + 2 * 1024 * 512 + 2 * 512 * 1024) + 4 * (1600 * 1024 + 1024 * 2048)
+
+LOADS = "G00 G01 E00 E01 L5 E11 W1 L9 L4 X1 L1 W2 L11 L2 G10 L0 W3 E10 G11 L10 L8 L6 W0 L7 L3 X0 L12".split()
+
+ORDER = [
+    ("XZ",),
+    ("G", 1, 0),
+    ("G", 0, 1),
+    ("E", 0, 0, 0),
+    ("E", 0, 1, 0),
+    ("E", 1, 1, 2),
+    ("D", 0, 1, 1, 1, 0),
+    ("D", 0, 0, 0, 0, 3),
+    ("D", 1, 0, 3, 0, 3),
+    ("D", 1, 1, 3, 0, 2),
+    ("X", 1, 1),
+    ("W", 1, 1, 0),
+    ("E", 1, 0, 0),
+    ("G", 3, 0),
+    ("G", 2, 1),
+    ("W", 3, 1, 0),
+    ("X", 0, 1),
+    ("W", 3, 0, 0),
+    ("W", 0, 0, 0),
+    ("D", 3, 0, 0, 0, 0),
+    ("W", 1, 0, 1),
+    ("D", 2, 0, 0, 1, 3),
+    ("DW", 5, 0, 2),
+    ("W", 2, 0, 1),
+    ("W", 0, 1, 0),
+    ("W", 2, 1, 1),
+    ("X", 1, 0),
+    ("D", 2, 1, 0, 2, 4),
+    ("DX", 0, 3, 0),
+    ("DX", 0, 0, 0),
+    ("DX", 0, 2, 0),
+    ("X", 0, 0),
+    ("DX", 0, 1, 1),
+    ("DW", 3, 0, 0),
+    ("DW", 2, 0, 1),
+    ("DW", 0, 0, 0),
+    ("D", 3, 1, 2, 1, 2),
+    ("DW", 7, 0, 2),
+    ("XR", 0),
+    ("DW", 6, 0, 0),
+    ("DW", 1, 0, 0),
+    ("FIN", 0, 1),
+    ("FIN", 0, 0),
+    ("FIN", 0, 2),
+    ("FIN", 0, 3),
+    ("DW", 0, 1, 0),
+    ("DW", 3, 1, 0),
+    ("DX", 1, 1, 1),
+    ("DX", 1, 2, 1),
+    ("DW", 5, 1, 1),
+    ("XR", 1),
+    ("DW", 1, 1, 2),
+    ("DW", 2, 1, 0),
+    ("FIN", 1, 2),
+    ("DX", 1, 0, 1),
+    ("FIN", 1, 1),
+    ("L3",),
+    ("DW", 6, 1, 0),
+    ("DW", 4, 0, 0),
+    ("FIN", 1, 0),
+    ("DW", 4, 1, 2),
+    ("DX", 1, 3, 2),
+    ("FIN", 1, 3),
+    ("DW", 7, 1, 2),
+]
+
+NA = 72
+
+
+def tile_efficientmultiscaledilatedattention_pa_v_kernel(tc, x, W_kv, b_kv, E_k, E_v, kv, grad_0, grad_1, out_0, out_1):
+    nc = tc.nc
+    with ExitStack() as ctx:
+        const = ctx.enter_context(tc.tile_pool(name="const", bufs=1))
+        pool = ctx.enter_context(tc.tile_pool(name="pool", bufs=1))
+        psum = ctx.enter_context(tc.psum_pool(name="psum", bufs=1))
+
+        ctx.enter_context(tc.manual_schedule())
+        ident = const.tile([128, 128], F32, name="ident", align_bytes=64)
+        make_identity(nc, ident[:])
+
+        def r8(name, shape, dt):
+            return pool.tile(shape, dt, name=name, tag="r8", bufs=6, align_bytes=64)
+
+        def p4(name):
+            return pool.tile([128, 2048], BF16, name=name, tag="p4", bufs=6, align_bytes=64)
+
+        def codes(name, tag, bufs):
+            c = pool.tile([128, 1024], U32, name=name + "c", tag=tag + "c", bufs=bufs, align_bytes=64)
+            s = pool.tile([128, 1024], U8, name=name + "s", tag=tag + "s", bufs=bufs, align_bytes=64)
+            return c, s
+
+        def quant(cs, a, fmt, src):
+            c, s = cs
+            nc.vector.quantize_mx(out=c[:, a:a + 512].bitcast(fmt), scales=s[:, a:a + 512], in_=src[:])
+
+        xf = x[0]
+        raw_e = [None, None]
+        raw_g = [None, None]
+        e_src = [E_k, E_v]
+        g_src = [grad_0[0], grad_1[0]]
+
+        def load_e(e, grp):
+            t = raw_e[e]
+            if grp == 1:
+                nc.sync.dma_start(out=t[:, 4:8, :], in_=e_src[e][288:800, :].rearrange("(p t) k -> p t k", t=4))
+            else:
+                nc.sync.dma_start(out=t[0:NA, 0:4, :], in_=e_src[e][0:288, :].rearrange("(p t) k -> p t k", t=4))
+                nc.sync.dma_start(out=t[NA:128, 0:4, :], in_=e_src[e][800:1024, :].rearrange("(p t) k -> p t k", t=4))
+
+        def load_g(e, b):
+            nc.sync.dma_start(out=raw_g[e][:, 4 * b:4 * b + 4, :],
+                              in_=g_src[e][4 * b:4 * b + 4].rearrange("h (p j) d -> p h (j d)", j=4))
+
+        raw_x = {}
+        raw_x[1] = pool.tile([128, 8, 1024], BF16, name="xB", tag="x16", bufs=2, align_bytes=64)
+        raw_x[0] = pool.tile([128, 8, 1024], BF16, name="xA", tag="x16", bufs=2, align_bytes=64)
+        xa = raw_x[0]
+        two = xf.rearrange("(a n) c -> a n c", n=160)
+        three = xf[0:378, :].rearrange("(a n) c -> a n c", n=126)
+        row3 = xf[0:480, :].rearrange("(n three) c -> n three c", three=3)
+        q0 = NA + 50
+        SECOND = ((0, 0, 8, 0), (1, 0, 8, 16), (2, 0, 4, 32), (2, 4, 8, 80), (3, 0, 8, 88), (4, 0, 8, 104))
+        THIRD = ((0, 6, 0, 8, 0, 3, 0), (1, 6, 0, 2, 0, 3, 24), (1, 6, 6, 8, 0, 3, 120), (1, 4, 2, 4, 0, 2, 30), (3, 6, 4, 6, 1, 3, 114))
+
+        def load_list(i):
+            if i < 6:
+                b, s0, s1, n0 = SECOND[i]
+                nc.sync.dma_start(out=xa[NA + b:NA + 50:5, s0:s1, :], in_=two[:, n0:n0 + 2 * (s1 - s0):2, :])
+            elif i < 11:
+                ps, pe, s0, s1, a0, a1, n0 = THIRD[i - 6]
+                nc.sync.dma_start(out=xa[q0 + ps:q0 + pe:2, s0:s1, :], in_=three[a0:a1, n0:n0 + 3 * (s1 - s0):3, :])
+            elif i == 11:
+                nc.sync.dma_start(out=xa[q0 + 5:q0 + 6, 2:4, :], in_=row3[120:122, 0:1, :].rearrange("n o c -> o n c"))
+            else:
+                nc.sync.dma_start(out=xa[q0 + 1:q0 + 2, 4:6, :], in_=row3[12:14, 0:1, :].rearrange("n o c -> o n c"))
+
+        raw_w = [None] * 4
+
+        def load(tok):
+            kind, i = tok[0], tok[1:]
+            if kind == "L":
+                load_list(int(i))
+            elif kind == "E":
+                if raw_e[int(i[0])] is None:
+                    raw_e[int(i[0])] = r8("e" + i[0], [128, 8, 512], BF16)
+                load_e(int(i[0]), int(i[1]))
+            elif kind == "G":
+                if raw_g[int(i[0])] is None:
+                    raw_g[int(i[0])] = r8("g" + i[0], [128, 8, 512], BF16)
+                load_g(int(i[0]), int(i[1]))
+            elif kind == "W":
+                w = raw_w[int(i)] = r8("w" + i, [128, 2, 2048], BF16)
+                nc.sync.dma_start(out=w[:], in_=W_kv[256 * int(i):256 * int(i) + 256, :].rearrange("(n p) f -> p n f", p=128))
+            elif i == "1":
+                nc.sync.dma_start(out=raw_x[1][:], in_=xf[576:1600, :].rearrange("(p j) c -> p j c", j=8))
+            else:
+                nc.sync.dma_start(out=xa[0:NA], in_=xf[0:576, :].rearrange("(p j) c -> p j c", j=8))
+
+        for tok in LOADS:
+            load(tok)
+
+        ec = [codes("ek", "e", 2), codes("ev", "e", 2)]
+        gc = [codes("g0", "g", 2), codes("g1", "g", 2)]
+        xc = [codes("xa", "x", 2), codes("xb", "x", 2)]
+        wc = [codes("w%d" % i, "w", 4) for i in range(4)]
+        tcod = [codes("t%d" % i, "t", 4) for i in range(4)]
+        dc = {}
+
+        def bank(name):
+            return psum.tile([128, 512], F32, name=name, tag="ps", bufs=8)
+
+        def evict(on_dve, dst, src):
+            if on_dve:
+                nc.vector.tensor_copy(out=dst, in_=src)
+            else:
+                nc.scalar.copy(out=dst, in_=src)
+
+        def flips(words_of, dst4, dve):
+            outs = []
+            for h in range(2):
+                ps = bank("pst")
+                v = ps[:].rearrange("p (t u c) -> p t u c", t=2, u=2)
+                for t in range(2):
+                    for u in range(2):
+                        nc.tensor.transpose(v[:, t, u, :], words_of(2 * h + t, u), ident[:])
+                outs.append(v.rearrange("p t u c -> p t c u"))
+
+            def copies():
+                for h in range(2):
+                    evict(dve > h, dst4[:, 2 * h:2 * h + 2], outs[h])
+            return copies
+
+        def quads(pre):
+            return pre[:].bitcast(F32).rearrange("p (t c u) -> p t c u", t=4, u=2)
+
+        def e_job(e, grp, dve=0):
+            box = {}
+
+            def s0():
+                words = raw_e[e][:].bitcast(F32)
+                box["p"] = p4("epre")
+                box["c"] = flips(lambda t, u: words[:, 4 * grp + t, u:256:2], quads(box["p"]), dve)
+            return [s0, lambda: box["c"](), lambda: quant(ec[e], 512 * grp, E4X4, box["p"])]
+
+        def g_job(fb, act=0):
+            e, b = divmod(fb, 2)
+            box = {}
+
+            def s1():
+                pre = box["p"] = p4("gpre")
+                src = raw_g[e][:, 4 * b:4 * b + 4, :].rearrange("p h (j d) -> p h d j", j=4)
+                dst = pre[:].rearrange("p (h d j) -> p h d j", h=4, j=4)
+                if act:
+                    nc.scalar.copy(out=dst, in_=src)
+                else:
+                    nc.vector.tensor_copy(out=dst, in_=src)
+            return [lambda: None, s1, lambda: quant(gc[e], 512 * b, E5X4, box["p"])]
+
+        def d_job(fb, grp, dve=0, tdve=0, iact=0):
+            e, b = divmod(fb, 2)
+            box = {}
+
+            def s0():
+                if fb not in dc:
+                    dc[fb] = codes("d%d" % fb, "d", 4)
+                box["ps"] = []
+                for t in range(4):
+                    ps = bank("psd")
+                    a = 512 * grp + 128 * t
+                    nc.tensor.matmul_mx(
+                        out=ps[:], lhsT=ec[e][0][:, a:a + 128].bitcast(E4X4), lhsT_scale=ec[e][1][:, a:a + 128],
+                        rhs=gc[e][0][:, 512 * b:512 * b + 512].bitcast(E5X4), rhs_scale=gc[e][1][:, 512 * b:512 * b + 512],
+                        start=True, stop=True)
+                    box["ps"].append(ps)
+
+            def s1():
+                d = box["d"] = pool.tile([128, 4, 512], BF16, name="dsb", tag="dsb", bufs=3, align_bytes=64)
+                for t in range(4):
+                    src = box["ps"][t][:].rearrange("p (m u e) -> p u m e", u=2, e=2)
+                    dst = d[:, t, :].rearrange("p (u m e) -> p u m e", u=2, e=2)
+                    if t >= 4 - dve:
+                        nc.vector.tensor_scalar(out=dst, in0=src, scalar1=0.5, scalar2=None, op0=MULT)
+                    else:
+                        nc.scalar.activation(out=dst, in_=src, func=COPY, scale=0.5)
+
+            def s2():
+                words = box["d"][:].bitcast(F32)
+                box["tp"] = p4("tpre")
+                box["c"] = flips(lambda t, u: words[:, t, 128 * u:128 * u + 128], quads(box["tp"]), tdve)
+                pre = box["dp"] = p4("dpre")
+                pv = pre[:].rearrange("p (f t) -> p f t", t=4)
+                dv = box["d"][:].rearrange("p t f -> p f t")
+                if iact < 4:
+                    nc.vector.tensor_copy(out=pv[:, 128 * iact:, :], in_=dv[:, 128 * iact:, :])
+                if iact > 0:
+                    nc.scalar.copy(out=pv[:, 0:128 * iact, :], in_=dv[:, 0:128 * iact, :])
+
+            def s3():
+                box["c"]()
+                quant(dc[fb], 512 * grp, E5X4, box["dp"])
+            return [s0, s1, s2, s3, lambda: quant(tcod[fb], 512 * grp, E5X4, box["tp"])]
+
+        def x_job(grp, h):
+            box = {}
+
+            def s1():
+                v = raw_x[grp][:].rearrange("p (t two) c -> p two c t", two=2)
+                pre = box["p"] = p4("xpre")
+                nc.vector.tensor_tensor(out=pre[:].rearrange("p (c t) -> p c t", t=4),
+                                        in0=v[:, 0, 512 * h:512 * h + 512, :], in1=v[:, 1, 512 * h:512 * h + 512, :], op=ADD)
+            return [lambda: None, s1, lambda: quant(xc[grp], 512 * h, E4X4, box["p"])]
+
+        def w_job(fb, half, dve=0):
+            box = {}
+
+            def words_of(t, u):
+                return raw_w[2 * half + t // 2][:].bitcast(F32)[:, t % 2, 256 * fb + u:256 * fb + 256:2]
+
+            def s0():
+                box["p"] = p4("wpre")
+                box["c"] = flips(words_of, quads(box["p"]), dve)
+            return [s0, lambda: box["c"](), lambda: quant(wc[fb], 512 * half, E4X4, box["p"])]
+
+        def dw_job(n, pair, dve=0):
+            box = {}
+
+            def s0():
+                box["ps"] = []
+                for fb in (2 * pair, 2 * pair + 1):
+                    ps = bank("psw")
+                    for k, grp in enumerate((1, 0)):
+                        nc.tensor.matmul_mx(
+                            out=ps[:], lhsT=xc[grp][0][:, 128 * n:128 * n + 128].bitcast(E4X4), lhsT_scale=xc[grp][1][:, 128 * n:128 * n + 128],
+                            rhs=dc[fb][0][:, 512 * grp:512 * grp + 512].bitcast(E5X4), rhs_scale=dc[fb][1][:, 512 * grp:512 * grp + 512],
+                            start=(k == 0), stop=(k == 1))
+                    box["ps"].append(ps)
+
+            def s1():
+                ob = box["o"] = pool.tile([128, 1024], F32, name="ob", tag="ob", bufs=4, align_bytes=64)
+                for i in range(2):
+                    evict(dve > i, ob[:, 512 * i:512 * i + 512].rearrange("p (m u e) -> p m u e", u=2, e=2),
+                          box["ps"][i][:].rearrange("p (u m e) -> p m u e", u=2, e=2))
+
+            def s2():
+                nc.sync.dma_start(out=out_1[128 * n:128 * n + 128, 1024 * pair:1024 * pair + 1024], in_=box["o"][:])
+            return [s0, s1, s2]
+
+        of = out_0[0]
+        parked = out_1[768:992, 1024:2048]
+        ys = {}
+
+        def dx_job(grp, t, dve=0):
+            box = {}
+
+            def s0():
+                a = 512 * grp + 128 * t
+                box["ps"] = []
+                for h in range(2):
+                    ps = bank("psx")
+                    for fb in range(4):
+                        nc.tensor.matmul_mx(
+                            out=ps[:], lhsT=tcod[fb][0][:, a:a + 128].bitcast(E5X4), lhsT_scale=tcod[fb][1][:, a:a + 128],
+                            rhs=wc[fb][0][:, 512 * h:512 * h + 512].bitcast(E4X4), rhs_scale=wc[fb][1][:, 512 * h:512 * h + 512],
+                            start=(fb == 0), stop=(fb == 3))
+                    box["ps"].append(ps)
+
+            def s1():
+                y = ys[(grp, t)] = r8("y", [128, 2, 1024], F32)
+                for h in range(2):
+                    evict(dve > h, y[:, 1, 512 * h:512 * h + 512], box["ps"][h][:])
+
+            def s2():
+                if grp == 0:
+                    nc.sync.dma_start(out=parked.rearrange("(q t) c -> q t c", t=4)[:, t, :], in_=ys[(0, t)][NA:128, 1, :])
+            return [s0, s1, s2]
+
+        xt_box = []
+
+        def xz_job():
+            def s0():
+                xt = pool.tile([128, 2, 2048], F32, name="xt", align_bytes=64)
+                xt_box.append(xt)
+                nc.vector.memset(xt[:].bitcast(I32), 0)
+            return [s0]
+
+        def xr_job(grp):
+            def s0():
+                xt = xt_box[0]
+                pr = parked[0:200, :].rearrange("(r s) c -> r s c", s=10)
+                for a in range(5):
+                    if grp == 0:
+                        r0, r1, p0, p1 = 0, (8 if a < 2 else 7), a, NA
+                    else:
+                        r0 = 8 if a < 2 else 7
+                        r1, p0, p1 = 20, 10 * r0 + a - NA, 128
+                    nc.sync.dma_start(out=xt[p0:p1:10, grp, :].rearrange("p (s c) -> p s c", s=2), in_=pr[r0:r1, 2 * a:2 * a + 2, :])
+            return [s0]
+
+        def fin_job(grp, t):
+            def s0():
+                y = ys[(grp, t)]
+                b = t // 2
+                nc.vector.tensor_tensor(out=y[:, 0, :], in0=y[:, 1, :], in1=xt_box[0][:, grp, 1024 * b:1024 * b + 1024], op=ADD)
+
+            def s1():
+                y = ys[(grp, t)]
+                if grp == 0:
+                    nc.sync.dma_start(out=of[0:576, :].rearrange("(p j) c -> p j c", j=8)[:, 2 * t:2 * t + 2, :], in_=y[0:NA])
+                else:
+                    nc.sync.dma_start(out=of[576:1600, :].rearrange("(p j) c -> p j c", j=8)[:, 2 * t:2 * t + 2, :], in_=y[:])
+            return [s0, s1]
+
+        def third_job():
+            rows = of[0:480, :].rearrange("(r c three) k -> r c three k", r=4, three=3)
+            box = {}
+
+            def s0():
+                z0 = box["a"] = pool.tile([128, 1024], F32, name="z0", tag="dsb", bufs=3, align_bytes=64)
+                z1 = box["b"] = pool.tile([128, 1024], F32, name="z1", tag="dsb", bufs=3, align_bytes=64)
+                for d in range(2):
+                    nc.gpsimd.dma_start(out=z0[d:48:2, :], in_=parked[200:224, :])
+                for r in range(4):
+                    m = 14 if r < 3 else 6
+                    nc.gpsimd.dma_start(out=z1[14 * r:14 * r + m, :], in_=rows[r, 0:m, 0, :])
+
+            def s1():
+                nc.vector.tensor_tensor(out=box["a"][0:48, :], in0=box["a"][0:48, :], in1=box["b"][0:48, :], op=ADD)
+
+            def s2():
+                for r in range(4):
+                    m = 14 if r < 3 else 6
+                    nc.gpsimd.dma_start(out=rows[r, 0:m, 0, :], in_=box["a"][14 * r:14 * r + m, :])
+            return [s0, s1, s2]
+
+        JOBS = {"E": e_job, "G": g_job, "D": d_job, "X": x_job, "W": w_job, "DW": dw_job, "DX": dx_job,
+                "XZ": xz_job, "XR": xr_job, "FIN": fin_job, "L3": third_job}
+        jobs = [JOBS[o[0]](*o[1:]) if o else [] for o in ORDER]
+        depth = 5
+        for i in range(len(jobs) + depth):
+            for s in range(depth - 1, -1, -1):
+                if 0 <= i - s < len(jobs) and s < len(jobs[i - s]):
+                    jobs[i - s][s]()

@@ -17,407 +17,306 @@ MULT = mybir.AluOpType.mult
 FLOPS = 2 * 1024 * 512 * 2048 + 2 * 1024 * 2048 * 1024 + 2 * 1024 * 1024 * 2048
 BYTES = 2 * (1600 * 1024 + 1024 * 2048 + 2 * 1024 * 512 + 2 * 512 * 1024) + 4 * (1600 * 1024 + 1024 * 2048)
 
-LOADS = "G00 G01 E00 E01 L5 E11 W1 L9 L4 X1 L1 W2 L11 L2 G10 L0 W3 E10 G11 L10 L8 L6 W0 L7 L3 X0 L12".split()
-
-ORDER = [
-    ("XZ",),
-    ("G", 1, 0),
-    ("G", 0, 1),
-    ("E", 0, 0, 0),
-    ("E", 0, 1, 0),
-    ("E", 1, 1, 2),
-    ("D", 0, 1, 1, 1, 0),
-    ("D", 0, 0, 0, 0, 3),
-    ("D", 1, 0, 3, 0, 3),
-    ("D", 1, 1, 3, 0, 2),
-    ("X", 1, 1),
-    ("W", 1, 1, 0),
-    ("E", 1, 0, 0),
-    ("G", 3, 0),
-    ("G", 2, 1),
-    ("W", 3, 1, 0),
-    ("X", 0, 1),
-    ("W", 3, 0, 0),
-    ("W", 0, 0, 0),
-    ("D", 3, 0, 0, 0, 0),
-    ("W", 1, 0, 1),
-    ("D", 2, 0, 0, 1, 3),
-    ("DW", 5, 0, 2),
-    ("W", 2, 0, 1),
-    ("W", 0, 1, 0),
-    ("W", 2, 1, 1),
-    ("X", 1, 0),
-    ("D", 2, 1, 0, 2, 4),
-    ("DX", 0, 3, 0),
-    ("DX", 0, 0, 0),
-    ("DX", 0, 2, 0),
-    ("X", 0, 0),
-    ("DX", 0, 1, 1),
-    ("DW", 3, 0, 0),
-    ("DW", 2, 0, 1),
-    ("DW", 0, 0, 0),
-    ("D", 3, 1, 2, 1, 2),
-    ("DW", 7, 0, 2),
-    ("XR", 0),
-    ("DW", 6, 0, 0),
-    ("DW", 1, 0, 0),
-    ("FIN", 0, 1),
-    ("FIN", 0, 0),
-    ("FIN", 0, 2),
-    ("FIN", 0, 3),
-    ("DW", 0, 1, 0),
-    ("DW", 3, 1, 0),
-    ("DX", 1, 1, 1),
-    ("DX", 1, 2, 1),
-    ("DW", 5, 1, 1),
-    ("XR", 1),
-    ("DW", 1, 1, 2),
-    ("DW", 2, 1, 0),
-    ("FIN", 1, 2),
-    ("DX", 1, 0, 1),
-    ("FIN", 1, 1),
-    ("L3",),
-    ("DW", 6, 1, 0),
-    ("DW", 4, 0, 0),
-    ("FIN", 1, 0),
-    ("DW", 4, 1, 2),
-    ("DX", 1, 3, 2),
-    ("FIN", 1, 3),
-    ("DW", 7, 1, 2),
-]
-
-NA = 72
+LISTS = 56
+SECOND = 50
 
 
 def tile_efficientmultiscaledilatedattention_pa_v_kernel(tc, x, W_kv, b_kv, E_k, E_v, kv, grad_0, grad_1, out_0, out_1):
     nc = tc.nc
     with ExitStack() as ctx:
-        const = ctx.enter_context(tc.tile_pool(name="const", bufs=1))
         pool = ctx.enter_context(tc.tile_pool(name="pool", bufs=1))
         psum = ctx.enter_context(tc.psum_pool(name="psum", bufs=1))
-
         ctx.enter_context(tc.manual_schedule())
-        ident = const.tile([128, 128], F32, name="ident", align_bytes=64)
+
+        ident = pool.tile([128, 128], F32, name="ident", align_bytes=64)
         make_identity(nc, ident[:])
 
-        def r8(name, shape, dt):
-            return pool.tile(shape, dt, name=name, tag="r8", bufs=6, align_bytes=64)
+        def row(name, shape, dt):
+            return pool.tile(shape, dt, name=name, tag="row", bufs=16, align_bytes=64)
 
-        def p4(name):
-            return pool.tile([128, 2048], BF16, name=name, tag="p4", bufs=6, align_bytes=64)
+        def stage(name):
+            return pool.tile([128, 2048], BF16, name=name, tag="stage", bufs=5, align_bytes=64)
 
-        def codes(name, tag, bufs):
-            c = pool.tile([128, 1024], U32, name=name + "c", tag=tag + "c", bufs=bufs, align_bytes=64)
-            s = pool.tile([128, 1024], U8, name=name + "s", tag=tag + "s", bufs=bufs, align_bytes=64)
-            return c, s
+        def operand(name):
+            codes = pool.tile([128, 1024], U32, name=name + "_codes", align_bytes=64)
+            scales = pool.tile([128, 1024], U8, name=name + "_scales", align_bytes=64)
+            return codes, scales
 
-        def quant(cs, a, fmt, src):
-            c, s = cs
-            nc.vector.quantize_mx(out=c[:, a:a + 512].bitcast(fmt), scales=s[:, a:a + 512], in_=src[:])
+        def quantise(op, col, fmt, src):
+            nc.vector.quantize_mx(out=op[0][:, col:col + 512].bitcast(fmt), scales=op[1][:, col:col + 512], in_=src[:])
 
-        xf = x[0]
-        raw_e = [None, None]
-        raw_g = [None, None]
-        e_src = [E_k, E_v]
-        g_src = [grad_0[0], grad_1[0]]
-
-        def load_e(e, grp):
-            t = raw_e[e]
-            if grp == 1:
-                nc.sync.dma_start(out=t[:, 4:8, :], in_=e_src[e][288:800, :].rearrange("(p t) k -> p t k", t=4))
-            else:
-                nc.sync.dma_start(out=t[0:NA, 0:4, :], in_=e_src[e][0:288, :].rearrange("(p t) k -> p t k", t=4))
-                nc.sync.dma_start(out=t[NA:128, 0:4, :], in_=e_src[e][800:1024, :].rearrange("(p t) k -> p t k", t=4))
-
-        def load_g(e, b):
-            nc.sync.dma_start(out=raw_g[e][:, 4 * b:4 * b + 4, :],
-                              in_=g_src[e][4 * b:4 * b + 4].rearrange("h (p j) d -> p h (j d)", j=4))
-
-        raw_x = {}
-        raw_x[1] = pool.tile([128, 8, 1024], BF16, name="xB", tag="x16", bufs=2, align_bytes=64)
-        raw_x[0] = pool.tile([128, 8, 1024], BF16, name="xA", tag="x16", bufs=2, align_bytes=64)
-        xa = raw_x[0]
-        two = xf.rearrange("(a n) c -> a n c", n=160)
-        three = xf[0:378, :].rearrange("(a n) c -> a n c", n=126)
-        row3 = xf[0:480, :].rearrange("(n three) c -> n three c", three=3)
-        q0 = NA + 50
-        SECOND = ((0, 0, 8, 0), (1, 0, 8, 16), (2, 0, 4, 32), (2, 4, 8, 80), (3, 0, 8, 88), (4, 0, 8, 104))
-        THIRD = ((0, 6, 0, 8, 0, 3, 0), (1, 6, 0, 2, 0, 3, 24), (1, 6, 6, 8, 0, 3, 120), (1, 4, 2, 4, 0, 2, 30), (3, 6, 4, 6, 1, 3, 114))
-
-        def load_list(i):
-            if i < 6:
-                b, s0, s1, n0 = SECOND[i]
-                nc.sync.dma_start(out=xa[NA + b:NA + 50:5, s0:s1, :], in_=two[:, n0:n0 + 2 * (s1 - s0):2, :])
-            elif i < 11:
-                ps, pe, s0, s1, a0, a1, n0 = THIRD[i - 6]
-                nc.sync.dma_start(out=xa[q0 + ps:q0 + pe:2, s0:s1, :], in_=three[a0:a1, n0:n0 + 3 * (s1 - s0):3, :])
-            elif i == 11:
-                nc.sync.dma_start(out=xa[q0 + 5:q0 + 6, 2:4, :], in_=row3[120:122, 0:1, :].rearrange("n o c -> o n c"))
-            else:
-                nc.sync.dma_start(out=xa[q0 + 1:q0 + 2, 4:6, :], in_=row3[12:14, 0:1, :].rearrange("n o c -> o n c"))
-
-        raw_w = [None] * 4
-
-        def load(tok):
-            kind, i = tok[0], tok[1:]
-            if kind == "L":
-                load_list(int(i))
-            elif kind == "E":
-                if raw_e[int(i[0])] is None:
-                    raw_e[int(i[0])] = r8("e" + i[0], [128, 8, 512], BF16)
-                load_e(int(i[0]), int(i[1]))
-            elif kind == "G":
-                if raw_g[int(i[0])] is None:
-                    raw_g[int(i[0])] = r8("g" + i[0], [128, 8, 512], BF16)
-                load_g(int(i[0]), int(i[1]))
-            elif kind == "W":
-                w = raw_w[int(i)] = r8("w" + i, [128, 2, 2048], BF16)
-                nc.sync.dma_start(out=w[:], in_=W_kv[256 * int(i):256 * int(i) + 256, :].rearrange("(n p) f -> p n f", p=128))
-            elif i == "1":
-                nc.sync.dma_start(out=raw_x[1][:], in_=xf[576:1600, :].rearrange("(p j) c -> p j c", j=8))
-            else:
-                nc.sync.dma_start(out=xa[0:NA], in_=xf[0:576, :].rearrange("(p j) c -> p j c", j=8))
-
-        for tok in LOADS:
-            load(tok)
-
-        ec = [codes("ek", "e", 2), codes("ev", "e", 2)]
-        gc = [codes("g0", "g", 2), codes("g1", "g", 2)]
-        xc = [codes("xa", "x", 2), codes("xb", "x", 2)]
-        wc = [codes("w%d" % i, "w", 4) for i in range(4)]
-        tcod = [codes("t%d" % i, "t", 4) for i in range(4)]
-        dc = {}
+        def mx(out, lhs, lfmt, lcol, rhs, rfmt, rcol, n, start, stop):
+            nc.tensor.matmul_mx(out=out, lhsT=lhs[0][:, lcol:lcol + 128].bitcast(lfmt), lhsT_scale=lhs[1][:, lcol:lcol + 128],
+                                rhs=rhs[0][:, rcol:rcol + n].bitcast(rfmt), rhs_scale=rhs[1][:, rcol:rcol + n],
+                                start=start, stop=stop)
 
         def bank(name):
-            return psum.tile([128, 512], F32, name=name, tag="ps", bufs=8)
+            return psum.tile([128, 512], F32, name=name, tag="bank", bufs=8)
 
-        def evict(on_dve, dst, src):
-            if on_dve:
+        def move(on_vector, dst, src):
+            if on_vector:
                 nc.vector.tensor_copy(out=dst, in_=src)
             else:
                 nc.scalar.copy(out=dst, in_=src)
 
-        def flips(words_of, dst4, dve):
-            outs = []
-            for h in range(2):
-                ps = bank("pst")
-                v = ps[:].rearrange("p (t u c) -> p t u c", t=2, u=2)
-                for t in range(2):
-                    for u in range(2):
-                        nc.tensor.transpose(v[:, t, u, :], words_of(2 * h + t, u), ident[:])
-                outs.append(v.rearrange("p t u c -> p t c u"))
+        def halve(on_vector, dst, src):
+            if on_vector:
+                nc.vector.tensor_scalar(out=dst, in0=src, scalar1=0.5, scalar2=None, op0=MULT)
+            else:
+                nc.scalar.activation(out=dst, in_=src, func=COPY, scale=0.5)
 
-            def copies():
-                for h in range(2):
-                    evict(dve > h, dst4[:, 2 * h:2 * h + 2], outs[h])
-            return copies
+        side = nc.gpsimd
+        xf = x[0]
+        of = out_0[0]
+        e_src = [E_k, E_v]
+        g_src = [grad_0[0], grad_1[0]]
+        parked = of[576:1024, :].rearrange("(m e) c -> m e c", e=2)[:, 1, :]
 
-        def quads(pre):
-            return pre[:].bitcast(F32).rearrange("p (t c u) -> p t c u", t=4, u=2)
+        raw_e, raw_g, raw_w = {}, {}, {}
 
-        def e_job(e, grp, dve=0):
+        def load_e(e, grp):
+            raw_e[(e, grp)] = row("raw_e", [128, 4, 512], BF16)
+            nc.sync.dma_start(out=raw_e[(e, grp)][:], in_=e_src[e][512 * grp:512 * grp + 512, :].rearrange("(p t) k -> p t k", t=4))
+
+        def load_g(fb):
+            e, b = divmod(fb, 2)
+            raw_g[fb] = row("raw_g", [128, 4, 512], BF16)
+            nc.sync.dma_start(out=raw_g[fb][:], in_=g_src[e][4 * b:4 * b + 4].rearrange("h (p j) d -> p h (j d)", j=4))
+
+        def load_w(i):
+            raw_w[i] = row("raw_w", [128, 2048], BF16)
+            nc.sync.dma_start(out=raw_w[i][:], in_=W_kv[128 * i:128 * i + 128, :])
+
+        raw_x = [pool.tile([128, 8, 1024], BF16, name="raw_x%d" % grp, align_bytes=64) for grp in range(2)]
+        even = xf.rearrange("(r n) c -> r n c", n=80)
+        third = xf[0:480, :].rearrange("(r n) c -> r n c", n=120)
+        runs = []
+        entry = 0
+        while entry < 48:
+            runs.append((entry, min(14 - entry % 14, 8 - entry % 8, 48 - entry)))
+            entry = entry + runs[-1][1]
+
+        def load_third(i):
+            entry, m = runs[i]
+            r, c = divmod(entry, 14)
+            p, s = divmod(entry, 8)
+            nc.sync.dma_start(out=raw_x[1][SECOND + p:SECOND + p + 1, s:s + m, :], in_=third[r:r + 1, 3 * c:3 * (c + m):3, :])
+
+        def load_x(part):
+            if part == 0:
+                nc.sync.dma_start(out=raw_x[0][:], in_=xf[0:1024, :].rearrange("(p j) c -> p j c", j=8))
+            elif part == 1:
+                nc.sync.dma_start(out=raw_x[1][LISTS:128], in_=xf[1024:1600, :].rearrange("(p j) c -> p j c", j=8))
+            else:
+                nc.sync.dma_start(out=raw_x[1][0:SECOND], in_=even[:, 0:40:2, :])
+
+        load_g(0)
+        load_e(0, 1)
+        load_g(1)
+        load_e(1, 1)
+        load_g(2)
+        load_g(3)
+        for i in range(8):
+            load_w(i)
+        load_e(0, 0)
+        load_e(1, 0)
+        load_x(0)
+        for i in range(len(runs)):
+            load_third(i)
+        load_x(2)
+        load_x(1)
+        extra = [pool.tile([128, 2, 1024], F32, name="extra%d" % grp, align_bytes=64) for grp in range(2)]
+
+        ec = [operand("ek"), operand("ev")]
+        gc = [operand("gk"), operand("gv")]
+        xc = [operand("x0"), operand("x1")]
+        wc = [operand("w%d" % i) for i in range(4)]
+        fc = [operand("f%d" % i) for i in range(4)]
+        lc = [operand("l%d" % i) for i in range(4)]
+
+        def nothing():
+            return None
+
+        def flip_job(words_of, op, col, vec, lag, turn=0):
             box = {}
 
             def s0():
-                words = raw_e[e][:].bitcast(F32)
-                box["p"] = p4("epre")
-                box["c"] = flips(lambda t, u: words[:, 4 * grp + t, u:256:2], quads(box["p"]), dve)
-            return [s0, lambda: box["c"](), lambda: quant(ec[e], 512 * grp, E4X4, box["p"])]
+                box["ps"] = []
+                for half in range(2):
+                    ps = bank("flip")
+                    v = ps[:].rearrange("p (t u c) -> p t u c", t=2, u=2)
+                    for t in range(2):
+                        for u in range(2):
+                            nc.tensor.transpose(v[:, t, u, :], words_of(2 * half + t, u), ident[:])
+                    box["ps"].append(v.rearrange("p t u c -> p t c u"))
 
-        def g_job(fb, act=0):
+            def s1():
+                box["st"] = stage("flipped")
+                dst = box["st"][:].bitcast(F32).rearrange("p (t c u) -> p t c u", t=4, u=2)
+                for half in range(2):
+                    pair = slice(2 * half, 2 * half + 2)
+                    if turn:
+                        move(half < vec, dst[:, pair, 0:turn], box["ps"][half][:, :, 128 - turn:128])
+                    move(half < vec, dst[:, pair, turn:128], box["ps"][half][:, :, 0:128 - turn])
+            return [s0, s1] + [nothing] * lag + [lambda: quantise(op, col, E4X4, box["st"])]
+
+        def e_job(e, grp, vec=0, lag=0):
+            return flip_job(lambda t, u: raw_e[(e, grp)][:].bitcast(F32)[:, t, u:256:2], ec[e], 512 * grp, vec, lag, LISTS * grp)
+
+        def w_job(fb, h, vec=0, lag=0):
+            return flip_job(lambda t, u: raw_w[4 * h + t][:].bitcast(F32)[:, 256 * fb + u:256 * fb + 256:2], wc[fb], 512 * h, vec, lag)
+
+        def g_job(fb):
             e, b = divmod(fb, 2)
             box = {}
 
             def s1():
-                pre = box["p"] = p4("gpre")
-                src = raw_g[e][:, 4 * b:4 * b + 4, :].rearrange("p h (j d) -> p h d j", j=4)
-                dst = pre[:].rearrange("p (h d j) -> p h d j", h=4, j=4)
-                if act:
-                    nc.scalar.copy(out=dst, in_=src)
-                else:
-                    nc.vector.tensor_copy(out=dst, in_=src)
-            return [lambda: None, s1, lambda: quant(gc[e], 512 * b, E5X4, box["p"])]
+                box["st"] = stage("g_sorted")
+                nc.vector.tensor_copy(out=box["st"][:].rearrange("p (j h m k) -> p j h m k", j=4, h=4, k=4),
+                                      in_=raw_g[fb][:].rearrange("p h (k m j) -> p j h m k", k=4, j=4))
+            return [s1, lambda: quantise(gc[e], 512 * b, E5X4, box["st"])]
 
-        def d_job(fb, grp, dve=0, tdve=0, iact=0):
+        def dkv_job(fb, grp, by_feature, vec=1, lag=0):
             e, b = divmod(fb, 2)
             box = {}
 
             def s0():
-                if fb not in dc:
-                    dc[fb] = codes("d%d" % fb, "d", 4)
                 box["ps"] = []
-                for t in range(4):
-                    ps = bank("psd")
-                    a = 512 * grp + 128 * t
-                    nc.tensor.matmul_mx(
-                        out=ps[:], lhsT=ec[e][0][:, a:a + 128].bitcast(E4X4), lhsT_scale=ec[e][1][:, a:a + 128],
-                        rhs=gc[e][0][:, 512 * b:512 * b + 512].bitcast(E5X4), rhs_scale=gc[e][1][:, 512 * b:512 * b + 512],
-                        start=True, stop=True)
+                for i in range(4):
+                    ps = bank("dkv")
+                    for k in range(4):
+                        if by_feature:
+                            mx(ps[:, 128 * k:128 * k + 128], gc[e], E5X4, 512 * b + 128 * k, ec[e], E4X4, 512 * grp + 128 * i, 128, True, True)
+                        else:
+                            mx(ps[:, 128 * k:128 * k + 128], ec[e], E4X4, 512 * grp + 128 * k, gc[e], E5X4, 512 * b + 128 * i, 128, True, True)
                     box["ps"].append(ps)
 
             def s1():
-                d = box["d"] = pool.tile([128, 4, 512], BF16, name="dsb", tag="dsb", bufs=3, align_bytes=64)
-                for t in range(4):
-                    src = box["ps"][t][:].rearrange("p (m u e) -> p u m e", u=2, e=2)
-                    dst = d[:, t, :].rearrange("p (u m e) -> p u m e", u=2, e=2)
-                    if t >= 4 - dve:
-                        nc.vector.tensor_scalar(out=dst, in0=src, scalar1=0.5, scalar2=None, op0=MULT)
-                    else:
-                        nc.scalar.activation(out=dst, in_=src, func=COPY, scale=0.5)
-
-            def s2():
-                words = box["d"][:].bitcast(F32)
-                box["tp"] = p4("tpre")
-                box["c"] = flips(lambda t, u: words[:, t, 128 * u:128 * u + 128], quads(box["tp"]), tdve)
-                pre = box["dp"] = p4("dpre")
-                pv = pre[:].rearrange("p (f t) -> p f t", t=4)
-                dv = box["d"][:].rearrange("p t f -> p f t")
-                if iact < 4:
-                    nc.vector.tensor_copy(out=pv[:, 128 * iact:, :], in_=dv[:, 128 * iact:, :])
-                if iact > 0:
-                    nc.scalar.copy(out=pv[:, 0:128 * iact, :], in_=dv[:, 0:128 * iact, :])
-
-            def s3():
-                box["c"]()
-                quant(dc[fb], 512 * grp, E5X4, box["dp"])
-            return [s0, s1, s2, s3, lambda: quant(tcod[fb], 512 * grp, E5X4, box["tp"])]
+                box["st"] = stage("dkv_bf16")
+                for i in range(4):
+                    move(i >= 4 - vec, box["st"][:, 512 * i:512 * i + 512].rearrange("p (n k) -> p n k", k=4),
+                         box["ps"][i][:].rearrange("p (k n) -> p n k", k=4))
+            return [s0, s1] + [nothing] * lag + [lambda: quantise((fc if by_feature else lc)[fb], 512 * grp, E5X4, box["st"])]
 
         def x_job(grp, h):
             box = {}
 
-            def s1():
-                v = raw_x[grp][:].rearrange("p (t two) c -> p two c t", two=2)
-                pre = box["p"] = p4("xpre")
-                nc.vector.tensor_tensor(out=pre[:].rearrange("p (c t) -> p c t", t=4),
-                                        in0=v[:, 0, 512 * h:512 * h + 512, :], in1=v[:, 1, 512 * h:512 * h + 512, :], op=ADD)
-            return [lambda: None, s1, lambda: quant(xc[grp], 512 * h, E4X4, box["p"])]
-
-        def w_job(fb, half, dve=0):
-            box = {}
-
-            def words_of(t, u):
-                return raw_w[2 * half + t // 2][:].bitcast(F32)[:, t % 2, 256 * fb + u:256 * fb + 256:2]
-
             def s0():
-                box["p"] = p4("wpre")
-                box["c"] = flips(words_of, quads(box["p"]), dve)
-            return [s0, lambda: box["c"](), lambda: quant(wc[fb], 512 * half, E4X4, box["p"])]
-
-        def dw_job(n, pair, dve=0):
-            box = {}
-
-            def s0():
-                box["ps"] = []
-                for fb in (2 * pair, 2 * pair + 1):
-                    ps = bank("psw")
-                    for k, grp in enumerate((1, 0)):
-                        nc.tensor.matmul_mx(
-                            out=ps[:], lhsT=xc[grp][0][:, 128 * n:128 * n + 128].bitcast(E4X4), lhsT_scale=xc[grp][1][:, 128 * n:128 * n + 128],
-                            rhs=dc[fb][0][:, 512 * grp:512 * grp + 512].bitcast(E5X4), rhs_scale=dc[fb][1][:, 512 * grp:512 * grp + 512],
-                            start=(k == 0), stop=(k == 1))
-                    box["ps"].append(ps)
+                v = raw_x[grp][:].rearrange("p (t two) c -> p two t c", two=2)
+                box["sum"] = stage("x_sum")
+                nc.vector.tensor_tensor(out=box["sum"][:].rearrange("p (t c) -> p t c", t=4),
+                                        in0=v[:, 0, :, 512 * h:512 * h + 512], in1=v[:, 1, :, 512 * h:512 * h + 512], op=ADD)
 
             def s1():
-                ob = box["o"] = pool.tile([128, 1024], F32, name="ob", tag="ob", bufs=4, align_bytes=64)
-                for i in range(2):
-                    evict(dve > i, ob[:, 512 * i:512 * i + 512].rearrange("p (m u e) -> p m u e", u=2, e=2),
-                          box["ps"][i][:].rearrange("p (u m e) -> p m u e", u=2, e=2))
+                box["st"] = stage("x_sorted")
+                nc.vector.tensor_copy(out=box["st"][:].rearrange("p (c t) -> p c t", t=4), in_=box["sum"][:].rearrange("p (t c) -> p c t", t=4))
+            return [s0, s1, lambda: quantise(xc[grp], 512 * h, E4X4, box["st"])]
 
-            def s2():
-                nc.sync.dma_start(out=out_1[128 * n:128 * n + 128, 1024 * pair:1024 * pair + 1024], in_=box["o"][:])
-            return [s0, s1, s2]
+        def tokens(grp, j):
+            return of[576 * grp:576 * grp + 1024, :].rearrange("(p j) c -> p j c", j=8)[:, j, :]
 
-        of = out_0[0]
-        parked = out_1[768:992, 1024:2048]
         ys = {}
 
-        def dx_job(grp, t, dve=0):
+        def dx_job(grp, t, h, vec=0):
             box = {}
 
             def s0():
-                a = 512 * grp + 128 * t
-                box["ps"] = []
-                for h in range(2):
-                    ps = bank("psx")
-                    for fb in range(4):
-                        nc.tensor.matmul_mx(
-                            out=ps[:], lhsT=tcod[fb][0][:, a:a + 128].bitcast(E5X4), lhsT_scale=tcod[fb][1][:, a:a + 128],
-                            rhs=wc[fb][0][:, 512 * h:512 * h + 512].bitcast(E4X4), rhs_scale=wc[fb][1][:, 512 * h:512 * h + 512],
-                            start=(fb == 0), stop=(fb == 3))
-                    box["ps"].append(ps)
+                box["ps"] = bank("dx")
+                for fb in range(4):
+                    mx(box["ps"][:], fc[fb], E5X4, 512 * grp + 128 * t, wc[fb], E4X4, 512 * h, 512, fb == 0, fb == 3)
 
             def s1():
-                y = ys[(grp, t)] = r8("y", [128, 2, 1024], F32)
-                for h in range(2):
-                    evict(dve > h, y[:, 1, 512 * h:512 * h + 512], box["ps"][h][:])
+                cols = slice(512 * h, 512 * h + 512)
+                if h == 0:
+                    ys[(grp, t, 1)] = row("y_second", [128, 1024], F32)
+                halve(vec, ys[(grp, t, 1)][:, cols], box["ps"][:])
 
             def s2():
-                if grp == 0:
-                    nc.sync.dma_start(out=parked.rearrange("(q t) c -> q t c", t=4)[:, t, :], in_=ys[(0, t)][NA:128, 1, :])
+                if h == 1:
+                    nc.sync.dma_start(out=tokens(grp, 2 * t + 1), in_=ys[(grp, t, 1)][:])
             return [s0, s1, s2]
 
-        xt_box = []
+        def zero_job(grp):
+            return [lambda: nc.vector.memset(extra[grp][:].bitcast(I32), 0)]
 
-        def xz_job():
+        def fetch_job(grp):
             def s0():
-                xt = pool.tile([128, 2, 2048], F32, name="xt", align_bytes=64)
-                xt_box.append(xt)
-                nc.vector.memset(xt[:].bitcast(I32), 0)
-            return [s0]
-
-        def xr_job(grp):
-            def s0():
-                xt = xt_box[0]
                 pr = parked[0:200, :].rearrange("(r s) c -> r s c", s=10)
+                r0, r1, p0 = ((0, 13, 0), (13, 20, LISTS + 2))[grp]
                 for a in range(5):
-                    if grp == 0:
-                        r0, r1, p0, p1 = 0, (8 if a < 2 else 7), a, NA
-                    else:
-                        r0 = 8 if a < 2 else 7
-                        r1, p0, p1 = 20, 10 * r0 + a - NA, 128
-                    nc.sync.dma_start(out=xt[p0:p1:10, grp, :].rearrange("p (s c) -> p s c", s=2), in_=pr[r0:r1, 2 * a:2 * a + 2, :])
+                    (side if grp else nc.sync).dma_start(out=extra[grp][p0 + a:p0 + a + 10 * (r1 - r0) - 9:10], in_=pr[r0:r1, 2 * a:2 * a + 2, :])
+                if grp == 0:
+                    ys["third"] = row("third_add", [128, 1024], F32)
+                    for d in range(2):
+                        nc.sync.dma_start(out=ys["third"][d:48:2, :], in_=parked[200:224, :])
             return [s0]
 
-        def fin_job(grp, t):
+        def first_job(grp, t):
             def s0():
-                y = ys[(grp, t)]
-                b = t // 2
-                nc.vector.tensor_tensor(out=y[:, 0, :], in0=y[:, 1, :], in1=xt_box[0][:, grp, 1024 * b:1024 * b + 1024], op=ADD)
+                ys[(grp, t, 0)] = row("y_first", [128, 1024], F32)
+                nc.vector.tensor_tensor(out=ys[(grp, t, 0)][:], in0=ys[(grp, t, 1)][:], in1=extra[grp][:, t // 2, :], op=ADD)
 
             def s1():
-                y = ys[(grp, t)]
-                if grp == 0:
-                    nc.sync.dma_start(out=of[0:576, :].rearrange("(p j) c -> p j c", j=8)[:, 2 * t:2 * t + 2, :], in_=y[0:NA])
-                else:
-                    nc.sync.dma_start(out=of[576:1600, :].rearrange("(p j) c -> p j c", j=8)[:, 2 * t:2 * t + 2, :], in_=y[:])
+                nc.sync.dma_start(out=tokens(grp, 2 * t)[LISTS * grp:128], in_=ys[(grp, t, 0)][LISTS * grp:128, :])
             return [s0, s1]
 
         def third_job():
-            rows = of[0:480, :].rearrange("(r c three) k -> r c three k", r=4, three=3)
+            rows = of[0:480, :].rearrange("(r n) k -> r n k", n=120)
             box = {}
 
             def s0():
-                z0 = box["a"] = pool.tile([128, 1024], F32, name="z0", tag="dsb", bufs=3, align_bytes=64)
-                z1 = box["b"] = pool.tile([128, 1024], F32, name="z1", tag="dsb", bufs=3, align_bytes=64)
-                for d in range(2):
-                    nc.gpsimd.dma_start(out=z0[d:48:2, :], in_=parked[200:224, :])
-                for r in range(4):
-                    m = 14 if r < 3 else 6
-                    nc.gpsimd.dma_start(out=z1[14 * r:14 * r + m, :], in_=rows[r, 0:m, 0, :])
+                box["a"] = ys["third"]
+                box["b"] = row("third_old", [128, 1024], F32)
+                side.dma_start(out=box["b"][0:42, :], in_=rows[0:3, 0:42:3, :])
+                side.dma_start(out=box["b"][42:48, :], in_=rows[3, 0:18:3, :])
 
             def s1():
                 nc.vector.tensor_tensor(out=box["a"][0:48, :], in0=box["a"][0:48, :], in1=box["b"][0:48, :], op=ADD)
 
             def s2():
-                for r in range(4):
-                    m = 14 if r < 3 else 6
-                    nc.gpsimd.dma_start(out=rows[r, 0:m, 0, :], in_=box["a"][14 * r:14 * r + m, :])
+                side.dma_start(out=rows[0:3, 0:42:3, :], in_=box["a"][0:42, :])
+                side.dma_start(out=rows[3, 0:18:3, :], in_=box["a"][42:48, :])
+            return [s0, nothing, nothing, nothing, s1, s2]
+
+        obs = {}
+
+        def dw_job(n, pair, vec=0):
+            box = {}
+
+            def s0():
+                box["ps"] = []
+                for fb in (2 * pair, 2 * pair + 1):
+                    ps = bank("dw")
+                    for grp in range(2):
+                        mx(ps[:], xc[grp], E4X4, 128 * n, lc[fb], E5X4, 512 * grp, 512, grp == 0, grp == 1)
+                    box["ps"].append(ps)
+
+            def s1():
+                box["o"] = row("dw_out", [128, 1024], F32)
+                for i in range(2):
+                    halve(i < vec, box["o"][:, 512 * i:512 * i + 512].rearrange("p (m j) -> p m j", j=4),
+                          box["ps"][i][:].rearrange("p (j m) -> p m j", j=4))
+
+            def s2():
+                nc.sync.dma_start(out=out_1[128 * n:128 * n + 128, 1024 * pair:1024 * pair + 1024], in_=box["o"][:])
             return [s0, s1, s2]
 
-        JOBS = {"E": e_job, "G": g_job, "D": d_job, "X": x_job, "W": w_job, "DW": dw_job, "DX": dx_job,
-                "XZ": xz_job, "XR": xr_job, "FIN": fin_job, "L3": third_job}
-        jobs = [JOBS[o[0]](*o[1:]) if o else [] for o in ORDER]
-        depth = 5
+        gap = [nothing]
+        jobs = [zero_job(0), zero_job(1), g_job(0), e_job(0, 1), gap, e_job(1, 1, 0, 1), g_job(1), dkv_job(0, 1, True, 0, 2), g_job(2), dkv_job(1, 1, True, 0, 2), g_job(3),
+                dkv_job(2, 1, True, 1, 1), dkv_job(3, 1, True, 2, 1)]
+        jobs += [w_job(0, 0, 1, 1), w_job(1, 0, 1, 1), dkv_job(0, 1, False, 2, 2), w_job(2, 0, 1), w_job(3, 0, 1), w_job(0, 1, 1)]
+        jobs += [dx_job(1, 0, 0), dx_job(1, 1, 0), w_job(1, 1, 1), w_job(2, 1, 1), dx_job(1, 2, 0), dx_job(1, 3, 0), w_job(3, 1, 1), e_job(0, 0, 1), e_job(1, 0, 1)]
+        jobs += [dx_job(1, 0, 1), dx_job(1, 1, 1), x_job(0, 0), dx_job(1, 2, 1), dx_job(1, 3, 1)]
+        jobs += [dkv_job(0, 0, True, 0, 1), fetch_job(1), dkv_job(1, 0, True, 1, 1), fetch_job(0), dkv_job(2, 0, True, 1, 1), dkv_job(3, 0, True, 1), dkv_job(0, 0, False, 1, 1), x_job(1, 0)]
+        jobs += [dx_job(0, 0, 0), dx_job(0, 0, 1), dkv_job(1, 1, False, 0, 1), dx_job(0, 1, 0), dx_job(0, 1, 1), dkv_job(1, 0, False, 1), first_job(0, 0)]
+        jobs += [dx_job(0, 2, 0), first_job(0, 1), dx_job(0, 2, 1), dx_job(0, 3, 0), x_job(0, 1), dx_job(0, 3, 1), first_job(0, 2), dw_job(0, 0), first_job(0, 3)]
+        jobs += [dw_job(1, 0), x_job(1, 1), dw_job(2, 0), dw_job(3, 0)]
+        for t in range(4):
+            jobs += [dkv_job(2 + t // 2, t % 2, False, 1, 1), first_job(1, t), dw_job(4 + t, 0)]
+        jobs += [third_job()]
+        for n in range(8):
+            jobs += [dw_job(n, 1, 1)]
+        depth = max(len(j) for j in jobs)
         for i in range(len(jobs) + depth):
             for s in range(depth - 1, -1, -1):
                 if 0 <= i - s < len(jobs) and s < len(jobs[i - s]):

@@ -32,7 +32,10 @@ def tile_efficientmultiscaledilatedattention_pa_v_kernel(tc, x, W_kv, b_kv, E_k,
         make_identity(nc, ident[:])
 
         def row(name, shape, dt):
-            return pool.tile(shape, dt, name=name, tag="row", bufs=16, align_bytes=64)
+            return pool.tile(shape, dt, name=name, tag="row", bufs=11, align_bytes=64)
+
+        def wide(name, shape, dt):
+            return pool.tile(shape, dt, name=name, tag="wide", bufs=4, align_bytes=64)
 
         def stage(name):
             return pool.tile([128, 2048], BF16, name=name, tag="stage", bufs=5, align_bytes=64)
@@ -84,8 +87,8 @@ def tile_efficientmultiscaledilatedattention_pa_v_kernel(tc, x, W_kv, b_kv, E_k,
             nc.sync.dma_start(out=raw_g[fb][:], in_=g_src[e][4 * b:4 * b + 4].rearrange("h (p j) d -> p h (j d)", j=4))
 
         def load_w(i):
-            raw_w[i] = row("raw_w", [128, 2048], BF16)
-            nc.sync.dma_start(out=raw_w[i][:], in_=W_kv[128 * i:128 * i + 128, :])
+            raw_w[i] = wide("raw_w", [128, 2, 2048], BF16)
+            nc.sync.dma_start(out=raw_w[i][:], in_=W_kv[256 * i:256 * i + 256, :].rearrange("(n p) f -> p n f", p=128))
 
         raw_x = [pool.tile([128, 8, 1024], BF16, name="raw_x%d" % grp, align_bytes=64) for grp in range(2)]
         even = xf.rearrange("(r n) c -> r n c", n=80)
@@ -108,7 +111,7 @@ def tile_efficientmultiscaledilatedattention_pa_v_kernel(tc, x, W_kv, b_kv, E_k,
             elif part == 1:
                 nc.sync.dma_start(out=raw_x[1][LISTS:128], in_=xf[1024:1600, :].rearrange("(p j) c -> p j c", j=8))
             else:
-                nc.sync.dma_start(out=raw_x[1][0:SECOND], in_=even[:, 0:40:2, :])
+                nc.scalar.dma_start(out=raw_x[1][0:SECOND], in_=even[:, 0:40:2, :])
 
         load_g(0)
         load_e(0, 1)
@@ -116,14 +119,13 @@ def tile_efficientmultiscaledilatedattention_pa_v_kernel(tc, x, W_kv, b_kv, E_k,
         load_e(1, 1)
         load_g(2)
         load_g(3)
-        for i in range(8):
+        for i in range(4):
             load_w(i)
-        load_e(0, 0)
-        load_e(1, 0)
+            load_third(2 * i)
+            load_third(2 * i + 1)
         load_x(0)
-        for i in range(len(runs)):
-            load_third(i)
-        load_x(2)
+        load_third(8)
+        load_e(0, 0)
         load_x(1)
         extra = [pool.tile([128, 2, 1024], F32, name="extra%d" % grp, align_bytes=64) for grp in range(2)]
 
@@ -164,7 +166,7 @@ def tile_efficientmultiscaledilatedattention_pa_v_kernel(tc, x, W_kv, b_kv, E_k,
             return flip_job(lambda t, u: raw_e[(e, grp)][:].bitcast(F32)[:, t, u:256:2], ec[e], 512 * grp, vec, lag, LISTS * grp)
 
         def w_job(fb, h, vec=0, lag=0):
-            return flip_job(lambda t, u: raw_w[4 * h + t][:].bitcast(F32)[:, 256 * fb + u:256 * fb + 256:2], wc[fb], 512 * h, vec, lag)
+            return flip_job(lambda t, u: raw_w[2 * h + t // 2][:].bitcast(F32)[:, t % 2, 256 * fb + u:256 * fb + 256:2], wc[fb], 512 * h, vec, lag)
 
         def g_job(fb):
             e, b = divmod(fb, 2)
@@ -227,14 +229,26 @@ def tile_efficientmultiscaledilatedattention_pa_v_kernel(tc, x, W_kv, b_kv, E_k,
 
             def s1():
                 cols = slice(512 * h, 512 * h + 512)
-                if h == 0:
-                    ys[(grp, t, 1)] = row("y_second", [128, 1024], F32)
-                halve(vec, ys[(grp, t, 1)][:, cols], box["ps"][:])
+                if grp == 1:
+                    if h == 0:
+                        ys[(grp, t, 1)] = row("y_second", [128, 1024], F32)
+                    halve(vec, ys[(grp, t, 1)][:, cols], box["ps"][:])
+                else:
+                    if h == 0:
+                        ys[t] = wide("y_both", [128, 2, 1024], F32)
+                    halve(vec, ys[t][:, 1, cols], box["ps"][:])
+                    nc.vector.scalar_tensor_tensor(out=ys[t][:, 0, cols], in0=box["ps"][:], scalar=0.5,
+                                                   in1=extra[0][:, t // 2, cols], op0=MULT, op1=ADD)
 
             def s2():
-                if h == 1:
+                if h == 1 and grp == 1:
                     nc.sync.dma_start(out=tokens(grp, 2 * t + 1), in_=ys[(grp, t, 1)][:])
+                elif h == 1:
+                    nc.sync.dma_start(out=of[0:1024, :].rearrange("(p j) c -> p j c", j=8)[:, 2 * t:2 * t + 2, :], in_=ys[t][:])
             return [s0, s1, s2]
+
+        def call_job(f, *args):
+            return [lambda: f(*args)]
 
         def zero_job(grp):
             return [lambda: nc.vector.memset(extra[grp][:].bitcast(I32), 0)]
@@ -276,7 +290,7 @@ def tile_efficientmultiscaledilatedattention_pa_v_kernel(tc, x, W_kv, b_kv, E_k,
             def s2():
                 side.dma_start(out=rows[0:3, 0:42:3, :], in_=box["a"][0:42, :])
                 side.dma_start(out=rows[3, 0:18:3, :], in_=box["a"][42:48, :])
-            return [s0, nothing, nothing, nothing, s1, s2]
+            return [s0, nothing, nothing, nothing, nothing, s1, s2]
 
         obs = {}
 
@@ -303,19 +317,17 @@ def tile_efficientmultiscaledilatedattention_pa_v_kernel(tc, x, W_kv, b_kv, E_k,
 
         gap = [nothing]
         jobs = [zero_job(0), zero_job(1), g_job(0), e_job(0, 1), gap, e_job(1, 1, 0, 1), g_job(1), dkv_job(0, 1, True, 0, 2), g_job(2), dkv_job(1, 1, True, 0, 2), g_job(3),
-                dkv_job(2, 1, True, 1, 1), dkv_job(3, 1, True, 2, 1)]
-        jobs += [w_job(0, 0, 1, 1), w_job(1, 0, 1, 1), dkv_job(0, 1, False, 2, 2), w_job(2, 0, 1), w_job(3, 0, 1), w_job(0, 1, 1)]
-        jobs += [dx_job(1, 0, 0), dx_job(1, 1, 0), w_job(1, 1, 1), w_job(2, 1, 1), dx_job(1, 2, 0), dx_job(1, 3, 0), w_job(3, 1, 1), e_job(0, 0, 1), e_job(1, 0, 1)]
-        jobs += [dx_job(1, 0, 1), dx_job(1, 1, 1), x_job(0, 0), dx_job(1, 2, 1), dx_job(1, 3, 1)]
-        jobs += [dkv_job(0, 0, True, 0, 1), fetch_job(1), dkv_job(1, 0, True, 1, 1), fetch_job(0), dkv_job(2, 0, True, 1, 1), dkv_job(3, 0, True, 1), dkv_job(0, 0, False, 1, 1), x_job(1, 0)]
-        jobs += [dx_job(0, 0, 0), dx_job(0, 0, 1), dkv_job(1, 1, False, 0, 1), dx_job(0, 1, 0), dx_job(0, 1, 1), dkv_job(1, 0, False, 1), first_job(0, 0)]
-        jobs += [dx_job(0, 2, 0), first_job(0, 1), dx_job(0, 2, 1), dx_job(0, 3, 0), x_job(0, 1), dx_job(0, 3, 1), first_job(0, 2), dw_job(0, 0), first_job(0, 3)]
-        jobs += [dw_job(1, 0), x_job(1, 1), dw_job(2, 0), dw_job(3, 0)]
+                dkv_job(2, 1, True, 1, 1), w_job(0, 0, 1, 1), dkv_job(3, 1, True, 2, 1)]
+        jobs += [w_job(1, 0, 1, 1), dkv_job(0, 1, False, 2, 2), w_job(2, 0, 1), w_job(3, 0, 1), dkv_job(1, 1, False, 2, 1), w_job(0, 1, 1, 1), call_job(load_x, 2), call_job(load_e, 1, 0)]
+        jobs += [dx_job(1, 0, 0), w_job(1, 1, 0, 1), dx_job(1, 1, 0), x_job(0, 0), w_job(2, 1), dx_job(1, 2, 0), w_job(3, 1), dx_job(1, 3, 0), x_job(0, 1), e_job(0, 0)]
+        jobs += [dx_job(1, 0, 1), dx_job(1, 1, 1), x_job(1, 0), dx_job(1, 2, 1), dx_job(1, 3, 1)]
+        jobs += [dkv_job(0, 0, False, 1), dkv_job(1, 0, False, 1), e_job(1, 0, 1, 1), fetch_job(1), dkv_job(0, 0, True, 1, 1), fetch_job(0)]
+        jobs += [dw_job(0, 0), dkv_job(1, 0, True, 1, 1), dw_job(1, 0), x_job(1, 1), dkv_job(2, 0, True, 0, 1), dw_job(2, 0), dkv_job(3, 0, True, 2), dw_job(3, 0), dw_job(4, 0, 1), dw_job(5, 0, 1)]
         for t in range(4):
-            jobs += [dkv_job(2 + t // 2, t % 2, False, 1, 1), first_job(1, t), dw_job(4 + t, 0)]
-        jobs += [third_job()]
-        for n in range(8):
-            jobs += [dw_job(n, 1, 1)]
+            jobs += [dx_job(0, t, 0), dx_job(0, t, 1), dkv_job(2 + t // 2, t % 2, False, 1, 1), first_job(1, t)]
+        jobs += [dw_job(6, 0, 1), dw_job(7, 0, 1), dw_job(0, 1, 1), third_job()]
+        for n in range(1, 8):
+            jobs += [dw_job(n, 1, n < 4)]
         depth = max(len(j) for j in jobs)
         for i in range(len(jobs) + depth):
             for s in range(depth - 1, -1, -1):

@@ -68,7 +68,6 @@ def tile_efficientmultiscaledilatedattention_pa_v_kernel(tc, x, W_kv, b_kv, E_k,
             else:
                 nc.scalar.activation(out=dst, in_=src, func=COPY, scale=0.5)
 
-        side = nc.gpsimd
         xf = x[0]
         of = out_0[0]
         e_src = [E_k, E_v]
@@ -174,8 +173,8 @@ def tile_efficientmultiscaledilatedattention_pa_v_kernel(tc, x, W_kv, b_kv, E_k,
 
             def s1():
                 box["st"] = stage("g_sorted")
-                nc.vector.tensor_copy(out=box["st"][:].rearrange("p (j h m k) -> p j h m k", j=4, h=4, k=4),
-                                      in_=raw_g[fb][:].rearrange("p h (k m j) -> p j h m k", k=4, j=4))
+                nc.vector.tensor_copy(out=box["st"][:].rearrange("p (j h m k) -> p h m j k", j=4, h=4, k=4),
+                                      in_=raw_g[fb][:].rearrange("p h (k m j) -> p h m j k", k=4, j=4))
             return [s1, lambda: quantise(gc[e], 512 * b, E5X4, box["st"])]
 
         def dkv_job(fb, grp, by_feature, vec=1, lag=0):
@@ -258,7 +257,7 @@ def tile_efficientmultiscaledilatedattention_pa_v_kernel(tc, x, W_kv, b_kv, E_k,
                 pr = parked[0:200, :].rearrange("(r s) c -> r s c", s=10)
                 r0, r1, p0 = ((0, 13, 0), (13, 20, LISTS + 2))[grp]
                 for a in range(5):
-                    (side if grp else nc.sync).dma_start(out=extra[grp][p0 + a:p0 + a + 10 * (r1 - r0) - 9:10], in_=pr[r0:r1, 2 * a:2 * a + 2, :])
+                    nc.sync.dma_start(out=extra[grp][p0 + a:p0 + a + 10 * (r1 - r0) - 9:10], in_=pr[r0:r1, 2 * a:2 * a + 2, :])
                 if grp == 0:
                     ys["third"] = row("third_add", [128, 1024], F32)
                     for d in range(2):
@@ -281,15 +280,15 @@ def tile_efficientmultiscaledilatedattention_pa_v_kernel(tc, x, W_kv, b_kv, E_k,
             def s0():
                 box["a"] = ys["third"]
                 box["b"] = row("third_old", [128, 1024], F32)
-                side.dma_start(out=box["b"][0:42, :], in_=rows[0:3, 0:42:3, :])
-                side.dma_start(out=box["b"][42:48, :], in_=rows[3, 0:18:3, :])
+                nc.sync.dma_start(out=box["b"][0:42, :], in_=rows[0:3, 0:42:3, :])
+                nc.sync.dma_start(out=box["b"][42:48, :], in_=rows[3, 0:18:3, :])
 
             def s1():
                 nc.vector.tensor_tensor(out=box["a"][0:48, :], in0=box["a"][0:48, :], in1=box["b"][0:48, :], op=ADD)
 
             def s2():
-                side.dma_start(out=rows[0:3, 0:42:3, :], in_=box["a"][0:42, :])
-                side.dma_start(out=rows[3, 0:18:3, :], in_=box["a"][42:48, :])
+                nc.sync.dma_start(out=rows[0:3, 0:42:3, :], in_=box["a"][0:42, :])
+                nc.sync.dma_start(out=rows[3, 0:18:3, :], in_=box["a"][42:48, :])
             return [s0, nothing, nothing, nothing, nothing, s1, s2]
 
         obs = {}
@@ -321,13 +320,13 @@ def tile_efficientmultiscaledilatedattention_pa_v_kernel(tc, x, W_kv, b_kv, E_k,
         jobs += [w_job(1, 0, 1, 1), dkv_job(0, 1, False, 2, 2), w_job(2, 0, 1), w_job(3, 0, 1), dkv_job(1, 1, False, 2, 1), w_job(0, 1, 1, 1), call_job(load_x, 2), call_job(load_e, 1, 0)]
         jobs += [dx_job(1, 0, 0), w_job(1, 1, 0, 1), dx_job(1, 1, 0), x_job(0, 0), w_job(2, 1), dx_job(1, 2, 0), w_job(3, 1), dx_job(1, 3, 0), x_job(0, 1), e_job(0, 0)]
         jobs += [dx_job(1, 0, 1), dx_job(1, 1, 1), x_job(1, 0), dx_job(1, 2, 1), dx_job(1, 3, 1)]
-        jobs += [dkv_job(0, 0, False, 1), dkv_job(1, 0, False, 1), e_job(1, 0, 1, 1), fetch_job(1), dkv_job(0, 0, True, 1, 1), fetch_job(0)]
-        jobs += [dw_job(0, 0), dkv_job(1, 0, True, 1, 1), dw_job(1, 0), x_job(1, 1), dkv_job(2, 0, True, 0, 1), dw_job(2, 0), dkv_job(3, 0, True, 2), dw_job(3, 0), dw_job(4, 0, 1), dw_job(5, 0, 1)]
+        jobs += [dkv_job(0, 0, False, 1), dkv_job(1, 0, False, 1), e_job(1, 0, 1, 1), fetch_job(0), dkv_job(0, 0, True, 1, 1)]
+        jobs += [dw_job(0, 0), dkv_job(1, 0, True, 1, 1), dw_job(1, 0), x_job(1, 1), fetch_job(1), dkv_job(2, 0, True, 0, 1), dw_job(2, 0), dkv_job(3, 0, True, 2), dw_job(3, 0), dw_job(4, 0, 1), dw_job(5, 0, 1)]
         for t in range(4):
             jobs += [dx_job(0, t, 0), dx_job(0, t, 1), dkv_job(2 + t // 2, t % 2, False, 1, 1), first_job(1, t)]
-        jobs += [dw_job(6, 0, 1), dw_job(7, 0, 1), dw_job(0, 1, 1), third_job()]
+        jobs += [dw_job(6, 0, 1), dw_job(7, 0, 1), third_job(), dw_job(0, 1, 1)]
         for n in range(1, 8):
-            jobs += [dw_job(n, 1, n < 4)]
+            jobs += [dw_job(n, 1, n < 3)]
         depth = max(len(j) for j in jobs)
         for i in range(len(jobs) + depth):
             for s in range(depth - 1, -1, -1):

@@ -149,20 +149,20 @@ def tile_efficientmultiscaledilatedattention_pa_v_kernel(tc, x, W_kv, b_kv, E_k,
                     for t in range(2):
                         for u in range(2):
                             nc.tensor.transpose(v[:, t, u, :], words_of(2 * half + t, u), ident[:])
-                    box["ps"].append(v.rearrange("p t u c -> p t c u"))
+                    box["ps"].append(v.rearrange("p t u (c r) -> p t c u r", r=2))
 
             def s1():
                 box["st"] = stage("flipped")
-                dst = box["st"][:].bitcast(F32).rearrange("p (t c u) -> p t c u", t=4, u=2)
+                dst = box["st"][:].bitcast(F32).rearrange("p (t c r u) -> p t c u r", t=4, r=2, u=2)
                 for half in range(2):
                     pair = slice(2 * half, 2 * half + 2)
                     if turn:
-                        move(half < vec, dst[:, pair, 0:turn], box["ps"][half][:, :, 128 - turn:128])
-                    move(half < vec, dst[:, pair, turn:128], box["ps"][half][:, :, 0:128 - turn])
+                        move(half < vec, dst[:, pair, 0:turn], box["ps"][half][:, :, 64 - turn:64])
+                    move(half < vec, dst[:, pair, turn:64], box["ps"][half][:, :, 0:64 - turn])
             return [s0, s1] + [nothing] * lag + [lambda: quantise(op, col, E4X4, box["st"])]
 
         def e_job(e, grp, vec=0, lag=0):
-            return flip_job(lambda t, u: raw_e[(e, grp)][:].bitcast(F32)[:, t, u:256:2], ec[e], 512 * grp, vec, lag, LISTS * grp)
+            return flip_job(lambda t, u: raw_e[(e, grp)][:].bitcast(F32)[:, t, u:256:2], ec[e], 512 * grp, vec, lag, LISTS // 2 * grp)
 
         def w_job(fb, h, vec=0, lag=0):
             return flip_job(lambda t, u: raw_w[2 * h + t // 2][:].bitcast(F32)[:, t % 2, 256 * fb + u:256 * fb + 256:2], wc[fb], 512 * h, vec, lag)
@@ -195,8 +195,8 @@ def tile_efficientmultiscaledilatedattention_pa_v_kernel(tc, x, W_kv, b_kv, E_k,
             def s1():
                 box["st"] = stage("dkv_bf16")
                 for i in range(4):
-                    move(i >= 4 - vec, box["st"][:, 512 * i:512 * i + 512].rearrange("p (n k) -> p n k", k=4),
-                         box["ps"][i][:].rearrange("p (k n) -> p n k", k=4))
+                    move(i >= 4 - vec, box["st"][:, 512 * i:512 * i + 512].rearrange("p (n r k) -> p n k r", k=4, r=4),
+                         box["ps"][i][:].rearrange("p (k n r) -> p n k r", k=4, r=4))
             return [s0, s1] + [nothing] * lag + [lambda: quantise((fc if by_feature else lc)[fb], 512 * grp, E5X4, box["st"])]
 
         def x_job(grp, h):
@@ -210,7 +210,8 @@ def tile_efficientmultiscaledilatedattention_pa_v_kernel(tc, x, W_kv, b_kv, E_k,
 
             def s1():
                 box["st"] = stage("x_sorted")
-                nc.vector.tensor_copy(out=box["st"][:].rearrange("p (c t) -> p c t", t=4), in_=box["sum"][:].rearrange("p (t c) -> p c t", t=4))
+                nc.vector.tensor_copy(out=box["st"][:].rearrange("p (c r t) -> p c t r", t=4, r=4),
+                                      in_=box["sum"][:].rearrange("p (t c r) -> p c t r", t=4, r=4))
             return [s0, s1, lambda: quantise(xc[grp], 512 * h, E4X4, box["st"])]
 
         def tokens(grp, j):
@@ -307,8 +308,8 @@ def tile_efficientmultiscaledilatedattention_pa_v_kernel(tc, x, W_kv, b_kv, E_k,
             def s1():
                 box["o"] = row("dw_out", [128, 1024], F32)
                 for i in range(2):
-                    halve(i < vec, box["o"][:, 512 * i:512 * i + 512].rearrange("p (m j) -> p m j", j=4),
-                          box["ps"][i][:].rearrange("p (j m) -> p m j", j=4))
+                    halve(i < vec, box["o"][:, 512 * i:512 * i + 512].rearrange("p (m r j) -> p m j r", j=4, r=2),
+                          box["ps"][i][:].rearrange("p (j m r) -> p m j r", j=4, r=2))
 
             def s2():
                 nc.sync.dma_start(out=out_1[128 * n:128 * n + 128, 1024 * pair:1024 * pair + 1024], in_=box["o"][:])
@@ -320,11 +321,11 @@ def tile_efficientmultiscaledilatedattention_pa_v_kernel(tc, x, W_kv, b_kv, E_k,
         jobs += [w_job(1, 0, 1, 1), dkv_job(0, 1, False, 2, 2), w_job(2, 0, 1), w_job(3, 0, 1), dkv_job(1, 1, False, 2, 1), w_job(0, 1, 1, 1), call_job(load_x, 2), call_job(load_e, 1, 0)]
         jobs += [dx_job(1, 0, 0), w_job(1, 1, 0, 1), dx_job(1, 1, 0), x_job(0, 0), w_job(2, 1), dx_job(1, 2, 0), w_job(3, 1), dx_job(1, 3, 0), x_job(0, 1), e_job(0, 0)]
         jobs += [dx_job(1, 0, 1), dx_job(1, 1, 1), x_job(1, 0), dx_job(1, 2, 1), dx_job(1, 3, 1)]
-        jobs += [dkv_job(0, 0, False, 1), dkv_job(1, 0, False, 1), e_job(1, 0, 1, 1), fetch_job(0), dkv_job(0, 0, True, 1, 1)]
-        jobs += [dw_job(0, 0), dkv_job(1, 0, True, 1, 1), dw_job(1, 0), x_job(1, 1), fetch_job(1), dkv_job(2, 0, True, 0, 1), dw_job(2, 0), dkv_job(3, 0, True, 2), dw_job(3, 0), dw_job(4, 0, 1), dw_job(5, 0, 1)]
+        jobs += [dkv_job(0, 0, False, 1), dkv_job(1, 0, False, 1), e_job(1, 0, 0, 1), fetch_job(0), dkv_job(0, 0, True, 1, 1)]
+        jobs += [dw_job(0, 0), dkv_job(1, 0, True, 1, 1), dw_job(1, 0), x_job(1, 1), fetch_job(1), dkv_job(2, 0, True, 0, 1), dw_job(2, 0), dkv_job(3, 0, True, 1), dw_job(3, 0), dw_job(4, 0), dw_job(5, 0)]
         for t in range(4):
             jobs += [dx_job(0, t, 0), dx_job(0, t, 1), dkv_job(2 + t // 2, t % 2, False, 1, 1), first_job(1, t)]
-        jobs += [dw_job(6, 0, 1), dw_job(7, 0, 1), third_job(), dw_job(0, 1, 1)]
+        jobs += [dw_job(6, 0), dw_job(7, 0), third_job(), dw_job(0, 1, 1)]
         for n in range(1, 8):
             jobs += [dw_job(n, 1, n < 3)]
         depth = max(len(j) for j in jobs)

@@ -17,7 +17,8 @@ MULT = mybir.AluOpType.mult
 FLOPS = 2 * 1024 * 512 * 2048 + 2 * 1024 * 2048 * 1024 + 2 * 1024 * 1024 * 2048
 BYTES = 2 * (1600 * 1024 + 1024 * 2048 + 2 * 1024 * 512 + 2 * 512 * 1024) + 4 * (1600 * 1024 + 1024 * 2048)
 
-LISTS = 56
+SORTED = ((0, 1), (1, 1), (2, 1), (3, 1))
+FIRST = 72
 SECOND = 50
 
 
@@ -78,7 +79,8 @@ def tile_efficientmultiscaledilatedattention_pa_v_kernel(tc, x, W_kv, b_kv, E_k,
 
         def load_e(e, grp):
             raw_e[(e, grp)] = row("raw_e", [128, 4, 512], BF16)
-            nc.sync.dma_start(out=raw_e[(e, grp)][:], in_=e_src[e][512 * grp:512 * grp + 512, :].rearrange("(p t) k -> p t k", t=4))
+            for queue, p0, p1, n0 in (((nc.sync, 0, 128, 288),), ((nc.sync, 0, FIRST, 0), (nc.scalar, FIRST, 128, 800)))[grp]:
+                queue.dma_start(out=raw_e[(e, grp)][p0:p1], in_=e_src[e][n0:n0 + 4 * (p1 - p0), :].rearrange("(p t) k -> p t k", t=4))
 
         def load_g(fb):
             e, b = divmod(fb, 2)
@@ -102,29 +104,30 @@ def tile_efficientmultiscaledilatedattention_pa_v_kernel(tc, x, W_kv, b_kv, E_k,
             entry, m = runs[i]
             r, c = divmod(entry, 14)
             p, s = divmod(entry, 8)
-            nc.sync.dma_start(out=raw_x[1][SECOND + p:SECOND + p + 1, s:s + m, :], in_=third[r:r + 1, 3 * c:3 * (c + m):3, :])
+            nc.sync.dma_start(out=raw_x[1][FIRST + SECOND + p:FIRST + SECOND + p + 1, s:s + m, :], in_=third[r:r + 1, 3 * c:3 * (c + m):3, :])
 
         def load_x(part):
             if part == 0:
-                nc.sync.dma_start(out=raw_x[0][:], in_=xf[0:1024, :].rearrange("(p j) c -> p j c", j=8))
+                nc.sync.dma_start(out=raw_x[0][:], in_=xf[576:1600, :].rearrange("(p j) c -> p j c", j=8))
             elif part == 1:
-                nc.sync.dma_start(out=raw_x[1][LISTS:128], in_=xf[1024:1600, :].rearrange("(p j) c -> p j c", j=8))
+                nc.sync.dma_start(out=raw_x[1][0:FIRST], in_=xf[0:576, :].rearrange("(p j) c -> p j c", j=8))
             else:
-                nc.scalar.dma_start(out=raw_x[1][0:SECOND], in_=even[:, 0:40:2, :])
+                nc.sync.dma_start(out=raw_x[1][FIRST:FIRST + SECOND], in_=even[:, 0:40:2, :])
 
-        load_g(0)
         load_e(0, 1)
-        load_g(1)
+        load_g(0)
         load_e(1, 1)
+        load_g(1)
         load_g(2)
         load_g(3)
         for i in range(4):
             load_w(i)
-            load_third(2 * i)
-            load_third(2 * i + 1)
         load_x(0)
-        load_third(8)
         load_e(0, 0)
+        load_e(1, 0)
+        for i in range(len(runs)):
+            load_third(i)
+        load_x(2)
         load_x(1)
         extra = [pool.tile([128, 2, 1024], F32, name="extra%d" % grp, align_bytes=64) for grp in range(2)]
 
@@ -138,7 +141,7 @@ def tile_efficientmultiscaledilatedattention_pa_v_kernel(tc, x, W_kv, b_kv, E_k,
         def nothing():
             return None
 
-        def flip_job(words_of, op, col, vec, lag, turn=0):
+        def flip_job(words_of, op, col, vec, lag):
             box = {}
 
             def s0():
@@ -155,16 +158,26 @@ def tile_efficientmultiscaledilatedattention_pa_v_kernel(tc, x, W_kv, b_kv, E_k,
                 box["st"] = stage("flipped")
                 dst = box["st"][:].bitcast(F32).rearrange("p (t c r u) -> p t c u r", t=4, r=2, u=2)
                 for half in range(2):
-                    pair = slice(2 * half, 2 * half + 2)
-                    if turn:
-                        move(half < vec, dst[:, pair, 0:turn], box["ps"][half][:, :, 64 - turn:64])
-                    move(half < vec, dst[:, pair, turn:64], box["ps"][half][:, :, 0:64 - turn])
+                    move(half < vec, dst[:, 2 * half:2 * half + 2], box["ps"][half])
             return [s0, s1] + [nothing] * lag + [lambda: quantise(op, col, E4X4, box["st"])]
 
         def e_job(e, grp, vec=0, lag=0):
-            return flip_job(lambda t, u: raw_e[(e, grp)][:].bitcast(F32)[:, t, u:256:2], ec[e], 512 * grp, vec, lag, LISTS // 2 * grp)
+            return flip_job(lambda t, u: raw_e[(e, grp)][:].bitcast(F32)[:, t, u:256:2], ec[e], 512 * grp, vec, lag)
+
+        sorted_w = {}
+
+        def sort_job(fb, h):
+            def s0():
+                sorted_w[(fb, h)] = stage("w_sorted")
+                dst = sorted_w[(fb, h)][:].bitcast(F32).rearrange("p (i n u w) -> p i n u w", i=2, n=2, u=2)
+                for i in range(2):
+                    src = raw_w[2 * h + i][:].bitcast(F32)[:, :, 256 * fb:256 * fb + 256]
+                    nc.vector.tensor_copy(out=dst[:, i].rearrange("p n u w -> p n w u"), in_=src.rearrange("p n (w u) -> p n w u", u=2))
+            return [s0]
 
         def w_job(fb, h, vec=0, lag=0):
+            if (fb, h) in SORTED:
+                return flip_job(lambda t, u: sorted_w[(fb, h)][:].bitcast(F32)[:, 256 * t + 128 * u:256 * t + 128 * u + 128], wc[fb], 512 * h, vec, lag)
             return flip_job(lambda t, u: raw_w[2 * h + t // 2][:].bitcast(F32)[:, t % 2, 256 * fb + u:256 * fb + 256:2], wc[fb], 512 * h, vec, lag)
 
         def g_job(fb):
@@ -215,7 +228,7 @@ def tile_efficientmultiscaledilatedattention_pa_v_kernel(tc, x, W_kv, b_kv, E_k,
             return [s0, s1, lambda: quantise(xc[grp], 512 * h, E4X4, box["st"])]
 
         def tokens(grp, j):
-            return of[576 * grp:576 * grp + 1024, :].rearrange("(p j) c -> p j c", j=8)[:, j, :]
+            return of[576 * (1 - grp):576 * (1 - grp) + 1024, :].rearrange("(p j) c -> p j c", j=8)[:, j, :]
 
         ys = {}
 
@@ -244,11 +257,8 @@ def tile_efficientmultiscaledilatedattention_pa_v_kernel(tc, x, W_kv, b_kv, E_k,
                 if h == 1 and grp == 1:
                     nc.sync.dma_start(out=tokens(grp, 2 * t + 1), in_=ys[(grp, t, 1)][:])
                 elif h == 1:
-                    nc.sync.dma_start(out=of[0:1024, :].rearrange("(p j) c -> p j c", j=8)[:, 2 * t:2 * t + 2, :], in_=ys[t][:])
+                    nc.sync.dma_start(out=of[576:1600, :].rearrange("(p j) c -> p j c", j=8)[:, 2 * t:2 * t + 2, :], in_=ys[t][:])
             return [s0, s1, s2]
-
-        def call_job(f, *args):
-            return [lambda: f(*args)]
 
         def zero_job(grp):
             return [lambda: nc.vector.memset(extra[grp][:].bitcast(I32), 0)]
@@ -256,13 +266,14 @@ def tile_efficientmultiscaledilatedattention_pa_v_kernel(tc, x, W_kv, b_kv, E_k,
         def fetch_job(grp):
             def s0():
                 pr = parked[0:200, :].rearrange("(r s) c -> r s c", s=10)
-                r0, r1, p0 = ((0, 13, 0), (13, 20, LISTS + 2))[grp]
                 for a in range(5):
-                    nc.sync.dma_start(out=extra[grp][p0 + a:p0 + a + 10 * (r1 - r0) - 9:10], in_=pr[r0:r1, 2 * a:2 * a + 2, :])
+                    split = (FIRST - a + 9) // 10
+                    r0, r1, p0 = ((split, 20, 10 * split + a - FIRST), (0, split, a))[grp]
+                    (nc.sync if grp else nc.gpsimd).dma_start(out=extra[grp][p0:p0 + 10 * (r1 - r0) - 9:10], in_=pr[r0:r1, 2 * a:2 * a + 2, :])
                 if grp == 0:
                     ys["third"] = row("third_add", [128, 1024], F32)
                     for d in range(2):
-                        nc.sync.dma_start(out=ys["third"][d:48:2, :], in_=parked[200:224, :])
+                        nc.gpsimd.dma_start(out=ys["third"][d:48:2, :], in_=parked[200:224, :])
             return [s0]
 
         def first_job(grp, t):
@@ -271,7 +282,7 @@ def tile_efficientmultiscaledilatedattention_pa_v_kernel(tc, x, W_kv, b_kv, E_k,
                 nc.vector.tensor_tensor(out=ys[(grp, t, 0)][:], in0=ys[(grp, t, 1)][:], in1=extra[grp][:, t // 2, :], op=ADD)
 
             def s1():
-                nc.sync.dma_start(out=tokens(grp, 2 * t)[LISTS * grp:128], in_=ys[(grp, t, 0)][LISTS * grp:128, :])
+                nc.sync.dma_start(out=tokens(grp, 2 * t)[0:FIRST], in_=ys[(grp, t, 0)][0:FIRST, :])
             return [s0, s1]
 
         def third_job():
@@ -281,16 +292,16 @@ def tile_efficientmultiscaledilatedattention_pa_v_kernel(tc, x, W_kv, b_kv, E_k,
             def s0():
                 box["a"] = ys["third"]
                 box["b"] = row("third_old", [128, 1024], F32)
-                nc.sync.dma_start(out=box["b"][0:42, :], in_=rows[0:3, 0:42:3, :])
-                nc.sync.dma_start(out=box["b"][42:48, :], in_=rows[3, 0:18:3, :])
+                nc.gpsimd.dma_start(out=box["b"][0:42, :], in_=rows[0:3, 0:42:3, :])
+                nc.gpsimd.dma_start(out=box["b"][42:48, :], in_=rows[3, 0:18:3, :])
 
             def s1():
                 nc.vector.tensor_tensor(out=box["a"][0:48, :], in0=box["a"][0:48, :], in1=box["b"][0:48, :], op=ADD)
 
             def s2():
-                nc.sync.dma_start(out=rows[0:3, 0:42:3, :], in_=box["a"][0:42, :])
-                nc.sync.dma_start(out=rows[3, 0:18:3, :], in_=box["a"][42:48, :])
-            return [s0, nothing, nothing, nothing, nothing, s1, s2]
+                nc.gpsimd.dma_start(out=rows[0:3, 0:42:3, :], in_=box["a"][0:42, :])
+                nc.gpsimd.dma_start(out=rows[3, 0:18:3, :], in_=box["a"][42:48, :])
+            return [s0], [s1, s2]
 
         obs = {}
 
@@ -316,18 +327,25 @@ def tile_efficientmultiscaledilatedattention_pa_v_kernel(tc, x, W_kv, b_kv, E_k,
             return [s0, s1, s2]
 
         gap = [nothing]
-        jobs = [zero_job(0), zero_job(1), g_job(0), e_job(0, 1), gap, e_job(1, 1, 0, 1), g_job(1), dkv_job(0, 1, True, 0, 2), g_job(2), dkv_job(1, 1, True, 0, 2), g_job(3),
-                dkv_job(2, 1, True, 1, 1), w_job(0, 0, 1, 1), dkv_job(3, 1, True, 2, 1)]
-        jobs += [w_job(1, 0, 1, 1), dkv_job(0, 1, False, 2, 2), w_job(2, 0, 1), w_job(3, 0, 1), dkv_job(1, 1, False, 2, 1), w_job(0, 1, 1, 1), call_job(load_x, 2), call_job(load_e, 1, 0)]
-        jobs += [dx_job(1, 0, 0), w_job(1, 1, 0, 1), dx_job(1, 1, 0), x_job(0, 0), w_job(2, 1), dx_job(1, 2, 0), w_job(3, 1), dx_job(1, 3, 0), x_job(0, 1), e_job(0, 0)]
-        jobs += [dx_job(1, 0, 1), dx_job(1, 1, 1), x_job(1, 0), dx_job(1, 2, 1), dx_job(1, 3, 1)]
-        jobs += [dkv_job(0, 0, False, 1), dkv_job(1, 0, False, 1), e_job(1, 0, 0, 1), fetch_job(0), dkv_job(0, 0, True, 1, 1)]
-        jobs += [dw_job(0, 0), dkv_job(1, 0, True, 1, 1), dw_job(1, 0), x_job(1, 1), fetch_job(1), dkv_job(2, 0, True, 0, 1), dw_job(2, 0), dkv_job(3, 0, True, 1), dw_job(3, 0), dw_job(4, 0), dw_job(5, 0)]
-        for t in range(4):
-            jobs += [dx_job(0, t, 0), dx_job(0, t, 1), dkv_job(2 + t // 2, t % 2, False, 1, 1), first_job(1, t)]
-        jobs += [dw_job(6, 0), dw_job(7, 0), third_job(), dw_job(0, 1, 1)]
-        for n in range(1, 8):
-            jobs += [dw_job(n, 1, n < 3)]
+        K = dkv_job
+        ek, ev = e_job(0, 1), e_job(1, 1)
+        g = [g_job(fb) for fb in range(4)]
+        f = [K(fb, 1, True, 2 * (fb == 3)) for fb in range(4)]
+        head = [zero_job(0)[0], zero_job(1)[0], ek[0], ek[1], ev[0], ev[1],
+                g[0][0], ek[2], g[0][1], f[0][0], f[0][1],
+                g[1][0], ev[2], g[1][1], f[1][0], f[1][1],
+                g[2][0], g[2][1], f[2][0], f[2][1],
+                g[3][0], f[0][2], g[3][1], f[3][0], f[1][2], f[3][1], f[2][2]]
+        for step in head:
+            step()
+        third_read, third_write = third_job()
+        jobs = [w_job(0, 0, 1), [f[3][2]], w_job(1, 0, 1), K(0, 1, False, 2, 3), w_job(2, 0, 1), sort_job(0, 1), w_job(3, 0), sort_job(1, 1), w_job(0, 1, 0, 1), sort_job(2, 1)]
+        jobs += [dx_job(1, 0, 0), sort_job(3, 1), w_job(1, 1), dx_job(1, 1, 0), x_job(0, 0), w_job(2, 1), w_job(3, 1), dx_job(1, 2, 0), e_job(0, 0), K(1, 1, False, 0), x_job(0, 1), dx_job(1, 3, 0), e_job(1, 0)]
+        jobs += [dx_job(1, 0, 1), K(0, 0, False, 1), dx_job(1, 1, 1), K(1, 0, False, 0), x_job(1, 0), dx_job(1, 2, 1), dx_job(1, 3, 1), K(0, 0, True, 1, 1), K(1, 0, True, 1, 1), fetch_job(1), fetch_job(0), x_job(1, 1)]
+        jobs += [dw_job(0, 0), K(2, 0, True, 0, 1), dw_job(1, 0), dw_job(2, 0), first_job(1, 0), K(3, 0, True, 1, 1), dw_job(3, 0), first_job(1, 1), dw_job(4, 0), first_job(1, 2), K(2, 1, False, 1, 1), dw_job(5, 0), first_job(1, 3)]
+        jobs += [dx_job(0, 0, 0), dx_job(0, 0, 1), third_read, K(3, 1, False, 2, 1), dx_job(0, 1, 0), dx_job(0, 1, 1), K(2, 0, False, 2, 1), dx_job(0, 2, 0), dx_job(0, 2, 1), K(3, 0, False, 2), dx_job(0, 3, 0), dx_job(0, 3, 1), dw_job(6, 0), third_write, dw_job(7, 0)]
+        for n in range(8):
+            jobs += [dw_job(n, 1, 1)]
         depth = max(len(j) for j in jobs)
         for i in range(len(jobs) + depth):
             for s in range(depth - 1, -1, -1):

@@ -17,7 +17,6 @@ MULT = mybir.AluOpType.mult
 FLOPS = 2 * 1024 * 512 * 2048 + 2 * 1024 * 2048 * 1024 + 2 * 1024 * 1024 * 2048
 BYTES = 2 * (1600 * 1024 + 1024 * 2048 + 2 * 1024 * 512 + 2 * 512 * 1024) + 4 * (1600 * 1024 + 1024 * 2048)
 
-SORTED = ((0, 1), (1, 1), (2, 1), (3, 1))
 FIRST = 72
 SECOND = 50
 
@@ -33,10 +32,7 @@ def tile_efficientmultiscaledilatedattention_pa_v_kernel(tc, x, W_kv, b_kv, E_k,
         make_identity(nc, ident[:])
 
         def row(name, shape, dt):
-            return pool.tile(shape, dt, name=name, tag="row", bufs=11, align_bytes=64)
-
-        def wide(name, shape, dt):
-            return pool.tile(shape, dt, name=name, tag="wide", bufs=4, align_bytes=64)
+            return pool.tile(shape, dt, name=name, tag="row", bufs=16, align_bytes=64)
 
         def stage(name):
             return pool.tile([128, 2048], BF16, name=name, tag="stage", bufs=5, align_bytes=64)
@@ -88,8 +84,8 @@ def tile_efficientmultiscaledilatedattention_pa_v_kernel(tc, x, W_kv, b_kv, E_k,
             nc.sync.dma_start(out=raw_g[fb][:], in_=g_src[e][4 * b:4 * b + 4].rearrange("h (p j) d -> p h (j d)", j=4))
 
         def load_w(i):
-            raw_w[i] = wide("raw_w", [128, 2, 2048], BF16)
-            nc.sync.dma_start(out=raw_w[i][:], in_=W_kv[256 * i:256 * i + 256, :].rearrange("(n p) f -> p n f", p=128))
+            raw_w[i] = row("raw_w", [128, 2048], BF16)
+            nc.sync.dma_start(out=raw_w[i][:], in_=W_kv[128 * i:128 * i + 128, :])
 
         raw_x = [pool.tile([128, 8, 1024], BF16, name="raw_x%d" % grp, align_bytes=64) for grp in range(2)]
         even = xf.rearrange("(r n) c -> r n c", n=80)
@@ -120,7 +116,7 @@ def tile_efficientmultiscaledilatedattention_pa_v_kernel(tc, x, W_kv, b_kv, E_k,
         load_g(1)
         load_g(2)
         load_g(3)
-        for i in range(4):
+        for i in range(8):
             load_w(i)
         load_x(0)
         load_e(0, 0)
@@ -164,21 +160,8 @@ def tile_efficientmultiscaledilatedattention_pa_v_kernel(tc, x, W_kv, b_kv, E_k,
         def e_job(e, grp, vec=0, lag=0):
             return flip_job(lambda t, u: raw_e[(e, grp)][:].bitcast(F32)[:, t, u:256:2], ec[e], 512 * grp, vec, lag)
 
-        sorted_w = {}
-
-        def sort_job(fb, h):
-            def s0():
-                sorted_w[(fb, h)] = stage("w_sorted")
-                dst = sorted_w[(fb, h)][:].bitcast(F32).rearrange("p (i n u w) -> p i n u w", i=2, n=2, u=2)
-                for i in range(2):
-                    src = raw_w[2 * h + i][:].bitcast(F32)[:, :, 256 * fb:256 * fb + 256]
-                    nc.vector.tensor_copy(out=dst[:, i].rearrange("p n u w -> p n w u"), in_=src.rearrange("p n (w u) -> p n w u", u=2))
-            return [s0]
-
         def w_job(fb, h, vec=0, lag=0):
-            if (fb, h) in SORTED:
-                return flip_job(lambda t, u: sorted_w[(fb, h)][:].bitcast(F32)[:, 256 * t + 128 * u:256 * t + 128 * u + 128], wc[fb], 512 * h, vec, lag)
-            return flip_job(lambda t, u: raw_w[2 * h + t // 2][:].bitcast(F32)[:, t % 2, 256 * fb + u:256 * fb + 256:2], wc[fb], 512 * h, vec, lag)
+            return flip_job(lambda t, u: raw_w[4 * h + t][:].bitcast(F32)[:, 256 * fb + u:256 * fb + 256:2], wc[fb], 512 * h, vec, lag)
 
         def g_job(fb):
             e, b = divmod(fb, 2)
@@ -242,22 +225,13 @@ def tile_efficientmultiscaledilatedattention_pa_v_kernel(tc, x, W_kv, b_kv, E_k,
 
             def s1():
                 cols = slice(512 * h, 512 * h + 512)
-                if grp == 1:
-                    if h == 0:
-                        ys[(grp, t, 1)] = row("y_second", [128, 1024], F32)
-                    halve(vec, ys[(grp, t, 1)][:, cols], box["ps"][:])
-                else:
-                    if h == 0:
-                        ys[t] = wide("y_both", [128, 2, 1024], F32)
-                    halve(vec, ys[t][:, 1, cols], box["ps"][:])
-                    nc.vector.scalar_tensor_tensor(out=ys[t][:, 0, cols], in0=box["ps"][:], scalar=0.5,
-                                                   in1=extra[0][:, t // 2, cols], op0=MULT, op1=ADD)
+                if h == 0:
+                    ys[(grp, t, 1)] = row("y_second", [128, 1024], F32)
+                halve(vec, ys[(grp, t, 1)][:, cols], box["ps"][:])
 
             def s2():
-                if h == 1 and grp == 1:
+                if h == 1:
                     nc.sync.dma_start(out=tokens(grp, 2 * t + 1), in_=ys[(grp, t, 1)][:])
-                elif h == 1:
-                    nc.sync.dma_start(out=of[576:1600, :].rearrange("(p j) c -> p j c", j=8)[:, 2 * t:2 * t + 2, :], in_=ys[t][:])
             return [s0, s1, s2]
 
         def zero_job(grp):
@@ -277,12 +251,14 @@ def tile_efficientmultiscaledilatedattention_pa_v_kernel(tc, x, W_kv, b_kv, E_k,
             return [s0]
 
         def first_job(grp, t):
+            live = FIRST if grp else 128
+
             def s0():
                 ys[(grp, t, 0)] = row("y_first", [128, 1024], F32)
                 nc.vector.tensor_tensor(out=ys[(grp, t, 0)][:], in0=ys[(grp, t, 1)][:], in1=extra[grp][:, t // 2, :], op=ADD)
 
             def s1():
-                nc.sync.dma_start(out=tokens(grp, 2 * t)[0:FIRST], in_=ys[(grp, t, 0)][0:FIRST, :])
+                nc.sync.dma_start(out=tokens(grp, 2 * t)[0:live], in_=ys[(grp, t, 0)][0:live, :])
             return [s0, s1]
 
         def third_job():
@@ -339,13 +315,20 @@ def tile_efficientmultiscaledilatedattention_pa_v_kernel(tc, x, W_kv, b_kv, E_k,
         for step in head:
             step()
         third_read, third_write = third_job()
-        jobs = [w_job(0, 0, 1), [f[3][2]], w_job(1, 0, 1), K(0, 1, False, 2, 3), w_job(2, 0, 1), sort_job(0, 1), w_job(3, 0), sort_job(1, 1), w_job(0, 1, 0, 1), sort_job(2, 1)]
-        jobs += [dx_job(1, 0, 0), sort_job(3, 1), w_job(1, 1), dx_job(1, 1, 0), x_job(0, 0), w_job(2, 1), w_job(3, 1), dx_job(1, 2, 0), e_job(0, 0), K(1, 1, False, 0), x_job(0, 1), dx_job(1, 3, 0), e_job(1, 0)]
-        jobs += [dx_job(1, 0, 1), K(0, 0, False, 1), dx_job(1, 1, 1), K(1, 0, False, 0), x_job(1, 0), dx_job(1, 2, 1), dx_job(1, 3, 1), K(0, 0, True, 1, 1), K(1, 0, True, 1, 1), fetch_job(1), fetch_job(0), x_job(1, 1)]
-        jobs += [dw_job(0, 0), K(2, 0, True, 0, 1), dw_job(1, 0), dw_job(2, 0), first_job(1, 0), K(3, 0, True, 1, 1), dw_job(3, 0), first_job(1, 1), dw_job(4, 0), first_job(1, 2), K(2, 1, False, 1, 1), dw_job(5, 0), first_job(1, 3)]
-        jobs += [dx_job(0, 0, 0), dx_job(0, 0, 1), third_read, K(3, 1, False, 2, 1), dx_job(0, 1, 0), dx_job(0, 1, 1), K(2, 0, False, 2, 1), dx_job(0, 2, 0), dx_job(0, 2, 1), K(3, 0, False, 2), dx_job(0, 3, 0), dx_job(0, 3, 1), dw_job(6, 0), third_write, dw_job(7, 0)]
+        flips = [w_job(fb, 0, 1) for fb in range(4)] + [w_job(0, 1), e_job(0, 0), w_job(1, 1), w_job(2, 1), w_job(3, 1), e_job(1, 0)]
+        between = [K(fb, 1, False, 1, 1) for fb in range(4)] + [dx_job(1, 0, 0), dx_job(1, 1, 0), K(0, 0, False, 0, 1), dx_job(1, 2, 0), K(1, 0, False, 1, 1), dx_job(1, 3, 0)]
+        jobs = [[f[3][2]]]
+        for i in range(10):
+            jobs += [flips[i], between[i]] + [x_job(0, (i - 5) // 2)] * (i in (5, 7))
+        jobs += [dx_job(1, 0, 1), x_job(1, 0), dx_job(1, 1, 1), dx_job(1, 2, 1), dx_job(1, 3, 1), x_job(1, 1)]
+        for i in range(4):
+            jobs += [K(i, 0, True, 2 * (i > 0), 1), dw_job(2 * i, 0), dw_job(2 * i + 1, 0)] + [fetch_job(1), fetch_job(0)] * (i == 0)
+            jobs += [first_job(1, t) for t in range(4) if t // 2 + 2 == i]
+        for t in range(4):
+            jobs += [K(2 + t, 0, False, 1, 1)] if t < 2 else []
+            jobs += [dx_job(0, t, 0), dx_job(0, t, 1)] + [third_read if t == 1 else gap, first_job(0, t)]
         for n in range(8):
-            jobs += [dw_job(n, 1, 1)]
+            jobs += [dw_job(n, 1, 1)] + [third_write] * (n == 2)
         depth = max(len(j) for j in jobs)
         for i in range(len(jobs) + depth):
             for s in range(depth - 1, -1, -1):

@@ -10,15 +10,16 @@ I32 = mybir.dt.int32
 U8 = mybir.dt.uint8
 E4X4 = mybir.dt.float8_e4m3fn_x4
 E5X4 = mybir.dt.float8_e5m2_x4
-COPY = mybir.ActivationFunctionType.Copy
 ADD = mybir.AluOpType.add
 MULT = mybir.AluOpType.mult
 
 FLOPS = 2 * 1024 * 512 * 2048 + 2 * 1024 * 2048 * 1024 + 2 * 1024 * 1024 * 2048
 BYTES = 2 * (1600 * 1024 + 1024 * 2048 + 2 * 1024 * 512 + 2 * 512 * 1024) + 4 * (1600 * 1024 + 1024 * 2048)
 
-FIRST = 72
-SECOND = 50
+ROWS = 15
+STAGES = 9
+MOVED = 576
+A, B = 0, 1
 
 
 def tile_efficientmultiscaledilatedattention_pa_v_kernel(tc, x, W_kv, b_kv, E_k, E_v, kv, grad_0, grad_1, out_0, out_1):
@@ -32,26 +33,23 @@ def tile_efficientmultiscaledilatedattention_pa_v_kernel(tc, x, W_kv, b_kv, E_k,
         make_identity(nc, ident[:])
 
         def row(name, shape, dt):
-            return pool.tile(shape, dt, name=name, tag="row", bufs=16, align_bytes=64)
+            return pool.tile(shape, dt, name=name, tag="row", bufs=ROWS, align_bytes=64)
 
         def stage(name):
-            return pool.tile([128, 2048], BF16, name=name, tag="stage", bufs=5, align_bytes=64)
+            return pool.tile([128, 2048], BF16, name=name, tag="stage", bufs=STAGES, align_bytes=64)
 
-        def operand(name):
-            codes = pool.tile([128, 1024], U32, name=name + "_codes", align_bytes=64)
-            scales = pool.tile([128, 1024], U8, name=name + "_scales", align_bytes=64)
+        def operand(name, width):
+            codes = pool.tile([128, width], U32, name=name + "_codes", align_bytes=64)
+            scales = pool.tile([128, width], U8, name=name + "_scales", align_bytes=64)
             return codes, scales
 
         def quantise(op, col, fmt, src):
             nc.vector.quantize_mx(out=op[0][:, col:col + 512].bitcast(fmt), scales=op[1][:, col:col + 512], in_=src[:])
 
-        def mx(out, lhs, lfmt, lcol, rhs, rfmt, rcol, n, start, stop):
+        def mx(out, lhs, lfmt, lcol, rhs, rfmt, rcol, start, stop):
             nc.tensor.matmul_mx(out=out, lhsT=lhs[0][:, lcol:lcol + 128].bitcast(lfmt), lhsT_scale=lhs[1][:, lcol:lcol + 128],
-                                rhs=rhs[0][:, rcol:rcol + n].bitcast(rfmt), rhs_scale=rhs[1][:, rcol:rcol + n],
+                                rhs=rhs[0][:, rcol:rcol + 512].bitcast(rfmt), rhs_scale=rhs[1][:, rcol:rcol + 512],
                                 start=start, stop=stop)
-
-        def bank(name):
-            return psum.tile([128, 512], F32, name=name, tag="bank", bufs=8)
 
         def move(on_vector, dst, src):
             if on_vector:
@@ -59,278 +57,359 @@ def tile_efficientmultiscaledilatedattention_pa_v_kernel(tc, x, W_kv, b_kv, E_k,
             else:
                 nc.scalar.copy(out=dst, in_=src)
 
-        def halve(on_vector, dst, src):
-            if on_vector:
-                nc.vector.tensor_scalar(out=dst, in0=src, scalar1=0.5, scalar2=None, op0=MULT)
-            else:
-                nc.scalar.activation(out=dst, in_=src, func=COPY, scale=0.5)
-
         xf = x[0]
         of = out_0[0]
         e_src = [E_k, E_v]
         g_src = [grad_0[0], grad_1[0]]
-        parked = of[576:1024, :].rearrange("(m e) c -> m e c", e=2)[:, 1, :]
 
-        raw_e, raw_g, raw_w = {}, {}, {}
+        steps = {}
+        held = {}
 
-        def load_e(e, grp):
-            raw_e[(e, grp)] = row("raw_e", [128, 4, 512], BF16)
-            for queue, p0, p1, n0 in (((nc.sync, 0, 128, 288),), ((nc.sync, 0, FIRST, 0), (nc.scalar, FIRST, 128, 800)))[grp]:
-                queue.dma_start(out=raw_e[(e, grp)][p0:p1], in_=e_src[e][n0:n0 + 4 * (p1 - p0), :].rearrange("(p t) k -> p t k", t=4))
-
-        def load_g(fb):
-            e, b = divmod(fb, 2)
-            raw_g[fb] = row("raw_g", [128, 4, 512], BF16)
-            nc.sync.dma_start(out=raw_g[fb][:], in_=g_src[e][4 * b:4 * b + 4].rearrange("h (p j) d -> p h (j d)", j=4))
-
-        def load_w(i):
-            raw_w[i] = row("raw_w", [128, 2048], BF16)
-            nc.sync.dma_start(out=raw_w[i][:], in_=W_kv[128 * i:128 * i + 128, :])
+        def step(name, needs, action, takes="", frees=""):
+            steps[name] = (list(needs), action, takes, frees)
 
         raw_x = [pool.tile([128, 8, 1024], BF16, name="raw_x%d" % grp, align_bytes=64) for grp in range(2)]
-        even = xf.rearrange("(r n) c -> r n c", n=80)
-        third = xf[0:480, :].rearrange("(r n) c -> r n c", n=120)
-        runs = []
-        entry = 0
-        while entry < 48:
-            runs.append((entry, min(14 - entry % 14, 8 - entry % 8, 48 - entry)))
-            entry = entry + runs[-1][1]
+        rest = pool.tile([128, 2, 1024], F32, name="rest", align_bytes=64)
+        ec = [operand("ek", 1024), operand("ev", 1024)]
+        gc = [operand("gk", 1024), operand("gv", 1024)]
+        xc = [operand("x0", 1024), operand("x1", 1024)]
+        wc = [operand("w%d" % i, 1024) for i in range(4)]
+        lc = [operand("l%d" % i, 1024) for i in range(4)]
+        fc = [operand("fa", 2048), operand("fb", 2048)]
+        zc = operand("moved", 4 * MOVED)
 
-        def load_third(i):
-            entry, m = runs[i]
-            r, c = divmod(entry, 14)
-            p, s = divmod(entry, 8)
-            nc.sync.dma_start(out=raw_x[1][FIRST + SECOND + p:FIRST + SECOND + p + 1, s:s + m, :], in_=third[r:r + 1, 3 * c:3 * (c + m):3, :])
+        def load(job, shape, src):
+            def action():
+                held[("raw", job)] = row("raw_" + job[0], shape, BF16)
+                nc.sync.dma_start(out=held[("raw", job)][:], in_=src)
+            step(("load", job), [], action, takes="r")
 
-        def load_x(part):
-            if part == 0:
-                nc.sync.dma_start(out=raw_x[0][:], in_=xf[576:1600, :].rearrange("(p j) c -> p j c", j=8))
-            elif part == 1:
-                nc.sync.dma_start(out=raw_x[1][0:FIRST], in_=xf[0:576, :].rearrange("(p j) c -> p j c", j=8))
-            else:
-                nc.sync.dma_start(out=raw_x[1][FIRST:FIRST + SECOND], in_=even[:, 0:40:2, :])
+        def quads(n0, n):
+            return xf[n0:n0 + 8 * n, :].rearrange("(p j) c -> p j c", j=8)
 
-        load_e(0, 1)
-        load_g(0)
-        load_e(1, 1)
-        load_g(1)
-        load_g(2)
-        load_g(3)
-        for i in range(8):
-            load_w(i)
-        load_x(0)
-        load_e(0, 0)
-        load_e(1, 0)
-        for i in range(len(runs)):
-            load_third(i)
-        load_x(2)
-        load_x(1)
-        extra = [pool.tile([128, 2, 1024], F32, name="extra%d" % grp, align_bytes=64) for grp in range(2)]
+        step("xa", [], lambda: nc.sync.dma_start(out=raw_x[A][:], in_=quads(0, 128)))
+        step("xb", [], lambda: [nc.sync.dma_start(out=raw_x[B][0:64], in_=quads(1024, 64)), nc.sync.dma_start(out=raw_x[B][64:72], in_=quads(1536, 8))])
+        step("x2", [], lambda: nc.scalar.dma_start(out=raw_x[B][72:122], in_=xf.rearrange("(r n) c -> r n c", n=80)[:, 0:40:2, :]))
 
-        ec = [operand("ek"), operand("ev")]
-        gc = [operand("gk"), operand("gv")]
-        xc = [operand("x0"), operand("x1")]
-        wc = [operand("w%d" % i) for i in range(4)]
-        fc = [operand("f%d" % i) for i in range(4)]
-        lc = [operand("l%d" % i) for i in range(4)]
+        def load_third():
+            third = xf[0:480, :].rearrange("(r n) c -> r n c", n=120)
+            entry = 0
+            while entry < 48:
+                m = min(14 - entry % 14, 8 - entry % 8, 48 - entry)
+                r, c = divmod(entry, 14)
+                p, s = divmod(entry, 8)
+                nc.gpsimd.dma_start(out=raw_x[B][122 + p:123 + p, s:s + m, :], in_=third[r:r + 1, 3 * c:3 * (c + m):3, :])
+                entry = entry + m
+        step("x3", [], load_third)
 
-        def nothing():
-            return None
+        def banked(job, count, needs, fill, empty, room, last_frees=""):
+            def filler(i):
+                def action():
+                    held[("bank", job, i)] = psum.tile([128, 512], F32, name=job[0], tag="bank", bufs=8)
+                    fill(held[("bank", job, i)], i)
+                return action
 
-        def flip_job(words_of, op, col, vec, lag):
-            box = {}
+            def emptier(i):
+                return lambda on_vector: empty(on_vector, held[("bank", job, i)], i)
+            for i in range(count):
+                step(("mm", job, i), needs, filler(i), takes="b", frees=last_frees if i == count - 1 else "")
+                step(("out", job, i), [("mm", job, i)] + ([("out", job, 0)] if i and room else []), emptier(i), takes=room if i == 0 else "", frees="b")
 
-            def s0():
-                box["ps"] = []
-                for half in range(2):
-                    ps = bank("flip")
-                    v = ps[:].rearrange("p (t u c) -> p t u c", t=2, u=2)
-                    for t in range(2):
-                        for u in range(2):
-                            nc.tensor.transpose(v[:, t, u, :], words_of(2 * half + t, u), ident[:])
-                    box["ps"].append(v.rearrange("p t u (c r) -> p t c u r", r=2))
+        def flip(job, needs, words_of, place, finish, last_frees):
+            def fill(ps, half):
+                v = ps[:].rearrange("p (t u c) -> p t u c", t=2, u=2)
+                for t in range(2):
+                    for u in range(2):
+                        nc.tensor.transpose(v[:, t, u, :], words_of(half, t, u), ident[:])
 
-            def s1():
-                box["st"] = stage("flipped")
-                dst = box["st"][:].bitcast(F32).rearrange("p (t c r u) -> p t c u r", t=4, r=2, u=2)
-                for half in range(2):
-                    move(half < vec, dst[:, 2 * half:2 * half + 2], box["ps"][half])
-            return [s0, s1] + [nothing] * lag + [lambda: quantise(op, col, E4X4, box["st"])]
+            def empty(on_vector, ps, half):
+                if half == 0:
+                    held[job] = stage("flipped")
+                dst = held[job][:].bitcast(F32)[:, 512 * half:512 * half + 512]
+                move(on_vector, dst.rearrange(place, t=2, u=2), ps[:].rearrange("p (t u c) -> " + place.split("-> ")[1], t=2, u=2))
+            banked(job, 2, needs, fill, empty, "s", last_frees)
+            step(("q", job), [("out", job, 0), ("out", job, 1)], finish, frees="s")
 
-        def e_job(e, grp, vec=0, lag=0):
-            return flip_job(lambda t, u: raw_e[(e, grp)][:].bitcast(F32)[:, t, u:256:2], ec[e], 512 * grp, vec, lag)
+        TILES = "p (t c u) -> p t c u"
+        PAIRS = "p (c t u) -> p c t u"
 
-        def w_job(fb, h, vec=0, lag=0):
-            return flip_job(lambda t, u: raw_w[4 * h + t][:].bitcast(F32)[:, 256 * fb + u:256 * fb + 256:2], wc[fb], 512 * h, vec, lag)
+        def e_job(e, grp):
+            job = ("e", e, grp)
+            load(job, [128, 4, 512], e_src[e][512 * grp:512 * grp + 512, :].rearrange("(p t) k -> p t k", t=4))
+            flip(job, [("load", job)], lambda half, t, u: held[("raw", job)][:].bitcast(F32)[:, 2 * half + t, u:256:2], TILES, lambda: quantise(ec[e], 512 * grp, E4X4, held[job]), "r")
+
+        def w_job(i):
+            job = ("w", i)
+
+            def finish():
+                for fb in range(4):
+                    nc.vector.quantize_mx(out=wc[fb][0][:, 128 * i:128 * i + 128].bitcast(E4X4), scales=wc[fb][1][:, 128 * i:128 * i + 128],
+                                          in_=held[job][:, 512 * fb:512 * fb + 512])
+            load(job, [128, 2048], W_kv[128 * i:128 * i + 128, :])
+            flip(job, [("load", job)], lambda half, t, u: held[("raw", job)][:].bitcast(F32)[:, 256 * (2 * half + t) + u:256 * (2 * half + t) + 256:2], TILES, finish, "r")
 
         def g_job(fb):
             e, b = divmod(fb, 2)
-            box = {}
+            job = ("g", fb)
 
-            def s1():
-                box["st"] = stage("g_sorted")
-                nc.vector.tensor_copy(out=box["st"][:].rearrange("p (j h m k) -> p h m j k", j=4, h=4, k=4),
-                                      in_=raw_g[fb][:].rearrange("p h (k m j) -> p h m j k", k=4, j=4))
-            return [s1, lambda: quantise(gc[e], 512 * b, E5X4, box["st"])]
+            def sort(on_vector):
+                held[job] = stage("g_sorted")
+                nc.vector.tensor_scalar(out=held[job][:].rearrange("p (u h n r k) -> p h n u r k", u=2, h=4, r=2, k=4),
+                                        in0=held[("raw", job)][:].rearrange("p h (k n u r) -> p h n u r k", k=4, u=2, r=2),
+                                        scalar1=0.5, scalar2=None, op0=MULT)
+            load(job, [128, 4, 512], g_src[e][4 * b:4 * b + 4].rearrange("h (p j) d -> p h (j d)", j=4))
+            step(("sort", job), [("load", job)], sort, takes="s", frees="r")
+            step(("q", job), [("sort", job)], lambda: quantise(gc[e], 512 * b, E5X4, held[job]), frees="s")
 
-        def dkv_job(fb, grp, by_feature, vec=1, lag=0):
+        def dkv_job(fb, grp):
             e, b = divmod(fb, 2)
-            box = {}
+            job, by_feature, by_landmark = ("d", fb, grp), ("f", fb, grp), ("l", fb, grp)
 
-            def s0():
-                box["ps"] = []
-                for i in range(4):
-                    ps = bank("dkv")
-                    for k in range(4):
-                        if by_feature:
-                            mx(ps[:, 128 * k:128 * k + 128], gc[e], E5X4, 512 * b + 128 * k, ec[e], E4X4, 512 * grp + 128 * i, 128, True, True)
-                        else:
-                            mx(ps[:, 128 * k:128 * k + 128], ec[e], E4X4, 512 * grp + 128 * k, gc[e], E5X4, 512 * b + 128 * i, 128, True, True)
-                    box["ps"].append(ps)
+            def empty(on_vector, ps, t):
+                if t == 0:
+                    held[job] = stage("dkv_bf16")
+                move(on_vector, held[job][:, 512 * t:512 * t + 512], ps[:])
+            banked(job, 4, [("q", ("g", fb)), ("q", ("e", e, grp))],
+                   lambda ps, t: mx(ps[:], ec[e], E4X4, 512 * grp + 128 * t, gc[e], E5X4, 512 * b, True, True), empty, "s")
+            done = [("out", job, t) for t in range(4)]
 
-            def s1():
-                box["st"] = stage("dkv_bf16")
-                for i in range(4):
-                    move(i >= 4 - vec, box["st"][:, 512 * i:512 * i + 512].rearrange("p (n r k) -> p n k r", k=4, r=4),
-                         box["ps"][i][:].rearrange("p (k n r) -> p n k r", k=4, r=4))
-            return [s0, s1] + [nothing] * lag + [lambda: quantise((fc if by_feature else lc)[fb], 512 * grp, E5X4, box["st"])]
+            def words(half, i, u):
+                t = 2 * i + half if grp == B else 2 * half + i
+                return held[job][:].bitcast(F32)[:, 256 * t + 128 * u:256 * t + 128 * u + 128]
+            flip(by_feature, done, words, PAIRS if grp == B else TILES, lambda: quantise(fc[grp], 512 * fb, E5X4, held[by_feature]), "")
+
+            def weave(on_vector):
+                held[by_landmark] = stage("dkv_woven")
+                move(on_vector, held[by_landmark][:].rearrange("p (c r t) -> p c t r", t=4, r=4), held[job][:].rearrange("p (t c r) -> p c t r", t=4, r=4))
+            step(("sort", by_landmark), done + [("mm", by_feature, 1)], weave, takes="s", frees="s")
+            step(("q", by_landmark), [("sort", by_landmark)], lambda: quantise(lc[fb], 512 * grp, E5X4, held[by_landmark]), frees="s")
 
         def x_job(grp, h):
-            box = {}
+            job = ("x", grp, h)
 
-            def s0():
+            def add():
                 v = raw_x[grp][:].rearrange("p (t two) c -> p two t c", two=2)
-                box["sum"] = stage("x_sum")
-                nc.vector.tensor_tensor(out=box["sum"][:].rearrange("p (t c) -> p t c", t=4),
+                held[("sum", job)] = stage("x_sum")
+                nc.vector.tensor_tensor(out=held[("sum", job)][:].rearrange("p (t c) -> p t c", t=4),
                                         in0=v[:, 0, :, 512 * h:512 * h + 512], in1=v[:, 1, :, 512 * h:512 * h + 512], op=ADD)
 
-            def s1():
-                box["st"] = stage("x_sorted")
-                nc.vector.tensor_copy(out=box["st"][:].rearrange("p (c r t) -> p c t r", t=4, r=4),
-                                      in_=box["sum"][:].rearrange("p (t c r) -> p c t r", t=4, r=4))
-            return [s0, s1, lambda: quantise(xc[grp], 512 * h, E4X4, box["st"])]
+            def sort(on_vector):
+                held[job] = stage("x_sorted")
+                move(on_vector, held[job][:].rearrange("p (c r t) -> p c t r", t=4, r=4), held[("sum", job)][:].rearrange("p (t c r) -> p c t r", t=4, r=4))
+            step(("add", job), ["xb", "x2", "x3"] if grp == B else ["xa"], add, takes="s")
+            step(("sort", job), [("add", job)], sort, takes="s", frees="s")
+            step(("q", job), [("sort", job)], lambda: quantise(xc[grp], 512 * h, E4X4, held[job]), frees="s")
 
-        def tokens(grp, j):
-            return of[576 * (1 - grp):576 * (1 - grp) + 1024, :].rearrange("(p j) c -> p j c", j=8)[:, j, :]
+        def zero():
+            nc.vector.memset(zc[0][:].bitcast(I32), 0)
+            nc.vector.memset(zc[1][:].bitcast(I32), 0)
+            nc.vector.memset(fc[B][1][:].bitcast(I32), 0)
 
-        ys = {}
-
-        def dx_job(grp, t, h, vec=0):
-            box = {}
-
-            def s0():
-                box["ps"] = bank("dx")
-                for fb in range(4):
-                    mx(box["ps"][:], fc[fb], E5X4, 512 * grp + 128 * t, wc[fb], E4X4, 512 * h, 512, fb == 0, fb == 3)
-
-            def s1():
-                cols = slice(512 * h, 512 * h + 512)
-                if h == 0:
-                    ys[(grp, t, 1)] = row("y_second", [128, 1024], F32)
-                halve(vec, ys[(grp, t, 1)][:, cols], box["ps"][:])
-
-            def s2():
-                if h == 1:
-                    nc.sync.dma_start(out=tokens(grp, 2 * t + 1), in_=ys[(grp, t, 1)][:])
-            return [s0, s1, s2]
-
-        def zero_job(grp):
-            return [lambda: nc.vector.memset(extra[grp][:].bitcast(I32), 0)]
-
-        def fetch_job(grp):
-            def s0():
-                pr = parked[0:200, :].rearrange("(r s) c -> r s c", s=10)
-                for a in range(5):
-                    split = (FIRST - a + 9) // 10
-                    r0, r1, p0 = ((split, 20, 10 * split + a - FIRST), (0, split, a))[grp]
-                    (nc.sync if grp else nc.gpsimd).dma_start(out=extra[grp][p0:p0 + 10 * (r1 - r0) - 9:10], in_=pr[r0:r1, 2 * a:2 * a + 2, :])
-                if grp == 0:
-                    ys["third"] = row("third_add", [128, 1024], F32)
+        def gather(which):
+            for plane in range(2):
+                view = (lambda ap: ap.bitcast(I32)) if plane == 0 else (lambda ap: ap)
+                src = view(fc[B][plane][:]).rearrange("p (f e c) -> p f e c", f=4, e=2)[:, :, :, 128:256]
+                dst = view(zc[plane][:]).rearrange("p (f c) -> p f c", f=4)
+                if which == B:
+                    nc.vector.tensor_copy(out=dst[:, :, 324:464].rearrange("p f (a m e) -> p f a m e", m=10, e=2)[:, :, :, 0:5, :],
+                                          in_=src[:, :, :, 81:116].rearrange("p f e (a m) -> p f a m e", m=5))
+                elif which == A:
+                    nc.vector.tensor_copy(out=dst[:, :, 0:384].rearrange("p f (e c) -> p f e c", e=2)[:, :, :, 0:130].rearrange("p f e (a b) -> p f e a b", b=10)[:, :, :, :, 0:5],
+                                          in_=src[:, :, :, 16:81].rearrange("p f e (a b) -> p f e a b", b=5))
+                else:
+                    nc.vector.tensor_copy(out=dst[:, :, 128:160].rearrange("p f (e n) -> p f e n", e=2), in_=src[:, :, :, 0:16])
+                    nc.vector.tensor_copy(out=dst[:, :, 464:470].rearrange("p f (m e) -> p f m e", e=2), in_=src[:, :, :, 113:116].rearrange("p f e m -> p f m e"))
                     for d in range(2):
-                        nc.gpsimd.dma_start(out=ys["third"][d:48:2, :], in_=parked[200:224, :])
-            return [s0]
+                        nc.vector.tensor_copy(out=dst[:, :, 480 + d:528:2].rearrange("p f (m e) -> p f m e", e=2), in_=src[:, :, :, 116:128].rearrange("p f e m -> p f m e"))
+        step("zero", [], zero)
+        for which in (A, B, 2):
+            step(("gather", which), ["zero"] + [("q", ("f", fb, B)) for fb in range(4)], lambda which=which: gather(which))
 
-        def first_job(grp, t):
-            live = FIRST if grp else 128
+        def product(op, pitch, col):
+            def fill(ps, h):
+                for fb in range(4):
+                    mx(ps[:], op, E5X4, pitch * fb + col, wc[fb], E4X4, 512 * h, fb == 0, fb == 3)
+            return fill
 
-            def s0():
-                ys[(grp, t, 0)] = row("y_first", [128, 1024], F32)
-                nc.vector.tensor_tensor(out=ys[(grp, t, 0)][:], in0=ys[(grp, t, 1)][:], in1=extra[grp][:, t // 2, :], op=ADD)
+        def needs_w(job):
+            for h in range(2):
+                steps[("mm", job, h)][0].extend([("q", ("w", 4 * h + i)) for i in range(4)])
 
-            def s1():
-                nc.sync.dma_start(out=tokens(grp, 2 * t)[0:live], in_=ys[(grp, t, 0)][0:live, :])
-            return [s0, s1]
+        def extra_job(job, col, which):
+            for h in range(2):
+                def action(h=h):
+                    held[("bank", job, h)] = psum.tile([128, 512], F32, name="extra", tag="bank", bufs=8)
+                    product(zc, MOVED, col)(held[("bank", job, h)], h)
+                step(("mm", job, h), [("gather", w) for w in which], action, takes="b")
+            needs_w(job)
 
-        def third_job():
-            rows = of[0:480, :].rearrange("(r n) k -> r n k", n=120)
-            box = {}
+        def dx_job(job, fill, needs, extra, last, tokens):
+            def empty(on_vector, ps, h):
+                if h == 0:
+                    held[job] = row("y_second", [128, 1024], F32)
+                move(on_vector, held[job][:, 512 * h:512 * h + 512], ps[:])
 
-            def s0():
-                box["a"] = ys["third"]
-                box["b"] = row("third_old", [128, 1024], F32)
-                nc.gpsimd.dma_start(out=box["b"][0:42, :], in_=rows[0:3, 0:42:3, :])
-                nc.gpsimd.dma_start(out=box["b"][42:48, :], in_=rows[3, 0:18:3, :])
+            def add(h):
+                if h == 0:
+                    held[("first", job)] = row("y_first", [128, 1024], F32)
+                cols = slice(512 * h, 512 * h + 512)
+                nc.vector.tensor_tensor(out=held[("first", job)][:, cols], in0=held[("bank", extra, h)][:], in1=held[job][:, cols], op=ADD)
+            banked(job, 2, needs, fill, empty, "r")
+            needs_w(job)
+            for h in range(2):
+                step(("add", job, h), [("out", job, h), ("mm", extra, h)] + ([("add", job, 0)] if h else []) + ([("add", last, h)] if last else []),
+                     lambda h=h: add(h), takes="" if h else "r", frees="b" if last else "")
+            step(("second", job), [("out", job, 0), ("out", job, 1)], lambda: nc.sync.dma_start(out=tokens(1), in_=held[job][:]))
+            step(("first", job), [("add", job, 1), ("second", job)], lambda: nc.sync.dma_start(out=tokens(0), in_=held[("first", job)][:]), frees="rr")
 
-            def s1():
-                nc.vector.tensor_tensor(out=box["a"][0:48, :], in0=box["a"][0:48, :], in1=box["b"][0:48, :], op=ADD)
-
-            def s2():
-                nc.gpsimd.dma_start(out=rows[0:3, 0:42:3, :], in_=box["a"][0:42, :])
-                nc.gpsimd.dma_start(out=rows[3, 0:18:3, :], in_=box["a"][42:48, :])
-            return [s0], [s1, s2]
-
-        obs = {}
-
-        def dw_job(n, pair, vec=0):
-            box = {}
-
-            def s0():
-                box["ps"] = []
-                for fb in (2 * pair, 2 * pair + 1):
-                    ps = bank("dw")
-                    for grp in range(2):
-                        mx(ps[:], xc[grp], E4X4, 128 * n, lc[fb], E5X4, 512 * grp, 512, grp == 0, grp == 1)
-                    box["ps"].append(ps)
-
-            def s1():
-                box["o"] = row("dw_out", [128, 1024], F32)
-                for i in range(2):
-                    halve(i < vec, box["o"][:, 512 * i:512 * i + 512].rearrange("p (m r j) -> p m j r", j=4, r=2),
-                          box["ps"][i][:].rearrange("p (j m r) -> p m j r", j=4, r=2))
-
-            def s2():
-                nc.sync.dma_start(out=out_1[128 * n:128 * n + 128, 1024 * pair:1024 * pair + 1024], in_=box["o"][:])
-            return [s0, s1, s2]
-
-        gap = [nothing]
-        K = dkv_job
-        ek, ev = e_job(0, 1), e_job(1, 1)
-        g = [g_job(fb) for fb in range(4)]
-        f = [K(fb, 1, True, 2 * (fb == 3)) for fb in range(4)]
-        head = [zero_job(0)[0], zero_job(1)[0], ek[0], ek[1], ev[0], ev[1],
-                g[0][0], ek[2], g[0][1], f[0][0], f[0][1],
-                g[1][0], ev[2], g[1][1], f[1][0], f[1][1],
-                g[2][0], g[2][1], f[2][0], f[2][1],
-                g[3][0], f[0][2], g[3][1], f[3][0], f[1][2], f[3][1], f[2][2]]
-        for step in head:
-            step()
-        third_read, third_write = third_job()
-        flips = [w_job(fb, 0, 1) for fb in range(4)] + [w_job(0, 1), e_job(0, 0), w_job(1, 1), w_job(2, 1), w_job(3, 1), e_job(1, 0)]
-        between = [K(fb, 1, False, 1, 1) for fb in range(4)] + [dx_job(1, 0, 0), dx_job(1, 1, 0), K(0, 0, False, 0, 1), dx_job(1, 2, 0), K(1, 0, False, 1, 1), dx_job(1, 3, 0)]
-        jobs = [[f[3][2]]]
-        for i in range(10):
-            jobs += [flips[i], between[i]] + [x_job(0, (i - 5) // 2)] * (i in (5, 7))
-        jobs += [dx_job(1, 0, 1), x_job(1, 0), dx_job(1, 1, 1), dx_job(1, 2, 1), dx_job(1, 3, 1), x_job(1, 1)]
-        for i in range(4):
-            jobs += [K(i, 0, True, 2 * (i > 0), 1), dw_job(2 * i, 0), dw_job(2 * i + 1, 0)] + [fetch_job(1), fetch_job(0)] * (i == 0)
-            jobs += [first_job(1, t) for t in range(4) if t // 2 + 2 == i]
         for t in range(4):
-            jobs += [K(2 + t, 0, False, 1, 1)] if t < 2 else []
-            jobs += [dx_job(0, t, 0), dx_job(0, t, 1)] + [third_read if t == 1 else gap, first_job(0, t)]
-        for n in range(8):
-            jobs += [dw_job(n, 1, 1)] + [third_write] * (n == 2)
-        depth = max(len(j) for j in jobs)
-        for i in range(len(jobs) + depth):
-            for s in range(depth - 1, -1, -1):
-                if 0 <= i - s < len(jobs) and s < len(jobs[i - s]):
-                    jobs[i - s][s]()
+            dx_job(("dx", A, t), product(fc[A], 512, 128 * t), [("q", ("f", fb, A)) for fb in range(4)], ("z", A, t // 2), ("dx", A, t - 1) if t % 2 else None,
+                   lambda d, t=t: of[0:1024, :].rearrange("(p j) c -> p j c", j=8)[:, 2 * t + d, :])
+        for t in range(2):
+            dx_job(("dx", B, t), product(fc[B], 512, 256 * t), [("q", ("f", fb, B)) for fb in range(4)], ("z", B, 0), ("dx", B, 0) if t else None,
+                   lambda d, t=t: of[1024:1536, :].rearrange("(p j) c -> p j c", j=4)[:, 2 * t + d, :])
+            extra_job(("z", A, t), 192 * t, [A])
+        extra_job(("z", B, 0), 320, [B])
+
+        def rest_job():
+            job, extra = ("dx", 2, 0), ("z", 2, 0)
+            rows = of[0:480, :].rearrange("(r n) k -> r n k", n=120)
+            spans = ((32, 74, rows[0:3, 0:42:3, :]), (74, 80, rows[3, 0:18:3, :]))
+            units = of[1536:1600, :].rearrange("(n e d) c -> e n d c", e=2, d=2)
+            extra_job(extra, 448, [B, 2])
+            banked(job, 2, [("gather", A), ("gather", 2)], product(zc, MOVED, 128), lambda on_vector, ps, h: move(on_vector, rest[0:32, 1, 512 * h:512 * h + 512], ps[0:32, :]), "")
+            needs_w(job)
+            step("third_read", [(k, ("dx", A, t)) for t in range(4) for k in ("first", "second")],
+                 lambda: [nc.gpsimd.dma_start(out=rest[p0:p1, 1, :], in_=hbm) for p0, p1, hbm in spans])
+            for h in range(2):
+                step(("add", job, h), [("out", job, h), ("mm", extra, h), "third_read"],
+                     lambda h=h: nc.vector.tensor_tensor(out=rest[0:80, 0, 512 * h:512 * h + 512], in0=held[("bank", extra, h)][0:80, :],
+                                                         in1=rest[0:80, 1, 512 * h:512 * h + 512], op=ADD), frees="b")
+            both = [("add", job, 0), ("add", job, 1)]
+            step("third_write", both, lambda: [nc.gpsimd.dma_start(out=hbm, in_=rest[p0:p1, 0, :]) for p0, p1, hbm in spans])
+            step("rest_store", both, lambda: [nc.sync.dma_start(out=units[e], in_=rest[16 * e:16 * e + 16]) for e in range(2)])
+
+        def dw_job(n, pair):
+            job = ("dw", n, pair)
+
+            def fill(ps, i):
+                for grp in range(2):
+                    mx(ps[:], xc[grp], E4X4, 128 * n, lc[2 * pair + i], E5X4, 512 * grp, grp == 0, grp == 1)
+
+            def empty(on_vector, ps, i):
+                if i == 0:
+                    held[job] = row("dw_out", [128, 1024], F32)
+                move(on_vector, held[job][:, 512 * i:512 * i + 512].rearrange("p (m u r) -> p m u r", u=2, r=2), ps[:].rearrange("p (u m r) -> p m u r", u=2, r=2))
+            banked(job, 2, [("q", ("x", grp, n // 4)) for grp in range(2)] + [("q", ("l", 2 * pair + i, grp)) for i in range(2) for grp in range(2)], fill, empty, "r")
+            step(("store", job), [("out", job, 0), ("out", job, 1)], lambda: nc.sync.dma_start(out=out_1[128 * n:128 * n + 128, 1024 * pair:1024 * pair + 1024], in_=held[job][:]), frees="r")
+
+        for grp in range(2):
+            for i in range(2):
+                e_job(i, grp)
+                x_job(grp, i)
+            for i in range(4):
+                dkv_job(i, grp)
+        for i in range(4):
+            g_job(i)
+        for i in range(8):
+            w_job(i)
+            dw_job(i, 0)
+            dw_job(i, 1)
+        rest_job()
+
+        def mm(job, *which):
+            return [("mm", job, i) for i in which]
+
+        def out(job, *which):
+            return [("out", job, i) for i in which]
+
+        def q(*jobs):
+            return [("q", job) for job in jobs]
+
+        def sort(*jobs):
+            return [("sort", job) for job in jobs]
+
+        E = [[("e", e, grp) for grp in range(2)] for e in range(2)]
+        G = [("g", i) for i in range(4)]
+        W = [("w", i) for i in range(8)]
+        D = [[("d", fb, grp) for fb in range(4)] for grp in range(2)]
+        F = [[("f", fb, grp) for fb in range(4)] for grp in range(2)]
+        L = [[("l", fb, grp) for fb in range(4)] for grp in range(2)]
+        X = [[("x", grp, h) for h in range(2)] for grp in range(2)]
+        DX = [[("dx", A, t) for t in range(4)], [("dx", B, t) for t in range(2)], [("dx", 2, 0)]]
+        Z = [[("z", A, 0), ("z", A, 1)], [("z", B, 0)], [("z", 2, 0)]]
+        DW = [[("dw", n, pair) for n in range(8)] for pair in range(2)]
+
+        sync = [("load", job) for job in [E[0][A], G[0], G[1], E[1][A], G[2], G[3]] + W[:4] + [E[0][B]] + W[4:] + [E[1][B]]] + ["xb", "xa"]
+        pool_queue = ["x3", "third_read", "third_write"]
+        tensor = mm(E[0][A], 0, 1) + mm(D[A][0], 0, 1, 2, 3) + mm(E[1][A], 0, 1)
+        scalar = out(E[0][A], 0, 1) + out(D[A][0], 0, 1, 2, 3) + out(E[1][A], 0)
+        vector = ["zero"] + sort(G[0]) + q(G[0], E[0][A]) + sort(G[1]) + q(G[1]) + sort(G[2]) + out(E[1][A], 1) + q(G[2], E[1][A]) + sort(G[3])
+        for i in range(1, 4):
+            tensor += mm(D[A][i], 0, 1) + mm(F[A][i - 1], 0, 1) + mm(D[A][i], 2, 3) + mm(W[i - 1], 0, 1)
+            scalar += out(D[A][i], 0, 1) + out(F[A][i - 1], 0) + out(D[A][i], 2, 3) + out(W[i - 1], 0)
+            vector += (q(G[3]) if i == 1 else q(W[i - 2])) + out(F[A][i - 1], 1) + out(W[i - 1], 1) + q(F[A][i - 1])
+        tensor += mm(W[3], 0, 1) + mm(F[A][3], 0, 1) + mm(E[0][B], 0, 1)
+        scalar += out(W[3], 0) + out(F[A][3], 0) + out(E[0][B], 0, 1) + ["x2"]
+        vector += q(W[2]) + out(W[3], 1) + out(F[A][3], 1) + q(W[3], F[A][3]) + sort(L[A][0]) + q(E[0][B])
+        beside = [q(L[A][0]) + sort(L[A][1]), q(L[A][1]) + sort(L[A][2]), q(L[A][2]) + sort(L[A][3]), q(L[A][3]) + sort(L[B][0])]
+        for t in range(4):
+            tensor += mm(W[4 + t], 0, 1) + mm(DX[A][t], 0) + mm(D[B][t // 2], 2 * (t % 2), 2 * (t % 2) + 1)
+            scalar += out(W[4 + t], 0, 1) + out(DX[A][t], 0) + out(D[B][t // 2], 2 * (t % 2), 2 * (t % 2) + 1)
+            vector += beside[t] + q(W[4 + t])
+        tensor += mm(E[1][B], 0, 1) + mm(F[B][0], 0, 1)
+        scalar += out(E[1][B], 0) + out(F[B][0], 0)
+        vector += q(L[B][0]) + out(E[1][B], 1) + out(F[B][0], 1) + q(E[1][B], F[B][0])
+        between = [mm(F[B][1], 0, 1) + mm(D[B][2], 0, 1, 2, 3), mm(D[B][3], 0, 1, 2, 3), mm(F[B][2], 0, 1), mm(F[B][3], 0, 1)]
+        beside = [sort(L[B][1]) + q(F[B][1], L[B][1]), out(D[B][2], 3) + [("add", X[B][0])] + out(D[B][3], 3), sort(X[B][0]) + out(F[B][2], 1) + q(F[B][2]), out(F[B][3], 1) + q(X[B][0], F[B][3]) + [("gather", A)]]
+        for t in range(4):
+            tensor += mm(DX[A][t], 1) + between[t]
+            vector += beside[t]
+            scalar += out(DX[A][t], 1) + [("out",) + s[1:] for s in between[t] if ("out",) + s[1:] not in sum(beside, [])]
+            sync += [("second", DX[A][t])]
+        zb, (b0, b1) = Z[B][0], DX[B]
+        tensor += mm(b0, 0, 1) + mm(Z[A][0], 0, 1) + mm(b1, 0, 1) + mm(Z[A][1], 0, 1) + mm(zb, 0, 1)
+        scalar += out(b0, 0, 1) + sort(L[B][2]) + out(b1, 0, 1) + sort(L[B][3], X[B][1])
+        vector += [("gather", B), ("add", X[A][0])] + [("add", DX[A][t], h) for h in range(2) for t in range(2)] + sort(X[A][0])
+        vector += q(L[B][2], X[A][0]) + [("add", X[B][1])] + [("add", DX[A][2 + t], h) for h in range(2) for t in range(2)] + [("add", job, h) for h in range(2) for job in DX[B]]
+        sync += [("second", b0), ("first", DX[A][0]), ("first", DX[A][1]), ("second", b1), ("first", DX[A][2]), ("first", DX[A][3]), ("first", b0), ("first", b1)]
+        beside = [q(L[B][3]) + [("add", X[A][1])], q(X[B][1]) + sort(X[A][1]), q(X[A][1]), [("gather", 2)]]
+        for n, job in enumerate(DW[0][:4] + DW[1][:4] + DW[0][4:] + DW[1][4:]):
+            tensor += mm(job, 0, 1)
+            scalar += out(job, 0, 1) if n < 4 else out(job, 0)
+            vector += beside[n] if n < 4 else out(job, 1)
+            sync += [("store", job)]
+            if n in (6, 9):
+                tensor += mm(DX[2][0], n // 8) + mm(Z[2][0], n // 8)
+                scalar += out(DX[2][0], n // 8)
+                vector += [("add", DX[2][0], n // 8)]
+            sync += ["rest_store"] * (n == 12)
+
+        room = {"b": 8, "s": STAGES, "r": ROWS}
+        written = set()
+
+        def ready(name):
+            needs, action, takes, frees = steps[name]
+            return all(n in written for n in needs) and all(room[c] > 0 for c in takes)
+
+        def write_out(name, queue):
+            needs, action, takes, frees = steps[name]
+            if name[0] in ("out", "sort"):
+                action(queue is vector)
+            else:
+                action()
+            for c in takes:
+                room[c] -= 1
+            for c in frees:
+                room[c] += 1
+            written.add(name)
+
+        while tensor or scalar or vector or sync or pool_queue:
+            before = len(written)
+            for queue in (sync, pool_queue, vector, scalar):
+                while queue and ready(queue[0]):
+                    write_out(queue.pop(0), queue)
+            if tensor and ready(tensor[0]):
+                write_out(tensor.pop(0), tensor)
+            assert len(written) > before, (tensor[:1], scalar[:1], vector[:1], sync[:1], pool_queue[:1], room)
+        assert len(written) == len(steps)

@@ -18,7 +18,7 @@ BYTES = 2 * (1600 * 1024 + 1024 * 2048 + 2 * 1024 * 512 + 2 * 512 * 1024) + 4 * 
 
 ROWS = 15
 STAGES = 9
-MOVED = 576
+MOVED = 512
 A, B = 0, 1
 
 
@@ -210,17 +210,18 @@ def tile_efficientmultiscaledilatedattention_pa_v_kernel(tc, x, W_kv, b_kv, E_k,
                 view = (lambda ap: ap.bitcast(I32)) if plane == 0 else (lambda ap: ap)
                 src = view(fc[B][plane][:]).rearrange("p (f e c) -> p f e c", f=4, e=2)[:, :, :, 128:256]
                 dst = view(zc[plane][:]).rearrange("p (f c) -> p f c", f=4)
-                if which == B:
-                    nc.vector.tensor_copy(out=dst[:, :, 324:464].rearrange("p f (a m e) -> p f a m e", m=10, e=2)[:, :, :, 0:5, :],
-                                          in_=src[:, :, :, 81:116].rearrange("p f e (a m) -> p f a m e", m=5))
-                elif which == A:
-                    nc.vector.tensor_copy(out=dst[:, :, 0:384].rearrange("p f (e c) -> p f e c", e=2)[:, :, :, 0:130].rearrange("p f e (a b) -> p f e a b", b=10)[:, :, :, :, 0:5],
-                                          in_=src[:, :, :, 16:81].rearrange("p f e (a b) -> p f e a b", b=5))
+                if which == A:
+                    for w in range(2):
+                        nc.vector.tensor_copy(out=dst[:, :, 128 * w:128 * w + 130].rearrange("p f (a b) -> p f a b", b=10)[:, :, :, 0:5],
+                                              in_=src[:, :, w, 16:81].rearrange("p f (a b) -> p f a b", b=5))
+                elif which == B:
+                    nc.vector.tensor_copy(out=dst[:, :, 260:380].rearrange("p f (a m e) -> p f a m e", m=10, e=2)[:, :, :, 0:5, :],
+                                          in_=src[:, :, :, 81:111].rearrange("p f e (a m) -> p f a m e", m=5))
+                    nc.vector.tensor_copy(out=dst[:, :, 380:384].rearrange("p f (m e) -> p f m e", e=2), in_=src[:, :, :, 111:113].rearrange("p f e m -> p f m e"))
                 else:
-                    nc.vector.tensor_copy(out=dst[:, :, 128:160].rearrange("p f (e n) -> p f e n", e=2), in_=src[:, :, :, 0:16])
-                    nc.vector.tensor_copy(out=dst[:, :, 464:470].rearrange("p f (m e) -> p f m e", e=2), in_=src[:, :, :, 113:116].rearrange("p f e m -> p f m e"))
                     for d in range(2):
-                        nc.vector.tensor_copy(out=dst[:, :, 480 + d:528:2].rearrange("p f (m e) -> p f m e", e=2), in_=src[:, :, :, 116:128].rearrange("p f e m -> p f m e"))
+                        nc.vector.tensor_copy(out=dst[:, :, 384 + d:444:2].rearrange("p f (m e) -> p f m e", e=2), in_=src[:, :, :, 113:128].rearrange("p f e m -> p f m e"))
+                    nc.vector.tensor_copy(out=dst[:, :, 444:476].rearrange("p f (e n) -> p f e n", e=2), in_=src[:, :, :, 0:16])
         step("zero", [], zero)
         for which in (A, B, 2):
             step(("gather", which), ["zero"] + [("q", ("f", fb, B)) for fb in range(4)], lambda which=which: gather(which))
@@ -268,26 +269,22 @@ def tile_efficientmultiscaledilatedattention_pa_v_kernel(tc, x, W_kv, b_kv, E_k,
         for t in range(2):
             dx_job(("dx", B, t), product(fc[B], 512, 256 * t), [("q", ("f", fb, B)) for fb in range(4)], ("z", B, 0), ("dx", B, 0) if t else None,
                    lambda d, t=t: of[1024:1536, :].rearrange("(p j) c -> p j c", j=4)[:, 2 * t + d, :])
-            extra_job(("z", A, t), 192 * t, [A])
-        extra_job(("z", B, 0), 320, [B])
+            extra_job(("z", A, t), 128 * t, [A])
+        extra_job(("z", B, 0), 256, [B])
 
         def rest_job():
-            job, extra = ("dx", 2, 0), ("z", 2, 0)
+            job = ("dx", 2, 0)
             rows = of[0:480, :].rearrange("(r n) k -> r n k", n=120)
-            spans = ((32, 74, rows[0:3, 0:42:3, :]), (74, 80, rows[3, 0:18:3, :]))
-            units = of[1536:1600, :].rearrange("(n e d) c -> e n d c", e=2, d=2)
-            extra_job(extra, 448, [B, 2])
-            banked(job, 2, [("gather", A), ("gather", 2)], product(zc, MOVED, 128), lambda on_vector, ps, h: move(on_vector, rest[0:32, 1, 512 * h:512 * h + 512], ps[0:32, :]), "")
+            spans = ((0, 12, of[1536:1560:2, :]), (12, 54, rows[0:3, 0:42:3, :]), (54, 60, rows[3, 0:18:3, :]))
+            units = of[1536:1600, :].rearrange("(n e d) c -> e d n c", e=2, d=2)
+            banked(job, 2, [("gather", 2)], product(zc, MOVED, 384), lambda on_vector, ps, h: move(on_vector, rest[0:92, 0, 512 * h:512 * h + 512], ps[0:92, :]), "")
             needs_w(job)
-            step("third_read", [(k, ("dx", A, t)) for t in range(4) for k in ("first", "second")],
+            step("rest_store", [("out", job, 0), ("out", job, 1)],
+                 lambda: [nc.sync.dma_start(out=units[e, d], in_=rest[60 + 16 * e:76 + 16 * e, 0, :]) for e in range(2) for d in range(2)])
+            step("third_read", ["rest_store"] + [(k, ("dx", A, t)) for t in range(4) for k in ("first", "second")],
                  lambda: [nc.gpsimd.dma_start(out=rest[p0:p1, 1, :], in_=hbm) for p0, p1, hbm in spans])
-            for h in range(2):
-                step(("add", job, h), [("out", job, h), ("mm", extra, h), "third_read"],
-                     lambda h=h: nc.vector.tensor_tensor(out=rest[0:80, 0, 512 * h:512 * h + 512], in0=held[("bank", extra, h)][0:80, :],
-                                                         in1=rest[0:80, 1, 512 * h:512 * h + 512], op=ADD), frees="b")
-            both = [("add", job, 0), ("add", job, 1)]
-            step("third_write", both, lambda: [nc.gpsimd.dma_start(out=hbm, in_=rest[p0:p1, 0, :]) for p0, p1, hbm in spans])
-            step("rest_store", both, lambda: [nc.sync.dma_start(out=units[e], in_=rest[16 * e:16 * e + 16]) for e in range(2)])
+            step("third_add", ["third_read"], lambda: nc.vector.tensor_tensor(out=rest[0:60, 1, :], in0=rest[0:60, 0, :], in1=rest[0:60, 1, :], op=ADD))
+            step("third_write", ["third_add"], lambda: [nc.gpsimd.dma_start(out=hbm, in_=rest[p0:p1, 1, :]) for p0, p1, hbm in spans])
 
         def dw_job(n, pair):
             job = ("dw", n, pair)
@@ -337,25 +334,26 @@ def tile_efficientmultiscaledilatedattention_pa_v_kernel(tc, x, W_kv, b_kv, E_k,
         L = [[("l", fb, grp) for fb in range(4)] for grp in range(2)]
         X = [[("x", grp, h) for h in range(2)] for grp in range(2)]
         DX = [[("dx", A, t) for t in range(4)], [("dx", B, t) for t in range(2)], [("dx", 2, 0)]]
-        Z = [[("z", A, 0), ("z", A, 1)], [("z", B, 0)], [("z", 2, 0)]]
+        Z = [[("z", A, 0), ("z", A, 1)], [("z", B, 0)]]
         DW = [[("dw", n, pair) for n in range(8)] for pair in range(2)]
 
         sync = [("load", job) for job in [E[0][A], G[0], G[1], E[1][A], G[2], G[3]] + W[:4] + [E[0][B]] + W[4:] + [E[1][B]]] + ["xb", "xa"]
+        steps["xa"][0].append("x2")
         pool_queue = ["x3", "third_read", "third_write"]
-        tensor = mm(E[0][A], 0, 1) + mm(D[A][0], 0, 1, 2, 3) + mm(E[1][A], 0, 1)
-        scalar = out(E[0][A], 0, 1) + out(D[A][0], 0, 1, 2, 3) + out(E[1][A], 0)
-        vector = ["zero"] + sort(G[0]) + q(G[0], E[0][A]) + sort(G[1]) + q(G[1]) + sort(G[2]) + out(E[1][A], 1) + q(G[2], E[1][A]) + sort(G[3])
-        for i in range(1, 4):
-            tensor += mm(D[A][i], 0, 1) + mm(F[A][i - 1], 0, 1) + mm(D[A][i], 2, 3) + mm(W[i - 1], 0, 1)
-            scalar += out(D[A][i], 0, 1) + out(F[A][i - 1], 0) + out(D[A][i], 2, 3) + out(W[i - 1], 0)
-            vector += (q(G[3]) if i == 1 else q(W[i - 2])) + out(F[A][i - 1], 1) + out(W[i - 1], 1) + q(F[A][i - 1])
-        tensor += mm(W[3], 0, 1) + mm(F[A][3], 0, 1) + mm(E[0][B], 0, 1)
-        scalar += out(W[3], 0) + out(F[A][3], 0) + out(E[0][B], 0, 1) + ["x2"]
-        vector += q(W[2]) + out(W[3], 1) + out(F[A][3], 1) + q(W[3], F[A][3]) + sort(L[A][0]) + q(E[0][B])
+        tensor = mm(E[0][A], 0, 1) + mm(D[A][0], 0, 1, 2, 3) + mm(E[1][A], 0, 1) + mm(D[A][1], 0, 1) + mm(F[A][0], 0, 1) + mm(D[A][1], 2, 3)
+        scalar = out(E[0][A], 0, 1) + out(D[A][0], 0, 1, 2, 3) + out(E[1][A], 0) + out(D[A][1], 0, 1) + out(F[A][0], 0, 1) + out(D[A][1], 2, 3)
+        vector = ["zero"] + sort(G[0]) + q(G[0], E[0][A]) + sort(G[1]) + q(G[1]) + sort(G[2]) + out(E[1][A], 1) + q(G[2], E[1][A]) + sort(G[3]) + q(F[A][0], G[3])
+        for i in range(2):
+            tensor += mm(D[A][2 + i], 0, 1) + mm(W[i], 0, 1) + mm(D[A][2 + i], 2, 3) + mm(F[A][1 + i], 0, 1)
+            scalar += out(D[A][2 + i], 0, 1) + out(W[i], 0) + out(D[A][2 + i], 2, 3) + out(F[A][1 + i], 0)
+            vector += out(W[i], 1) + (q(F[A][i]) if i else []) + out(F[A][1 + i], 1) + q(W[i])
+        tensor += mm(W[2], 0, 1) + mm(F[A][3], 0, 1) + mm(W[3], 0, 1) + mm(E[0][B], 0, 1)
+        scalar += out(W[2], 0) + out(F[A][3], 0) + out(W[3], 0) + out(E[0][B], 0, 1) + ["x2"]
+        vector += out(W[2], 1) + q(F[A][2]) + out(F[A][3], 1) + q(W[2]) + out(W[3], 1) + q(F[A][3], W[3]) + sort(L[A][0]) + q(E[0][B])
         beside = [q(L[A][0]) + sort(L[A][1]), q(L[A][1]) + sort(L[A][2]), q(L[A][2]) + sort(L[A][3]), q(L[A][3]) + sort(L[B][0])]
         for t in range(4):
-            tensor += mm(W[4 + t], 0, 1) + mm(DX[A][t], 0) + mm(D[B][t // 2], 2 * (t % 2), 2 * (t % 2) + 1)
-            scalar += out(W[4 + t], 0, 1) + out(DX[A][t], 0) + out(D[B][t // 2], 2 * (t % 2), 2 * (t % 2) + 1)
+            tensor += mm(DX[A][t], 0) + mm(W[4 + t], 0, 1) + mm(D[B][t // 2], 2 * (t % 2), 2 * (t % 2) + 1)
+            scalar += out(DX[A][t], 0) + out(W[4 + t], 0, 1) + out(D[B][t // 2], 2 * (t % 2), 2 * (t % 2) + 1)
             vector += beside[t] + q(W[4 + t])
         tensor += mm(E[1][B], 0, 1) + mm(F[B][0], 0, 1)
         scalar += out(E[1][B], 0) + out(F[B][0], 0)
@@ -367,23 +365,26 @@ def tile_efficientmultiscaledilatedattention_pa_v_kernel(tc, x, W_kv, b_kv, E_k,
             vector += beside[t]
             scalar += out(DX[A][t], 1) + [("out",) + s[1:] for s in between[t] if ("out",) + s[1:] not in sum(beside, [])]
             sync += [("second", DX[A][t])]
-        zb, (b0, b1) = Z[B][0], DX[B]
-        tensor += mm(b0, 0, 1) + mm(Z[A][0], 0, 1) + mm(b1, 0, 1) + mm(Z[A][1], 0, 1) + mm(zb, 0, 1)
-        scalar += out(b0, 0, 1) + sort(L[B][2]) + out(b1, 0, 1) + sort(L[B][3], X[B][1])
-        vector += [("gather", B), ("add", X[A][0])] + [("add", DX[A][t], h) for h in range(2) for t in range(2)] + sort(X[A][0])
-        vector += q(L[B][2], X[A][0]) + [("add", X[B][1])] + [("add", DX[A][2 + t], h) for h in range(2) for t in range(2)] + [("add", job, h) for h in range(2) for job in DX[B]]
-        sync += [("second", b0), ("first", DX[A][0]), ("first", DX[A][1]), ("second", b1), ("first", DX[A][2]), ("first", DX[A][3]), ("first", b0), ("first", b1)]
-        beside = [q(L[B][3]) + [("add", X[A][1])], q(X[B][1]) + sort(X[A][1]), q(X[A][1]), [("gather", 2)]]
+        zb, (b0, b1), last = Z[B][0], DX[B], DX[2][0]
+        tensor += mm(b0, 0, 1) + mm(Z[A][0], 0, 1) + mm(Z[A][1], 0, 1) + mm(b1, 0, 1)
+        scalar += out(b0, 0, 1) + sort(L[B][2], L[B][3]) + out(b1, 0, 1)
+        vector += [("add", X[A][0])] + [("add", DX[A][t], h) for h in range(2) for t in range(2)] + sort(X[A][0])
+        vector += [("add", DX[A][2 + t], 0) for t in range(2)] + q(X[A][0]) + [("add", DX[A][2 + t], 1) for t in range(2)]
+        sync += [("second", b0)] + [("first", job) for job in DX[A]] + [("second", b1)]
+        beside = [[("gather", 2)] + q(L[B][2]), [("add", X[B][1])] + q(L[B][3]), sort(X[B][1]), [("add", X[A][1])] + q(X[B][1]), sort(X[A][1]), [("gather", B)] + q(X[A][1])]
         for n, job in enumerate(DW[0][:4] + DW[1][:4] + DW[0][4:] + DW[1][4:]):
             tensor += mm(job, 0, 1)
-            scalar += out(job, 0, 1) if n < 4 else out(job, 0)
-            vector += beside[n] if n < 4 else out(job, 1)
+            scalar += out(job, 0, 1) if n < 6 else out(job, 0)
+            vector += (beside[n] if n < 6 else out(job, 1)) + ["third_add"] * (n == 11)
             sync += [("store", job)]
-            if n in (6, 9):
-                tensor += mm(DX[2][0], n // 8) + mm(Z[2][0], n // 8)
-                scalar += out(DX[2][0], n // 8)
-                vector += [("add", DX[2][0], n // 8)]
-            sync += ["rest_store"] * (n == 12)
+            if n == 3:
+                tensor += mm(last, 0, 1)
+                scalar += out(last, 0, 1)
+                sync += ["rest_store"]
+            if n == 9:
+                tensor += mm(zb, 0, 1)
+                vector += [("add", tile, h) for h in range(2) for tile in DX[B]]
+                sync += [("first", b0), ("first", b1)]
 
         room = {"b": 8, "s": STAGES, "r": ROWS}
         written = set()

@@ -91,16 +91,20 @@ def tile_efficientmultiscaledilatedattention_pa_v_kernel(tc, x, W_kv, b_kv, E_k,
         step("xb", [], lambda: [nc.sync.dma_start(out=raw_x[B][0:64], in_=quads(1024, 64)), nc.sync.dma_start(out=raw_x[B][64:72], in_=quads(1536, 8))])
         step("x2", [], lambda: nc.scalar.dma_start(out=raw_x[B][72:122], in_=xf.rearrange("(r n) c -> r n c", n=80)[:, 0:40:2, :]))
 
-        def load_third():
-            third = xf[0:480, :].rearrange("(r n) c -> r n c", n=120)
-            entry = 0
-            while entry < 48:
-                m = min(14 - entry % 14, 8 - entry % 8, 48 - entry)
-                r, c = divmod(entry, 14)
-                p, s = divmod(entry, 8)
-                nc.gpsimd.dma_start(out=raw_x[B][122 + p:123 + p, s:s + m, :], in_=third[r:r + 1, 3 * c:3 * (c + m):3, :])
-                entry = entry + m
-        step("x3", [], load_third)
+        third = xf[0:480, :].rearrange("(r n) c -> r n c", n=120)
+        runs = []
+        entry = 0
+        while entry < 48:
+            runs.append((entry, min(14 - entry % 14, 8 - entry % 8, 48 - entry)))
+            entry = entry + runs[-1][1]
+
+        def load_third(i):
+            entry, m = runs[i]
+            r, c = divmod(entry, 14)
+            p, s = divmod(entry, 8)
+            step(("x3", i), [], lambda: nc.sync.dma_start(out=raw_x[B][122 + p:123 + p, s:s + m, :], in_=third[r:r + 1, 3 * c:3 * (c + m):3, :]))
+        for i in range(len(runs)):
+            load_third(i)
 
         def banked(job, count, needs, fill, empty, room, last_frees=""):
             def filler(i):
@@ -196,7 +200,7 @@ def tile_efficientmultiscaledilatedattention_pa_v_kernel(tc, x, W_kv, b_kv, E_k,
             def sort(on_vector):
                 held[job] = stage("x_sorted")
                 move(on_vector, held[job][:].rearrange("p (c r t) -> p c t r", t=4, r=4), held[("sum", job)][:].rearrange("p (t c r) -> p c t r", t=4, r=4))
-            step(("add", job), ["xb", "x2", "x3"] if grp == B else ["xa"], add, takes="s")
+            step(("add", job), ["xb", "x2"] + [("x3", i) for i in range(len(runs))] if grp == B else ["xa"], add, takes="s")
             step(("sort", job), [("add", job)], sort, takes="s", frees="s")
             step(("q", job), [("sort", job)], lambda: quantise(xc[grp], 512 * h, E4X4, held[job]), frees="s")
 
@@ -337,9 +341,12 @@ def tile_efficientmultiscaledilatedattention_pa_v_kernel(tc, x, W_kv, b_kv, E_k,
         Z = [[("z", A, 0), ("z", A, 1)], [("z", B, 0)]]
         DW = [[("dw", n, pair) for n in range(8)] for pair in range(2)]
 
-        sync = [("load", job) for job in [E[0][A], G[0], G[1], E[1][A], G[2], G[3]] + W[:4] + [E[0][B]] + W[4:] + [E[1][B]]] + ["xb", "xa"]
+        sync = [("load", job) for job in (E[0][A], G[0], G[1], E[1][A], G[2], G[3], W[0])]
+        for i, job in enumerate(W[1:4] + [E[0][B]] + W[4:] + [E[1][B]]):
+            sync += [("load", job), ("x3", i)]
+        sync += ["xb", "xa"]
         steps["xa"][0].append("x2")
-        pool_queue = ["x3", "third_read", "third_write"]
+        pool_queue = ["third_read", "third_write"]
         tensor = mm(E[0][A], 0, 1) + mm(D[A][0], 0, 1, 2, 3) + mm(E[1][A], 0, 1) + mm(D[A][1], 0, 1) + mm(F[A][0], 0, 1) + mm(D[A][1], 2, 3)
         scalar = out(E[0][A], 0, 1) + out(D[A][0], 0, 1, 2, 3) + out(E[1][A], 0) + out(D[A][1], 0, 1) + out(F[A][0], 0, 1) + out(D[A][1], 2, 3)
         vector = ["zero"] + sort(G[0]) + q(G[0], E[0][A]) + sort(G[1]) + q(G[1]) + sort(G[2]) + out(E[1][A], 1) + q(G[2], E[1][A]) + sort(G[3]) + q(F[A][0], G[3])
@@ -359,29 +366,25 @@ def tile_efficientmultiscaledilatedattention_pa_v_kernel(tc, x, W_kv, b_kv, E_k,
         scalar += out(E[1][B], 0) + out(F[B][0], 0)
         vector += q(L[B][0]) + out(E[1][B], 1) + out(F[B][0], 1) + q(E[1][B], F[B][0])
         between = [mm(F[B][1], 0, 1) + mm(D[B][2], 0, 1, 2, 3), mm(D[B][3], 0, 1, 2, 3), mm(F[B][2], 0, 1), mm(F[B][3], 0, 1)]
-        beside = [sort(L[B][1]) + q(F[B][1], L[B][1]), out(D[B][2], 3) + [("add", X[B][0])] + out(D[B][3], 3), sort(X[B][0]) + out(F[B][2], 1) + q(F[B][2]), out(F[B][3], 1) + q(X[B][0], F[B][3]) + [("gather", A)]]
+        beside = [sort(L[B][1]) + q(F[B][1], L[B][1]), out(D[B][2], 3) + [("add", X[B][0])] + out(D[B][3], 3), sort(X[B][0]) + out(F[B][2], 1) + q(F[B][2]), out(F[B][3], 1) + q(F[B][3]) + [("gather", 2), ("gather", A)] + q(X[B][0])]
         for t in range(4):
             tensor += mm(DX[A][t], 1) + between[t]
             vector += beside[t]
             scalar += out(DX[A][t], 1) + [("out",) + s[1:] for s in between[t] if ("out",) + s[1:] not in sum(beside, [])]
             sync += [("second", DX[A][t])]
         zb, (b0, b1), last = Z[B][0], DX[B], DX[2][0]
-        tensor += mm(b0, 0, 1) + mm(Z[A][0], 0, 1) + mm(Z[A][1], 0, 1) + mm(b1, 0, 1)
-        scalar += out(b0, 0, 1) + sort(L[B][2], L[B][3]) + out(b1, 0, 1)
+        tensor += mm(b0, 0, 1) + mm(last, 0, 1) + mm(Z[A][0], 0, 1) + mm(Z[A][1], 0, 1) + mm(b1, 0, 1)
+        scalar += out(b0, 0, 1) + out(last, 0, 1) + sort(L[B][2], L[B][3]) + out(b1, 0, 1)
         vector += [("add", X[A][0])] + [("add", DX[A][t], h) for h in range(2) for t in range(2)] + sort(X[A][0])
         vector += [("add", DX[A][2 + t], 0) for t in range(2)] + q(X[A][0]) + [("add", DX[A][2 + t], 1) for t in range(2)]
-        sync += [("second", b0)] + [("first", job) for job in DX[A]] + [("second", b1)]
-        beside = [[("gather", 2)] + q(L[B][2]), [("add", X[B][1])] + q(L[B][3]), sort(X[B][1]), [("add", X[A][1])] + q(X[B][1]), sort(X[A][1]), [("gather", B)] + q(X[A][1])]
+        sync += [("second", b0), "rest_store"] + [("first", job) for job in DX[A]] + [("second", b1)]
+        beside = [q(L[B][2]), [("add", X[B][1])] + q(L[B][3]), sort(X[B][1]), [("add", X[A][1])] + q(X[B][1]), sort(X[A][1]), [("gather", B)] + q(X[A][1])]
         for n, job in enumerate(DW[0][:4] + DW[1][:4] + DW[0][4:] + DW[1][4:]):
             tensor += mm(job, 0, 1)
             scalar += out(job, 0, 1) if n < 6 else out(job, 0)
-            vector += (beside[n] if n < 6 else out(job, 1)) + ["third_add"] * (n == 11)
+            vector += (beside[n] if n < 6 else out(job, 1)) + ["third_add"] * (n == 10)
             sync += [("store", job)]
-            if n == 3:
-                tensor += mm(last, 0, 1)
-                scalar += out(last, 0, 1)
-                sync += ["rest_store"]
-            if n == 9:
+            if n == 7:
                 tensor += mm(zb, 0, 1)
                 vector += [("add", tile, h) for h in range(2) for tile in DX[B]]
                 sync += [("first", b0), ("first", b1)]

@@ -279,16 +279,16 @@ def tile_efficientmultiscaledilatedattention_pa_v_kernel(tc, x, W_kv, b_kv, E_k,
         def rest_job():
             job = ("dx", 2, 0)
             rows = of[0:480, :].rearrange("(r n) k -> r n k", n=120)
-            spans = ((0, 12, of[1536:1560:2, :]), (12, 54, rows[0:3, 0:42:3, :]), (54, 60, rows[3, 0:18:3, :]))
+            spans = [(0, 12, of[1536:1560:2, :])] + [(12 + 14 * r, min(26 + 14 * r, 60), rows[r, 0:3 * min(14, 48 - 14 * r):3, :]) for r in range(4)]
             units = of[1536:1600, :].rearrange("(n e d) c -> e d n c", e=2, d=2)
             banked(job, 2, [("gather", 2)], product(zc, MOVED, 384), lambda on_vector, ps, h: move(on_vector, rest[0:92, 0, 512 * h:512 * h + 512], ps[0:92, :]), "")
             needs_w(job)
             step("rest_store", [("out", job, 0), ("out", job, 1)],
                  lambda: [nc.sync.dma_start(out=units[e, d], in_=rest[60 + 16 * e:76 + 16 * e, 0, :]) for e in range(2) for d in range(2)])
             step("third_read", ["rest_store"] + [(k, ("dx", A, t)) for t in range(4) for k in ("first", "second")],
-                 lambda: [nc.gpsimd.dma_start(out=rest[p0:p1, 1, :], in_=hbm) for p0, p1, hbm in spans])
+                 lambda: [nc.sync.dma_start(out=rest[p0:p1, 1, :], in_=hbm) for p0, p1, hbm in spans])
             step("third_add", ["third_read"], lambda: nc.vector.tensor_tensor(out=rest[0:60, 1, :], in0=rest[0:60, 0, :], in1=rest[0:60, 1, :], op=ADD))
-            step("third_write", ["third_add"], lambda: [nc.gpsimd.dma_start(out=hbm, in_=rest[p0:p1, 1, :]) for p0, p1, hbm in spans])
+            step("third_write", ["third_add"], lambda: [nc.sync.dma_start(out=hbm, in_=rest[p0:p1, 1, :]) for p0, p1, hbm in spans])
 
         def dw_job(n, pair):
             job = ("dw", n, pair)
@@ -346,7 +346,7 @@ def tile_efficientmultiscaledilatedattention_pa_v_kernel(tc, x, W_kv, b_kv, E_k,
             sync += [("load", job), ("x3", i)]
         sync += ["xb", "xa"]
         steps["xa"][0].append("x2")
-        pool_queue = ["third_read", "third_write"]
+        pool_queue = []
         tensor = mm(E[0][A], 0, 1) + mm(D[A][0], 0, 1, 2, 3) + mm(E[1][A], 0, 1) + mm(D[A][1], 0, 1) + mm(F[A][0], 0, 1) + mm(D[A][1], 2, 3)
         scalar = out(E[0][A], 0, 1) + out(D[A][0], 0, 1, 2, 3) + out(E[1][A], 0) + out(D[A][1], 0, 1) + out(F[A][0], 0, 1) + out(D[A][1], 2, 3)
         vector = ["zero"] + sort(G[0]) + q(G[0], E[0][A]) + sort(G[1]) + q(G[1]) + sort(G[2]) + out(E[1][A], 1) + q(G[2], E[1][A]) + sort(G[3]) + q(F[A][0], G[3])
@@ -382,8 +382,8 @@ def tile_efficientmultiscaledilatedattention_pa_v_kernel(tc, x, W_kv, b_kv, E_k,
         for n, job in enumerate(DW[0][:4] + DW[1][:4] + DW[0][4:] + DW[1][4:]):
             tensor += mm(job, 0, 1)
             scalar += out(job, 0, 1) if n < 6 else out(job, 0)
-            vector += (beside[n] if n < 6 else out(job, 1)) + ["third_add"] * (n == 10)
-            sync += [("store", job)]
+            vector += (beside[n] if n < 6 else out(job, 1)) + ["third_add"] * (n == 9)
+            sync += [("store", job)] + ["third_read"] * (n == 4) + ["third_write"] * (n == 11)
             if n == 7:
                 tensor += mm(zb, 0, 1)
                 vector += [("add", tile, h) for h in range(2) for tile in DX[B]]

@@ -16,10 +16,12 @@ MULT = mybir.AluOpType.mult
 FLOPS = 2 * 1024 * 512 * 2048 + 2 * 1024 * 2048 * 1024 + 2 * 1024 * 1024 * 2048
 BYTES = 2 * (1600 * 1024 + 1024 * 2048 + 2 * 1024 * 512 + 2 * 512 * 1024) + 4 * (1600 * 1024 + 1024 * 2048)
 
-ROWS = 15
+A, B, SMALL = 0, 1, 2
+BANKS = 8
 STAGES = 9
+ROWS = 15
 MOVED = 512
-A, B = 0, 1
+BACK = 60
 
 
 def tile_efficientmultiscaledilatedattention_pa_v_kernel(tc, x, W_kv, b_kv, E_k, E_v, kv, grad_0, grad_1, out_0, out_1):
@@ -38,6 +40,9 @@ def tile_efficientmultiscaledilatedattention_pa_v_kernel(tc, x, W_kv, b_kv, E_k,
         def stage(name):
             return pool.tile([128, 2048], BF16, name=name, tag="stage", bufs=STAGES, align_bytes=64)
 
+        def bank(name):
+            return psum.tile([128, 512], F32, name=name, tag="bank", bufs=BANKS)
+
         def operand(name, width):
             codes = pool.tile([128, width], U32, name=name + "_codes", align_bytes=64)
             scales = pool.tile([128, width], U8, name=name + "_scales", align_bytes=64)
@@ -46,8 +51,8 @@ def tile_efficientmultiscaledilatedattention_pa_v_kernel(tc, x, W_kv, b_kv, E_k,
         def quantise(op, col, fmt, src):
             nc.vector.quantize_mx(out=op[0][:, col:col + 512].bitcast(fmt), scales=op[1][:, col:col + 512], in_=src[:])
 
-        def mx(out, lhs, lfmt, lcol, rhs, rfmt, rcol, start, stop):
-            nc.tensor.matmul_mx(out=out, lhsT=lhs[0][:, lcol:lcol + 128].bitcast(lfmt), lhsT_scale=lhs[1][:, lcol:lcol + 128],
+        def mx(ps, lhs, lfmt, lcol, rhs, rfmt, rcol, start, stop):
+            nc.tensor.matmul_mx(out=ps, lhsT=lhs[0][:, lcol:lcol + 128].bitcast(lfmt), lhsT_scale=lhs[1][:, lcol:lcol + 128],
                                 rhs=rhs[0][:, rcol:rcol + 512].bitcast(rfmt), rhs_scale=rhs[1][:, rcol:rcol + 512],
                                 start=start, stop=stop)
 
@@ -99,9 +104,9 @@ def tile_efficientmultiscaledilatedattention_pa_v_kernel(tc, x, W_kv, b_kv, E_k,
             entry = entry + runs[-1][1]
 
         def load_third(i):
-            entry, m = runs[i]
-            r, c = divmod(entry, 14)
-            p, s = divmod(entry, 8)
+            start, m = runs[i]
+            r, c = divmod(start, 14)
+            p, s = divmod(start, 8)
             step(("x3", i), [], lambda: nc.sync.dma_start(out=raw_x[B][122 + p:123 + p, s:s + m, :], in_=third[r:r + 1, 3 * c:3 * (c + m):3, :]))
         for i in range(len(runs)):
             load_third(i)
@@ -109,7 +114,7 @@ def tile_efficientmultiscaledilatedattention_pa_v_kernel(tc, x, W_kv, b_kv, E_k,
         def banked(job, count, needs, fill, empty, room, last_frees=""):
             def filler(i):
                 def action():
-                    held[("bank", job, i)] = psum.tile([128, 512], F32, name=job[0], tag="bank", bufs=8)
+                    held[("bank", job, i)] = bank(job[0])
                     fill(held[("bank", job, i)], i)
                 return action
 
@@ -140,7 +145,8 @@ def tile_efficientmultiscaledilatedattention_pa_v_kernel(tc, x, W_kv, b_kv, E_k,
         def e_job(e, grp):
             job = ("e", e, grp)
             load(job, [128, 4, 512], e_src[e][512 * grp:512 * grp + 512, :].rearrange("(p t) k -> p t k", t=4))
-            flip(job, [("load", job)], lambda half, t, u: held[("raw", job)][:].bitcast(F32)[:, 2 * half + t, u:256:2], TILES, lambda: quantise(ec[e], 512 * grp, E4X4, held[job]), "r")
+            flip(job, [("load", job)], lambda half, t, u: held[("raw", job)][:].bitcast(F32)[:, 2 * half + t, u:256:2], TILES,
+                 lambda: quantise(ec[e], 512 * grp, E4X4, held[job]), "r")
 
         def w_job(i):
             job = ("w", i)
@@ -150,13 +156,15 @@ def tile_efficientmultiscaledilatedattention_pa_v_kernel(tc, x, W_kv, b_kv, E_k,
                     nc.vector.quantize_mx(out=wc[fb][0][:, 128 * i:128 * i + 128].bitcast(E4X4), scales=wc[fb][1][:, 128 * i:128 * i + 128],
                                           in_=held[job][:, 512 * fb:512 * fb + 512])
             load(job, [128, 2048], W_kv[128 * i:128 * i + 128, :])
-            flip(job, [("load", job)], lambda half, t, u: held[("raw", job)][:].bitcast(F32)[:, 256 * (2 * half + t) + u:256 * (2 * half + t) + 256:2], TILES, finish, "r")
+            flip(job, [("load", job)], lambda half, t, u: held[("raw", job)][:].bitcast(F32)[:, 256 * (2 * half + t) + u:256 * (2 * half + t) + 256:2],
+                 TILES, finish, "r")
 
         def g_job(fb):
             e, b = divmod(fb, 2)
             job = ("g", fb)
 
             def sort(on_vector):
+                assert on_vector
                 held[job] = stage("g_sorted")
                 nc.vector.tensor_scalar(out=held[job][:].rearrange("p (u h n r k) -> p h n u r k", u=2, h=4, r=2, k=4),
                                         in0=held[("raw", job)][:].rearrange("p h (k n u r) -> p h n u r k", k=4, u=2, r=2),
@@ -225,9 +233,9 @@ def tile_efficientmultiscaledilatedattention_pa_v_kernel(tc, x, W_kv, b_kv, E_k,
                 else:
                     for d in range(2):
                         nc.vector.tensor_copy(out=dst[:, :, 384 + d:444:2].rearrange("p f (m e) -> p f m e", e=2), in_=src[:, :, :, 113:128].rearrange("p f e m -> p f m e"))
-                    nc.vector.tensor_copy(out=dst[:, :, 444:476].rearrange("p f (e n) -> p f e n", e=2), in_=src[:, :, :, 0:16])
+                    nc.vector.tensor_copy(out=dst[:, :, 444:476].rearrange("p f (n e) -> p f n e", e=2), in_=src[:, :, :, 0:16].rearrange("p f e n -> p f n e"))
         step("zero", [], zero)
-        for which in (A, B, 2):
+        for which in (A, B, SMALL):
             step(("gather", which), ["zero"] + [("q", ("f", fb, B)) for fb in range(4)], lambda which=which: gather(which))
 
         def product(op, pitch, col):
@@ -243,12 +251,12 @@ def tile_efficientmultiscaledilatedattention_pa_v_kernel(tc, x, W_kv, b_kv, E_k,
         def extra_job(job, col, which):
             for h in range(2):
                 def action(h=h):
-                    held[("bank", job, h)] = psum.tile([128, 512], F32, name="extra", tag="bank", bufs=8)
+                    held[("bank", job, h)] = bank("extra")
                     product(zc, MOVED, col)(held[("bank", job, h)], h)
-                step(("mm", job, h), [("gather", w) for w in which], action, takes="b")
+                step(("mm", job, h), [("gather", which)], action, takes="b")
             needs_w(job)
 
-        def dx_job(job, fill, needs, extra, last, tokens):
+        def dx_job(job, fill, needs, extra, mate, tokens):
             def empty(on_vector, ps, h):
                 if h == 0:
                     held[job] = row("y_second", [128, 1024], F32)
@@ -262,8 +270,8 @@ def tile_efficientmultiscaledilatedattention_pa_v_kernel(tc, x, W_kv, b_kv, E_k,
             banked(job, 2, needs, fill, empty, "r")
             needs_w(job)
             for h in range(2):
-                step(("add", job, h), [("out", job, h), ("mm", extra, h)] + ([("add", job, 0)] if h else []) + ([("add", last, h)] if last else []),
-                     lambda h=h: add(h), takes="" if h else "r", frees="b" if last else "")
+                step(("add", job, h), [("out", job, h), ("mm", extra, h)] + ([("add", job, 0)] if h else []) + ([("add", mate, h)] if mate else []),
+                     lambda h=h: add(h), takes="" if h else "r", frees="b" if mate else "")
             step(("second", job), [("out", job, 0), ("out", job, 1)], lambda: nc.sync.dma_start(out=tokens(1), in_=held[job][:]))
             step(("first", job), [("add", job, 1), ("second", job)], lambda: nc.sync.dma_start(out=tokens(0), in_=held[("first", job)][:]), frees="rr")
 
@@ -273,22 +281,25 @@ def tile_efficientmultiscaledilatedattention_pa_v_kernel(tc, x, W_kv, b_kv, E_k,
         for t in range(2):
             dx_job(("dx", B, t), product(fc[B], 512, 256 * t), [("q", ("f", fb, B)) for fb in range(4)], ("z", B, 0), ("dx", B, 0) if t else None,
                    lambda d, t=t: of[1024:1536, :].rearrange("(p j) c -> p j c", j=4)[:, 2 * t + d, :])
-            extra_job(("z", A, t), 128 * t, [A])
-        extra_job(("z", B, 0), 256, [B])
+            extra_job(("z", A, t), 128 * t, A)
+        extra_job(("z", B, 0), 256, B)
 
-        def rest_job():
-            job = ("dx", 2, 0)
-            rows = of[0:480, :].rearrange("(r n) k -> r n k", n=120)
-            spans = [(0, 12, of[1536:1560:2, :])] + [(12 + 14 * r, min(26 + 14 * r, 60), rows[r, 0:3 * min(14, 48 - 14 * r):3, :]) for r in range(4)]
-            units = of[1536:1600, :].rearrange("(n e d) c -> e d n c", e=2, d=2)
-            banked(job, 2, [("gather", 2)], product(zc, MOVED, 384), lambda on_vector, ps, h: move(on_vector, rest[0:92, 0, 512 * h:512 * h + 512], ps[0:92, :]), "")
+        rows_3 = of[0:480, :].rearrange("(r n) k -> r n k", n=120)
+        spans = [(0, 12, of[1536:1560:2, :])] + [(12 + 14 * r, min(26 + 14 * r, BACK), rows_3[r, 0:3 * min(14, 48 - 14 * r):3, :]) for r in range(4)]
+
+        def small_job():
+            job = ("dx", SMALL, 0)
+            banked(job, 2, [("gather", SMALL)], product(zc, MOVED, 384),
+                   lambda on_vector, ps, h: move(on_vector, rest[0:BACK + 32, 0, 512 * h:512 * h + 512], ps[0:BACK + 32, :]), "")
             needs_w(job)
             step("rest_store", [("out", job, 0), ("out", job, 1)],
-                 lambda: [nc.sync.dma_start(out=units[e, d], in_=rest[60 + 16 * e:76 + 16 * e, 0, :]) for e in range(2) for d in range(2)])
-            step("third_read", ["rest_store"] + [(k, ("dx", A, t)) for t in range(4) for k in ("first", "second")],
-                 lambda: [nc.sync.dma_start(out=rest[p0:p1, 1, :], in_=hbm) for p0, p1, hbm in spans])
-            step("third_add", ["third_read"], lambda: nc.vector.tensor_tensor(out=rest[0:60, 1, :], in0=rest[0:60, 0, :], in1=rest[0:60, 1, :], op=ADD))
-            step("third_write", ["third_add"], lambda: [nc.sync.dma_start(out=hbm, in_=rest[p0:p1, 1, :]) for p0, p1, hbm in spans])
+                 lambda: nc.sync.dma_start(out=of[1536:1600, :].rearrange("(n d) c -> n d c", d=2), in_=rest[BACK:BACK + 32, 0:1, :].to_broadcast([32, 2, 1024])))
+            for i, (p0, p1, hbm) in enumerate(spans):
+                step(("read", i), ["rest_store"] + [(k, ("dx", A, t)) for t in range(4) for k in ("first", "second")],
+                     lambda p0=p0, p1=p1, hbm=hbm: nc.sync.dma_start(out=rest[p0:p1, 1, :], in_=hbm))
+                step(("write", i), ["back_add"], lambda p0=p0, p1=p1, hbm=hbm: nc.sync.dma_start(out=hbm, in_=rest[p0:p1, 1, :]))
+            step("back_add", [("read", i) for i in range(len(spans))],
+                 lambda: nc.vector.tensor_tensor(out=rest[0:BACK, 1, :], in0=rest[0:BACK, 0, :], in1=rest[0:BACK, 1, :], op=ADD))
 
         def dw_job(n, pair):
             job = ("dw", n, pair)
@@ -302,7 +313,8 @@ def tile_efficientmultiscaledilatedattention_pa_v_kernel(tc, x, W_kv, b_kv, E_k,
                     held[job] = row("dw_out", [128, 1024], F32)
                 move(on_vector, held[job][:, 512 * i:512 * i + 512].rearrange("p (m u r) -> p m u r", u=2, r=2), ps[:].rearrange("p (u m r) -> p m u r", u=2, r=2))
             banked(job, 2, [("q", ("x", grp, n // 4)) for grp in range(2)] + [("q", ("l", 2 * pair + i, grp)) for i in range(2) for grp in range(2)], fill, empty, "r")
-            step(("store", job), [("out", job, 0), ("out", job, 1)], lambda: nc.sync.dma_start(out=out_1[128 * n:128 * n + 128, 1024 * pair:1024 * pair + 1024], in_=held[job][:]), frees="r")
+            step(("store", job), [("out", job, 0), ("out", job, 1)],
+                 lambda: nc.sync.dma_start(out=out_1[128 * n:128 * n + 128, 1024 * pair:1024 * pair + 1024], in_=held[job][:]), frees="r")
 
         for grp in range(2):
             for i in range(2):
@@ -316,7 +328,7 @@ def tile_efficientmultiscaledilatedattention_pa_v_kernel(tc, x, W_kv, b_kv, E_k,
             w_job(i)
             dw_job(i, 0)
             dw_job(i, 1)
-        rest_job()
+        small_job()
 
         def mm(job, *which):
             return [("mm", job, i) for i in which]
@@ -330,6 +342,12 @@ def tile_efficientmultiscaledilatedattention_pa_v_kernel(tc, x, W_kv, b_kv, E_k,
         def sort(*jobs):
             return [("sort", job) for job in jobs]
 
+        def pool_x(job):
+            return [("add", job)]
+
+        def add_extra(tiles):
+            return [("add", tile, h) for h in range(2) for tile in tiles]
+
         E = [[("e", e, grp) for grp in range(2)] for e in range(2)]
         G = [("g", i) for i in range(4)]
         W = [("w", i) for i in range(8)]
@@ -337,16 +355,17 @@ def tile_efficientmultiscaledilatedattention_pa_v_kernel(tc, x, W_kv, b_kv, E_k,
         F = [[("f", fb, grp) for fb in range(4)] for grp in range(2)]
         L = [[("l", fb, grp) for fb in range(4)] for grp in range(2)]
         X = [[("x", grp, h) for h in range(2)] for grp in range(2)]
-        DX = [[("dx", A, t) for t in range(4)], [("dx", B, t) for t in range(2)], [("dx", 2, 0)]]
+        DX = [[("dx", A, t) for t in range(4)], [("dx", B, t) for t in range(2)]]
         Z = [[("z", A, 0), ("z", A, 1)], [("z", B, 0)]]
         DW = [[("dw", n, pair) for n in range(8)] for pair in range(2)]
+        small = ("dx", SMALL, 0)
 
         sync = [("load", job) for job in (E[0][A], G[0], G[1], E[1][A], G[2], G[3], W[0])]
         for i, job in enumerate(W[1:4] + [E[0][B]] + W[4:] + [E[1][B]]):
             sync += [("load", job), ("x3", i)]
         sync += ["xb", "xa"]
         steps["xa"][0].append("x2")
-        pool_queue = []
+
         tensor = mm(E[0][A], 0, 1) + mm(D[A][0], 0, 1, 2, 3) + mm(E[1][A], 0, 1) + mm(D[A][1], 0, 1) + mm(F[A][0], 0, 1) + mm(D[A][1], 2, 3)
         scalar = out(E[0][A], 0, 1) + out(D[A][0], 0, 1, 2, 3) + out(E[1][A], 0) + out(D[A][1], 0, 1) + out(F[A][0], 0, 1) + out(D[A][1], 2, 3)
         vector = ["zero"] + sort(G[0]) + q(G[0], E[0][A]) + sort(G[1]) + q(G[1]) + sort(G[2]) + out(E[1][A], 1) + q(G[2], E[1][A]) + sort(G[3]) + q(F[A][0], G[3])
@@ -357,39 +376,50 @@ def tile_efficientmultiscaledilatedattention_pa_v_kernel(tc, x, W_kv, b_kv, E_k,
         tensor += mm(W[2], 0, 1) + mm(F[A][3], 0, 1) + mm(W[3], 0, 1) + mm(E[0][B], 0, 1)
         scalar += out(W[2], 0) + out(F[A][3], 0) + out(W[3], 0) + out(E[0][B], 0, 1) + ["x2"]
         vector += out(W[2], 1) + q(F[A][2]) + out(F[A][3], 1) + q(W[2]) + out(W[3], 1) + q(F[A][3], W[3]) + sort(L[A][0]) + q(E[0][B])
-        beside = [q(L[A][0]) + sort(L[A][1]), q(L[A][1]) + sort(L[A][2]), q(L[A][2]) + sort(L[A][3]), q(L[A][3]) + sort(L[B][0])]
+
+        woven = L[A] + L[B]
         for t in range(4):
-            tensor += mm(DX[A][t], 0) + mm(W[4 + t], 0, 1) + mm(D[B][t // 2], 2 * (t % 2), 2 * (t % 2) + 1)
-            scalar += out(DX[A][t], 0) + out(W[4 + t], 0, 1) + out(D[B][t // 2], 2 * (t % 2), 2 * (t % 2) + 1)
-            vector += beside[t] + q(W[4 + t])
+            half = (2 * (t % 2), 2 * (t % 2) + 1)
+            tensor += mm(DX[A][t], 0) + mm(W[4 + t], 0, 1) + mm(D[B][t // 2], *half)
+            scalar += out(DX[A][t], 0) + out(W[4 + t], 0, 1) + out(D[B][t // 2], *half)
+            vector += q(woven[t]) + sort(woven[t + 1]) + q(W[4 + t])
+
         tensor += mm(E[1][B], 0, 1) + mm(F[B][0], 0, 1)
         scalar += out(E[1][B], 0) + out(F[B][0], 0)
         vector += q(L[B][0]) + out(E[1][B], 1) + out(F[B][0], 1) + q(E[1][B], F[B][0])
         between = [mm(F[B][1], 0, 1) + mm(D[B][2], 0, 1, 2, 3), mm(D[B][3], 0, 1, 2, 3), mm(F[B][2], 0, 1), mm(F[B][3], 0, 1)]
-        beside = [sort(L[B][1]) + q(F[B][1], L[B][1]), out(D[B][2], 3) + [("add", X[B][0])] + out(D[B][3], 3), sort(X[B][0]) + out(F[B][2], 1) + q(F[B][2]), out(F[B][3], 1) + q(F[B][3]) + [("gather", 2), ("gather", A)] + q(X[B][0])]
+        emptied = [out(F[B][1], 0, 1) + out(D[B][2], 0, 1, 2), out(D[B][3], 0, 1, 2), out(F[B][2], 0), out(F[B][3], 0)]
+        beside = [sort(L[B][1]) + q(F[B][1], L[B][1]),
+                  out(D[B][2], 3) + pool_x(X[B][0]) + out(D[B][3], 3),
+                  sort(X[B][0]) + out(F[B][2], 1) + q(F[B][2]),
+                  out(F[B][3], 1) + q(F[B][3]) + [("gather", SMALL), ("gather", A)] + q(X[B][0])]
         for t in range(4):
             tensor += mm(DX[A][t], 1) + between[t]
             vector += beside[t]
-            scalar += out(DX[A][t], 1) + [("out",) + s[1:] for s in between[t] if ("out",) + s[1:] not in sum(beside, [])]
+            scalar += out(DX[A][t], 1) + emptied[t]
             sync += [("second", DX[A][t])]
-        zb, (b0, b1), last = Z[B][0], DX[B], DX[2][0]
-        tensor += mm(b0, 0, 1) + mm(last, 0, 1) + mm(Z[A][0], 0, 1) + mm(Z[A][1], 0, 1) + mm(b1, 0, 1)
-        scalar += out(b0, 0, 1) + out(last, 0, 1) + sort(L[B][2], L[B][3]) + out(b1, 0, 1)
-        vector += [("add", X[A][0])] + [("add", DX[A][t], h) for h in range(2) for t in range(2)] + sort(X[A][0])
-        vector += [("add", DX[A][2 + t], 0) for t in range(2)] + q(X[A][0]) + [("add", DX[A][2 + t], 1) for t in range(2)]
-        sync += [("second", b0), "rest_store"] + [("first", job) for job in DX[A]] + [("second", b1)]
-        beside = [q(L[B][2]), [("add", X[B][1])] + q(L[B][3]), sort(X[B][1]), [("add", X[A][1])] + q(X[B][1]), sort(X[A][1]), [("gather", B)] + q(X[A][1])]
+
+        tensor += mm(DX[B][0], 0, 1) + mm(small, 0, 1) + mm(Z[A][0], 0, 1) + mm(Z[A][1], 0, 1)
+        scalar += out(DX[B][0], 0, 1) + out(small, 0, 1) + sort(X[A][0], L[B][2])
+        vector += pool_x(X[A][0]) + add_extra(DX[A][:2]) + q(X[A][0]) + add_extra(DX[A][2:])
+        sync += [("second", DX[B][0]), "rest_store"] + [("first", job) for job in DX[A]]
+
+        beside = [sort(L[B][3]) + q(L[B][2]), pool_x(X[B][1]) + q(L[B][3]), sort(X[B][1]), pool_x(X[A][1]) + q(X[B][1]), sort(X[A][1]), [("gather", B)] + q(X[A][1])]
+        read_at, half_at, add_at, write_at = 4, 7, 9, 11
         for n, job in enumerate(DW[0][:4] + DW[1][:4] + DW[0][4:] + DW[1][4:]):
             tensor += mm(job, 0, 1)
-            scalar += out(job, 0, 1) if n < 6 else out(job, 0)
-            vector += (beside[n] if n < 6 else out(job, 1)) + ["third_add"] * (n == 9)
-            sync += [("store", job)] + ["third_read"] * (n == 4) + ["third_write"] * (n == 11)
-            if n == 7:
-                tensor += mm(zb, 0, 1)
-                vector += [("add", tile, h) for h in range(2) for tile in DX[B]]
-                sync += [("first", b0), ("first", b1)]
+            scalar += out(job, 0, 1) if n < len(beside) else out(job, 0)
+            vector += (beside[n] if n < len(beside) else out(job, 1)) + ["back_add"] * (n == add_at)
+            sync += [("store", job)]
+            sync += [("read", i) for i in range(len(spans)) if n == read_at + i // 2]
+            sync += [("write", i) for i in range(len(spans)) if n == write_at + i // 2]
+            if n == half_at:
+                tensor += mm(DX[B][1], 0, 1) + mm(Z[B][0], 0, 1)
+                scalar += out(DX[B][1], 0, 1)
+                vector += add_extra(DX[B])
+                sync += [("second", DX[B][1])] + [("first", tile) for tile in DX[B]]
 
-        room = {"b": 8, "s": STAGES, "r": ROWS}
+        room = {"b": BANKS, "s": STAGES, "r": ROWS}
         written = set()
 
         def ready(name):
@@ -408,12 +438,12 @@ def tile_efficientmultiscaledilatedattention_pa_v_kernel(tc, x, W_kv, b_kv, E_k,
                 room[c] += 1
             written.add(name)
 
-        while tensor or scalar or vector or sync or pool_queue:
+        while tensor or scalar or vector or sync:
             before = len(written)
-            for queue in (sync, pool_queue, vector, scalar):
+            for queue in (sync, vector, scalar):
                 while queue and ready(queue[0]):
                     write_out(queue.pop(0), queue)
             if tensor and ready(tensor[0]):
                 write_out(tensor.pop(0), tensor)
-            assert len(written) > before, (tensor[:1], scalar[:1], vector[:1], sync[:1], pool_queue[:1], room)
+            assert len(written) > before
         assert len(written) == len(steps)

from contextlib import ExitStack

import concourse.mybir as mybir
from concourse.masks import make_identity

F32 = mybir.dt.float32
BF16 = mybir.dt.bfloat16
U32 = mybir.dt.uint32
I32 = mybir.dt.int32
U8 = mybir.dt.uint8
E4X4 = mybir.dt.float8_e4m3fn_x4
E5X4 = mybir.dt.float8_e5m2_x4
ADD = mybir.AluOpType.add
MULT = mybir.AluOpType.mult

FLOPS = 2 * 1024 * 512 * 2048 + 2 * 1024 * 2048 * 1024 + 2 * 1024 * 1024 * 2048
BYTES = 2 * (1600 * 1024 + 1024 * 2048 + 2 * 1024 * 512 + 2 * 512 * 1024) + 4 * (1600 * 1024 + 1024 * 2048)

A, B, SMALL = 0, 1, 2
BANKS = 8
STAGES = 9
ROWS = 15
MOVED = 512
BACK = 60


def tile_efficientmultiscaledilatedattention_pa_v_kernel(tc, x, W_kv, b_kv, E_k, E_v, kv, grad_0, grad_1, out_0, out_1):
    nc = tc.nc
    with ExitStack() as ctx:
        pool = ctx.enter_context(tc.tile_pool(name="pool", bufs=1))
        psum = ctx.enter_context(tc.psum_pool(name="psum", bufs=1))
        ctx.enter_context(tc.manual_schedule())

        ident = pool.tile([128, 128], F32, name="ident", align_bytes=64)
        make_identity(nc, ident[:])

        def row(name, shape, dt):
            return pool.tile(shape, dt, name=name, tag="row", bufs=ROWS, align_bytes=64)

        def stage(name):
            return pool.tile([128, 2048], BF16, name=name, tag="stage", bufs=STAGES, align_bytes=64)

        def bank(name):
            return psum.tile([128, 512], F32, name=name, tag="bank", bufs=BANKS)

        def operand(name, width):
            codes = pool.tile([128, width], U32, name=name + "_codes", align_bytes=64)
            scales = pool.tile([128, width], U8, name=name + "_scales", align_bytes=64)
            return codes, scales

        def quantise(op, col, fmt, src):
            nc.vector.quantize_mx(out=op[0][:, col:col + 512].bitcast(fmt), scales=op[1][:, col:col + 512], in_=src[:])

        def mx(ps, lhs, lfmt, lcol, rhs, rfmt, rcol, start, stop):
            nc.tensor.matmul_mx(out=ps, lhsT=lhs[0][:, lcol:lcol + 128].bitcast(lfmt), lhsT_scale=lhs[1][:, lcol:lcol + 128],
                                rhs=rhs[0][:, rcol:rcol + 512].bitcast(rfmt), rhs_scale=rhs[1][:, rcol:rcol + 512],
                                start=start, stop=stop)

        def move(on_vector, dst, src):
            if on_vector:
                nc.vector.tensor_copy(out=dst, in_=src)
            else:
                nc.scalar.copy(out=dst, in_=src)

        xf = x[0]
        of = out_0[0]
        e_src = [E_k, E_v]
        g_src = [grad_0[0], grad_1[0]]

        steps = {}
        held = {}

        def step(name, needs, action, takes="", frees=""):
            steps[name] = (list(needs), action, takes, frees)

        raw_x = [pool.tile([128, 8, 1024], BF16, name="raw_x%d" % grp, align_bytes=64) for grp in range(2)]
        rest = pool.tile([128, 2, 1024], F32, name="rest", align_bytes=64)
        ec = [operand("ek", 1024), operand("ev", 1024)]
        gc = [operand("gk", 1024), operand("gv", 1024)]
        xc = [operand("x0", 1024), operand("x1", 1024)]
        wc = [operand("w%d" % i, 1024) for i in range(4)]
        lc = [operand("l%d" % i, 1024) for i in range(4)]
        fc = [operand("fa", 2048), operand("fb", 2048)]
        zc = operand("moved", 4 * MOVED)

        def load(job, shape, src):
            def action():
                held[("raw", job)] = row("raw_" + job[0], shape, BF16)
                nc.sync.dma_start(out=held[("raw", job)][:], in_=src)
            step(("load", job), [], action, takes="r")

        def quads(n0, n):
            return xf[n0:n0 + 8 * n, :].rearrange("(p j) c -> p j c", j=8)

        step("xa", [], lambda: nc.sync.dma_start(out=raw_x[A][:], in_=quads(0, 128)))
        step("xb", [], lambda: [nc.sync.dma_start(out=raw_x[B][0:64], in_=quads(1024, 64)), nc.sync.dma_start(out=raw_x[B][64:72], in_=quads(1536, 8))])
        step("x2", [], lambda: nc.scalar.dma_start(out=raw_x[B][72:122], in_=xf.rearrange("(r n) c -> r n c", n=80)[:, 0:40:2, :]))

        third = xf[0:480, :].rearrange("(r n) c -> r n c", n=120)
        runs = []
        entry = 0
        while entry < 48:
            runs.append((entry, min(14 - entry % 14, 8 - entry % 8, 48 - entry)))
            entry = entry + runs[-1][1]

        def load_third(i):
            start, m = runs[i]
            r, c = divmod(start, 14)
            p, s = divmod(start, 8)
            step(("x3", i), [], lambda: nc.sync.dma_start(out=raw_x[B][122 + p:123 + p, s:s + m, :], in_=third[r:r + 1, 3 * c:3 * (c + m):3, :]))
        for i in range(len(runs)):
            load_third(i)

        def banked(job, count, needs, fill, empty, room, last_frees=""):
            def filler(i):
                def action():
                    held[("bank", job, i)] = bank(job[0])
                    fill(held[("bank", job, i)], i)
                return action

            def emptier(i):
                return lambda on_vector: empty(on_vector, held[("bank", job, i)], i)
            for i in range(count):
                step(("mm", job, i), needs, filler(i), takes="b", frees=last_frees if i == count - 1 else "")
                step(("out", job, i), [("mm", job, i)] + ([("out", job, 0)] if i and room else []), emptier(i), takes=room if i == 0 else "", frees="b")

        def flip(job, needs, words_of, place, finish, last_frees):
            def fill(ps, half):
                v = ps[:].rearrange("p (t u c) -> p t u c", t=2, u=2)
                for t in range(2):
                    for u in range(2):
                        nc.tensor.transpose(v[:, t, u, :], words_of(half, t, u), ident[:])

            def empty(on_vector, ps, half):
                if half == 0:
                    held[job] = stage("flipped")
                dst = held[job][:].bitcast(F32)[:, 512 * half:512 * half + 512]
                move(on_vector, dst.rearrange(place, t=2, u=2), ps[:].rearrange("p (t u c) -> " + place.split("-> ")[1], t=2, u=2))
            banked(job, 2, needs, fill, empty, "s", last_frees)
            step(("q", job), [("out", job, 0), ("out", job, 1)], finish, frees="s")

        TILES = "p (t c u) -> p t c u"
        PAIRS = "p (c t u) -> p c t u"

        def e_job(e, grp):
            job = ("e", e, grp)
            load(job, [128, 4, 512], e_src[e][512 * grp:512 * grp + 512, :].rearrange("(p t) k -> p t k", t=4))
            flip(job, [("load", job)], lambda half, t, u: held[("raw", job)][:].bitcast(F32)[:, 2 * half + t, u:256:2], TILES,
                 lambda: quantise(ec[e], 512 * grp, E4X4, held[job]), "r")

        def w_job(i):
            job = ("w", i)

            def finish():
                for fb in range(4):
                    nc.vector.quantize_mx(out=wc[fb][0][:, 128 * i:128 * i + 128].bitcast(E4X4), scales=wc[fb][1][:, 128 * i:128 * i + 128],
                                          in_=held[job][:, 512 * fb:512 * fb + 512])
            load(job, [128, 2048], W_kv[128 * i:128 * i + 128, :])
            flip(job, [("load", job)], lambda half, t, u: held[("raw", job)][:].bitcast(F32)[:, 256 * (2 * half + t) + u:256 * (2 * half + t) + 256:2],
                 TILES, finish, "r")

        def g_job(fb):
            e, b = divmod(fb, 2)
            job = ("g", fb)

            def sort(on_vector):
                assert on_vector
                held[job] = stage("g_sorted")
                nc.vector.tensor_scalar(out=held[job][:].rearrange("p (u h n r k) -> p h n u r k", u=2, h=4, r=2, k=4),
                                        in0=held[("raw", job)][:].rearrange("p h (k n u r) -> p h n u r k", k=4, u=2, r=2),
                                        scalar1=0.5, scalar2=None, op0=MULT)
            load(job, [128, 4, 512], g_src[e][4 * b:4 * b + 4].rearrange("h (p j) d -> p h (j d)", j=4))
            step(("sort", job), [("load", job)], sort, takes="s", frees="r")
            step(("q", job), [("sort", job)], lambda: quantise(gc[e], 512 * b, E5X4, held[job]), frees="s")

        def dkv_job(fb, grp):
            e, b = divmod(fb, 2)
            job, by_feature, by_landmark = ("d", fb, grp), ("f", fb, grp), ("l", fb, grp)

            def empty(on_vector, ps, t):
                if t == 0:
                    held[job] = stage("dkv_bf16")
                move(on_vector, held[job][:, 512 * t:512 * t + 512], ps[:])
            banked(job, 4, [("q", ("g", fb)), ("q", ("e", e, grp))],
                   lambda ps, t: mx(ps[:], ec[e], E4X4, 512 * grp + 128 * t, gc[e], E5X4, 512 * b, True, True), empty, "s")
            done = [("out", job, t) for t in range(4)]

            def words(half, i, u):
                t = 2 * i + half if grp == B else 2 * half + i
                return held[job][:].bitcast(F32)[:, 256 * t + 128 * u:256 * t + 128 * u + 128]
            flip(by_feature, done, words, PAIRS if grp == B else TILES, lambda: quantise(fc[grp], 512 * fb, E5X4, held[by_feature]), "")

            def weave(on_vector):
                held[by_landmark] = stage("dkv_woven")
                move(on_vector, held[by_landmark][:].rearrange("p (c r t) -> p c t r", t=4, r=4), held[job][:].rearrange("p (t c r) -> p c t r", t=4, r=4))
            step(("sort", by_landmark), done + [("mm", by_feature, 1)], weave, takes="s", frees="s")
            step(("q", by_landmark), [("sort", by_landmark)], lambda: quantise(lc[fb], 512 * grp, E5X4, held[by_landmark]), frees="s")

        def x_job(grp, h):
            job = ("x", grp, h)

            def add():
                v = raw_x[grp][:].rearrange("p (t two) c -> p two t c", two=2)
                held[("sum", job)] = stage("x_sum")
                nc.vector.tensor_tensor(out=held[("sum", job)][:].rearrange("p (t c) -> p t c", t=4),
                                        in0=v[:, 0, :, 512 * h:512 * h + 512], in1=v[:, 1, :, 512 * h:512 * h + 512], op=ADD)

            def sort(on_vector):
                held[job] = stage("x_sorted")
                move(on_vector, held[job][:].rearrange("p (c r t) -> p c t r", t=4, r=4), held[("sum", job)][:].rearrange("p (t c r) -> p c t r", t=4, r=4))
            step(("add", job), ["xb", "x2"] + [("x3", i) for i in range(len(runs))] if grp == B else ["xa"], add, takes="s")
            step(("sort", job), [("add", job)], sort, takes="s", frees="s")
            step(("q", job), [("sort", job)], lambda: quantise(xc[grp], 512 * h, E4X4, held[job]), frees="s")

        def zero():
            nc.vector.memset(zc[0][:].bitcast(I32), 0)
            nc.vector.memset(zc[1][:].bitcast(I32), 0)
            nc.vector.memset(fc[B][1][:].bitcast(I32), 0)

        def gather(which):
            for plane in range(2):
                view = (lambda ap: ap.bitcast(I32)) if plane == 0 else (lambda ap: ap)
                src = view(fc[B][plane][:]).rearrange("p (f e c) -> p f e c", f=4, e=2)[:, :, :, 128:256]
                dst = view(zc[plane][:]).rearrange("p (f c) -> p f c", f=4)
                if which == A:
                    for w in range(2):
                        nc.vector.tensor_copy(out=dst[:, :, 128 * w:128 * w + 130].rearrange("p f (a b) -> p f a b", b=10)[:, :, :, 0:5],
                                              in_=src[:, :, w, 16:81].rearrange("p f (a b) -> p f a b", b=5))
                elif which == B:
                    nc.vector.tensor_copy(out=dst[:, :, 260:380].rearrange("p f (a m e) -> p f a m e", m=10, e=2)[:, :, :, 0:5, :],
                                          in_=src[:, :, :, 81:111].rearrange("p f e (a m) -> p f a m e", m=5))
                    nc.vector.tensor_copy(out=dst[:, :, 380:384].rearrange("p f (m e) -> p f m e", e=2), in_=src[:, :, :, 111:113].rearrange("p f e m -> p f m e"))
                else:
                    for d in range(2):
                        nc.vector.tensor_copy(out=dst[:, :, 384 + d:444:2].rearrange("p f (m e) -> p f m e", e=2), in_=src[:, :, :, 113:128].rearrange("p f e m -> p f m e"))
                    nc.vector.tensor_copy(out=dst[:, :, 444:476].rearrange("p f (n e) -> p f n e", e=2), in_=src[:, :, :, 0:16].rearrange("p f e n -> p f n e"))
        step("zero", [], zero)
        for which in (A, B, SMALL):
            step(("gather", which), ["zero"] + [("q", ("f", fb, B)) for fb in range(4)], lambda which=which: gather(which))

        def product(op, pitch, col):
            def fill(ps, h):
                for fb in range(4):
                    mx(ps[:], op, E5X4, pitch * fb + col, wc[fb], E4X4, 512 * h, fb == 0, fb == 3)
            return fill

        def needs_w(job):
            for h in range(2):
                steps[("mm", job, h)][0].extend([("q", ("w", 4 * h + i)) for i in range(4)])

        def extra_job(job, col, which):
            for h in range(2):
                def action(h=h):
                    held[("bank", job, h)] = bank("extra")
                    product(zc, MOVED, col)(held[("bank", job, h)], h)
                step(("mm", job, h), [("gather", which)], action, takes="b")
            needs_w(job)

        def dx_job(job, fill, needs, extra, mate, tokens):
            def empty(on_vector, ps, h):
                if h == 0:
                    held[job] = row("y_second", [128, 1024], F32)
                move(on_vector, held[job][:, 512 * h:512 * h + 512], ps[:])

            def add(h):
                if h == 0:
                    held[("first", job)] = row("y_first", [128, 1024], F32)
                cols = slice(512 * h, 512 * h + 512)
                nc.vector.tensor_tensor(out=held[("first", job)][:, cols], in0=held[("bank", extra, h)][:], in1=held[job][:, cols], op=ADD)
            banked(job, 2, needs, fill, empty, "r")
            needs_w(job)
            for h in range(2):
                step(("add", job, h), [("out", job, h), ("mm", extra, h)] + ([("add", job, 0)] if h else []) + ([("add", mate, h)] if mate else []),
                     lambda h=h: add(h), takes="" if h else "r", frees="b" if mate else "")
            step(("second", job), [("out", job, 0), ("out", job, 1)], lambda: nc.sync.dma_start(out=tokens(1), in_=held[job][:]))
            step(("first", job), [("add", job, 1), ("second", job)], lambda: nc.sync.dma_start(out=tokens(0), in_=held[("first", job)][:]), frees="rr")

        for t in range(4):
            dx_job(("dx", A, t), product(fc[A], 512, 128 * t), [("q", ("f", fb, A)) for fb in range(4)], ("z", A, t // 2), ("dx", A, t - 1) if t % 2 else None,
                   lambda d, t=t: of[0:1024, :].rearrange("(p j) c -> p j c", j=8)[:, 2 * t + d, :])
        for t in range(2):
            dx_job(("dx", B, t), product(fc[B], 512, 256 * t), [("q", ("f", fb, B)) for fb in range(4)], ("z", B, 0), ("dx", B, 0) if t else None,
                   lambda d, t=t: of[1024:1536, :].rearrange("(p j) c -> p j c", j=4)[:, 2 * t + d, :])
            extra_job(("z", A, t), 128 * t, A)
        extra_job(("z", B, 0), 256, B)

        rows_3 = of[0:480, :].rearrange("(r n) k -> r n k", n=120)
        spans = [(0, 12, of[1536:1560:2, :])] + [(12 + 14 * r, min(26 + 14 * r, BACK), rows_3[r, 0:3 * min(14, 48 - 14 * r):3, :]) for r in range(4)]

        def small_job():
            job = ("dx", SMALL, 0)
            banked(job, 2, [("gather", SMALL)], product(zc, MOVED, 384),
                   lambda on_vector, ps, h: move(on_vector, rest[0:BACK + 32, 0, 512 * h:512 * h + 512], ps[0:BACK + 32, :]), "")
            needs_w(job)
            step("rest_store", [("out", job, 0), ("out", job, 1)],
                 lambda: nc.sync.dma_start(out=of[1536:1600, :].rearrange("(n d) c -> n d c", d=2), in_=rest[BACK:BACK + 32, 0:1, :].to_broadcast([32, 2, 1024])))
            for i, (p0, p1, hbm) in enumerate(spans):
                step(("read", i), ["rest_store"] + [(k, ("dx", A, t)) for t in range(4) for k in ("first", "second")],
                     lambda p0=p0, p1=p1, hbm=hbm: nc.sync.dma_start(out=rest[p0:p1, 1, :], in_=hbm))
                step(("write", i), ["back_add"], lambda p0=p0, p1=p1, hbm=hbm: nc.sync.dma_start(out=hbm, in_=rest[p0:p1, 1, :]))
            step("back_add", [("read", i) for i in range(len(spans))],
                 lambda: nc.vector.tensor_tensor(out=rest[0:BACK, 1, :], in0=rest[0:BACK, 0, :], in1=rest[0:BACK, 1, :], op=ADD))

        def dw_job(n, pair):
            job = ("dw", n, pair)

            def fill(ps, i):
                for grp in range(2):
                    mx(ps[:], xc[grp], E4X4, 128 * n, lc[2 * pair + i], E5X4, 512 * grp, grp == 0, grp == 1)

            def empty(on_vector, ps, i):
                if i == 0:
                    held[job] = row("dw_out", [128, 1024], F32)
                move(on_vector, held[job][:, 512 * i:512 * i + 512].rearrange("p (m u r) -> p m u r", u=2, r=2), ps[:].rearrange("p (u m r) -> p m u r", u=2, r=2))
            banked(job, 2, [("q", ("x", grp, n // 4)) for grp in range(2)] + [("q", ("l", 2 * pair + i, grp)) for i in range(2) for grp in range(2)], fill, empty, "r")
            step(("store", job), [("out", job, 0), ("out", job, 1)],
                 lambda: nc.sync.dma_start(out=out_1[128 * n:128 * n + 128, 1024 * pair:1024 * pair + 1024], in_=held[job][:]), frees="r")

        for grp in range(2):
            for i in range(2):
                e_job(i, grp)
                x_job(grp, i)
            for i in range(4):
                dkv_job(i, grp)
        for i in range(4):
            g_job(i)
        for i in range(8):
            w_job(i)
            dw_job(i, 0)
            dw_job(i, 1)
        small_job()

        def mm(job, *which):
            return [("mm", job, i) for i in which]

        def out(job, *which):
            return [("out", job, i) for i in which]

        def q(*jobs):
            return [("q", job) for job in jobs]

        def sort(*jobs):
            return [("sort", job) for job in jobs]

        def pool_x(job):
            return [("add", job)]

        def add_extra(tiles):
            return [("add", tile, h) for h in range(2) for tile in tiles]

        E = [[("e", e, grp) for grp in range(2)] for e in range(2)]
        G = [("g", i) for i in range(4)]
        W = [("w", i) for i in range(8)]
        D = [[("d", fb, grp) for fb in range(4)] for grp in range(2)]
        F = [[("f", fb, grp) for fb in range(4)] for grp in range(2)]
        L = [[("l", fb, grp) for fb in range(4)] for grp in range(2)]
        X = [[("x", grp, h) for h in range(2)] for grp in range(2)]
        DX = [[("dx", A, t) for t in range(4)], [("dx", B, t) for t in range(2)]]
        Z = [[("z", A, 0), ("z", A, 1)], [("z", B, 0)]]
        DW = [[("dw", n, pair) for n in range(8)] for pair in range(2)]
        small = ("dx", SMALL, 0)

        sync = [("load", job) for job in (E[0][A], G[0], G[1], E[1][A], G[2], G[3], W[0])]
        for i, job in enumerate(W[1:4] + [E[0][B]] + W[4:] + [E[1][B]]):
            sync += [("load", job), ("x3", i)]
        sync += ["xb", "xa"]
        steps["xa"][0].append("x2")

        tensor = mm(E[0][A], 0, 1) + mm(D[A][0], 0, 1, 2, 3) + mm(E[1][A], 0, 1) + mm(D[A][1], 0, 1) + mm(F[A][0], 0, 1) + mm(D[A][1], 2, 3)
        scalar = out(E[0][A], 0, 1) + out(D[A][0], 0, 1, 2, 3) + out(E[1][A], 0) + out(D[A][1], 0, 1) + out(F[A][0], 0, 1) + out(D[A][1], 2, 3)
        vector = ["zero"] + sort(G[0]) + q(G[0], E[0][A]) + sort(G[1]) + q(G[1]) + sort(G[2]) + out(E[1][A], 1) + q(G[2], E[1][A]) + sort(G[3]) + q(F[A][0], G[3])
        for i in range(2):
            tensor += mm(D[A][2 + i], 0, 1) + mm(W[i], 0, 1) + mm(D[A][2 + i], 2, 3) + mm(F[A][1 + i], 0, 1)
            scalar += out(D[A][2 + i], 0, 1) + out(W[i], 0) + out(D[A][2 + i], 2, 3) + out(F[A][1 + i], 0)
            vector += out(W[i], 1) + (q(F[A][i]) if i else []) + out(F[A][1 + i], 1) + q(W[i])
        tensor += mm(W[2], 0, 1) + mm(F[A][3], 0, 1) + mm(W[3], 0, 1) + mm(E[0][B], 0, 1)
        scalar += out(W[2], 0) + out(F[A][3], 0) + out(W[3], 0) + out(E[0][B], 0, 1) + ["x2"]
        vector += out(W[2], 1) + q(F[A][2]) + out(F[A][3], 1) + q(W[2]) + out(W[3], 1) + q(F[A][3], W[3]) + sort(L[A][0]) + q(E[0][B])

        woven = L[A] + L[B]
        for t in range(4):
            half = (2 * (t % 2), 2 * (t % 2) + 1)
            tensor += mm(DX[A][t], 0) + mm(W[4 + t], 0, 1) + mm(D[B][t // 2], *half)
            scalar += out(DX[A][t], 0) + out(W[4 + t], 0, 1) + out(D[B][t // 2], *half)
            vector += q(woven[t]) + sort(woven[t + 1]) + q(W[4 + t])

        tensor += mm(E[1][B], 0, 1) + mm(F[B][0], 0, 1)
        scalar += out(E[1][B], 0) + out(F[B][0], 0)
        vector += q(L[B][0]) + out(E[1][B], 1) + out(F[B][0], 1) + q(E[1][B], F[B][0])
        between = [mm(F[B][1], 0, 1) + mm(D[B][2], 0, 1, 2, 3), mm(D[B][3], 0, 1, 2, 3), mm(F[B][2], 0, 1), mm(F[B][3], 0, 1)]
        emptied = [out(F[B][1], 0, 1) + out(D[B][2], 0, 1, 2), out(D[B][3], 0, 1, 2), out(F[B][2], 0), out(F[B][3], 0)]
        beside = [sort(L[B][1]) + q(F[B][1], L[B][1]),
                  out(D[B][2], 3) + pool_x(X[B][0]) + out(D[B][3], 3),
                  sort(X[B][0]) + out(F[B][2], 1) + q(F[B][2]),
                  out(F[B][3], 1) + q(F[B][3]) + [("gather", SMALL), ("gather", A)] + q(X[B][0])]
        for t in range(4):
            tensor += mm(DX[A][t], 1) + between[t]
            vector += beside[t]
            scalar += out(DX[A][t], 1) + emptied[t]
            sync += [("second", DX[A][t])]

        tensor += mm(DX[B][0], 0, 1) + mm(small, 0, 1) + mm(Z[A][0], 0, 1) + mm(Z[A][1], 0, 1)
        scalar += out(DX[B][0], 0, 1) + out(small, 0, 1) + sort(X[A][0], L[B][2])
        vector += pool_x(X[A][0]) + add_extra(DX[A][:2]) + q(X[A][0]) + add_extra(DX[A][2:])
        sync += [("second", DX[B][0]), "rest_store"] + [("first", job) for job in DX[A]]

        beside = [sort(L[B][3]) + q(L[B][2]), pool_x(X[B][1]) + q(L[B][3]), sort(X[B][1]), pool_x(X[A][1]) + q(X[B][1]), sort(X[A][1]), [("gather", B)] + q(X[A][1])]
        read_at, half_at, add_at, write_at = 4, 7, 9, 11
        for n, job in enumerate(DW[0][:4] + DW[1][:4] + DW[0][4:] + DW[1][4:]):
            tensor += mm(job, 0, 1)
            scalar += out(job, 0, 1) if n < len(beside) else out(job, 0)
            vector += (beside[n] if n < len(beside) else out(job, 1)) + ["back_add"] * (n == add_at)
            sync += [("store", job)]
            sync += [("read", i) for i in range(len(spans)) if n == read_at + i // 2]
            sync += [("write", i) for i in range(len(spans)) if n == write_at + i // 2]
            if n == half_at:
                tensor += mm(DX[B][1], 0, 1) + mm(Z[B][0], 0, 1)
                scalar += out(DX[B][1], 0, 1)
                vector += add_extra(DX[B])
                sync += [("second", DX[B][1])] + [("first", tile) for tile in DX[B]]

        room = {"b": BANKS, "s": STAGES, "r": ROWS}
        written = set()

        def ready(name):
            needs, action, takes, frees = steps[name]
            return all(n in written for n in needs) and all(room[c] > 0 for c in takes)

        def write_out(name, queue):
            needs, action, takes, frees = steps[name]
            if name[0] in ("out", "sort"):
                action(queue is vector)
            else:
                action()
            for c in takes:
                room[c] -= 1
            for c in frees:
                room[c] += 1
            written.add(name)

        while tensor or scalar or vector or sync:
            before = len(written)
            for queue in (sync, vector, scalar):
                while queue and ready(queue[0]):
                    write_out(queue.pop(0), queue)
            if tensor and ready(tensor[0]):
                write_out(tensor.pop(0), tensor)
            assert len(written) > before
        assert len(written) == len(steps)
